import numpy as np
import ml_dtypes


def mxq(x, axis, fmt="e4m3"):
    dtype, down = {"e4m3": (ml_dtypes.float8_e4m3fn, 7), "e5m2": (ml_dtypes.float8_e5m2, 14)}[fmt]
    v = np.moveaxis(np.asarray(x, np.float32).astype(ml_dtypes.bfloat16).astype(np.float64), axis, -1)
    blocks = v.reshape(v.shape[:-1] + (-1, 32))
    amax = np.abs(blocks).max(-1, keepdims=True)
    byte = np.maximum(np.where(amax > 0, np.frexp(amax)[1] - 1 + 127, 0) - down, 1)
    scale = np.exp2(byte - 127.0)
    codes = (blocks / scale).astype(np.float32).astype(dtype).astype(np.float64)
    return np.moveaxis((codes * scale).reshape(v.shape), -1, axis)


WIDE = False


def mx_kscale(k):
    if not WIDE:
        return np.ones(k)
    levels = np.array([10, -10, 5, -5, 0])
    a = np.random.permutation(np.resize(levels, k // 512 * 4)).reshape(k // 512, 4)
    idx = np.arange(k)
    return np.exp2(a[idx // 512, idx % 128 // 32])


BF16 = ml_dtypes.bfloat16


def bf(x):
    return np.asarray(x, np.float32).astype(BF16)


def f64(x):
    return np.asarray(x).astype(np.float64)


E2M1 = np.array([0.0, 0.5, 1.0, 1.5, 2.0, 3.0, 4.0, 6.0, -0.0, -0.5, -1.0, -1.5, -2.0, -3.0, -4.0, -6.0])


def pack_weight(w, fmt):
    k, n = w.shape
    w = f64(bf(w)).reshape(k // 32, 32, n)
    amax = np.abs(w).max(1)
    if fmt == "e4m3":
        byte = np.frexp(amax)[1] - 1 + 127 - 7
    else:
        mant, ex = np.frexp(amax / 6.0)
        byte = np.where(mant > 0.5, ex, ex - 1) + 127
    byte = np.clip(np.where(amax > 0, byte, 1), 1, 254)
    scaled = (w * np.exp2(127.0 - byte)[:, None, :]).reshape(k, n).astype(np.float32)
    by_word = np.ascontiguousarray(scaled.reshape(k // 512, 128, 4, n).transpose(0, 1, 3, 2))
    if fmt == "e4m3":
        words = by_word.astype(ml_dtypes.float8_e4m3fn).view(np.uint8)
    else:
        c = by_word.astype(ml_dtypes.float4_e2m1fn).view(np.uint8) & 0xF
        words = c[..., 0::2] | (c[..., 1::2] << 4)
    return np.ascontiguousarray(words), np.ascontiguousarray(byte.astype(np.uint8).reshape(k // 512, 16, n))


def unpack_weight(words, scales, fmt):
    g, p, n, _ = words.shape
    if fmt == "e4m3":
        vals = np.ascontiguousarray(words).view(ml_dtypes.float8_e4m3fn).astype(np.float64)
    else:
        nib = np.empty((g, p, n, 4), np.uint8)
        nib[..., 0::2] = words & 0xF
        nib[..., 1::2] = words >> 4
        vals = E2M1[nib]
    vals = vals * np.repeat(np.exp2(scales.astype(np.float64) - 127.0), 8, axis=1)[..., None]
    return vals.transpose(0, 1, 3, 2).reshape(g * 512, n)


N, X_DIM, Y_DIM, HID = 1024, 512, 512, 2048
FMT = "e4m3"


def setup_inputs():
    s = mx_kscale(X_DIM)
    t, u = mx_kscale(HID), mx_kscale(HID)
    col = 0.6 + 0.6 * np.random.standard_normal(Y_DIM)
    x_samples = bf(np.random.standard_normal((N, X_DIM)) * s)
    y_samples = bf(np.random.standard_normal((N, Y_DIM)) + col)
    mu_W1_words, mu_W1_scales = pack_weight(np.random.standard_normal((X_DIM, HID)) / np.sqrt(X_DIM) / s[:, None] * t, FMT)
    mu_b1 = bf(np.random.standard_normal(HID) * 0.8 * t)
    mu_W2_words, mu_W2_scales = pack_weight(np.random.standard_normal((HID, Y_DIM)) * 1.2 / np.sqrt(HID) / t[:, None], FMT)
    mu_b2 = bf(0.4 + 0.4 * np.random.standard_normal(Y_DIM))
    lv_W1_words, lv_W1_scales = pack_weight(np.random.standard_normal((X_DIM, HID)) / np.sqrt(X_DIM) / s[:, None] * u, FMT)
    lv_b1 = bf(np.random.standard_normal(HID) * 0.8 * u)
    lv_W2_words, lv_W2_scales = pack_weight(np.random.standard_normal((HID, Y_DIM)) / np.sqrt(HID) / u[:, None], FMT)
    lv_b2 = bf(0.3 + 0.4 * np.random.standard_normal(Y_DIM))
    return {
        "x_samples": x_samples,
        "y_samples": y_samples,
        "mu_W1_words": mu_W1_words,
        "mu_W1_scales": mu_W1_scales,
        "mu_b1": mu_b1,
        "mu_W2_words": mu_W2_words,
        "mu_W2_scales": mu_W2_scales,
        "mu_b2": mu_b2,
        "lv_W1_words": lv_W1_words,
        "lv_W1_scales": lv_W1_scales,
        "lv_b1": lv_b1,
        "lv_W2_words": lv_W2_words,
        "lv_W2_scales": lv_W2_scales,
        "lv_b2": lv_b2,
    }


def reference(x_samples, y_samples, mu_W1_words, mu_W1_scales, mu_b1, mu_W2_words, mu_W2_scales, mu_b2, lv_W1_words, lv_W1_scales, lv_b1, lv_W2_words, lv_W2_scales, lv_b2):
    x = f64(x_samples)
    y = f64(y_samples)
    xq = mxq(x, 1, "e4m3")
    h_mu = np.maximum((xq @ unpack_weight(mu_W1_words, mu_W1_scales, FMT)) + f64(mu_b1), 0.0)
    mu = (mxq(h_mu, 1, "e4m3") @ unpack_weight(mu_W2_words, mu_W2_scales, FMT)) + f64(mu_b2)
    h_lv = np.maximum((xq @ unpack_weight(lv_W1_words, lv_W1_scales, FMT)) + f64(lv_b1), 0.0)
    logvar = np.tanh((mxq(h_lv, 1, "e4m3") @ unpack_weight(lv_W2_words, lv_W2_scales, FMT)) + f64(lv_b2))
    w = 0.5 * np.exp(-logvar)
    n = x.shape[0]
    pos_row = -(((mu - y) ** 2) * w).sum(axis=1)
    Sy = y.sum(axis=0)
    Sy2 = (y ** 2).sum(axis=0)
    neg_row = -(w * (n * mu ** 2 - 2.0 * mu * Sy + Sy2)).sum(axis=1) / (n * n)
    return pos_row, neg_row

@@ -1,0 +1,406 @@
+from contextlib import ExitStack
+
+import concourse.mybir as mybir
+from concourse.masks import make_identity
+
+FLOPS = 4 * 2 * 1024 * 512 * 2048
+
+F32 = mybir.dt.float32
+BF16 = mybir.dt.bfloat16
+I32 = mybir.dt.int32
+U32 = mybir.dt.uint32
+U8 = mybir.dt.uint8
+FP8X4 = mybir.dt.float8_e4m3fn_x4
+ALU = mybir.AluOpType
+ACT = mybir.ActivationFunctionType
+
+P = 128
+N_ROWS = 1024
+X_DIM = 512
+Y_DIM = 512
+HID = 2048
+ROW_TILES = N_ROWS // P
+K_PASS = 512
+HID_PASSES = HID // K_PASS
+MU, LV = 0, 1
+UNITS = 2 * ROW_TILES
+
+
+def tile_infoncemi_pa_kernel(
+    tc,
+    x_samples,
+    y_samples,
+    mu_W1_words,
+    mu_W1_scales,
+    mu_b1,
+    mu_W2_words,
+    mu_W2_scales,
+    mu_b2,
+    lv_W1_words,
+    lv_W1_scales,
+    lv_b1,
+    lv_W2_words,
+    lv_W2_scales,
+    lv_b2,
+    out_0,
+    out_1,
+):
+    nc = tc.nc
+    w1_words_in = {MU: mu_W1_words, LV: lv_W1_words}
+    w1_scales_in = {MU: mu_W1_scales, LV: lv_W1_scales}
+    w2_words_in = {MU: mu_W2_words, LV: lv_W2_words}
+    w2_scales_in = {MU: mu_W2_scales, LV: lv_W2_scales}
+    b1_in = {MU: mu_b1, LV: lv_b1}
+    b2_in = {MU: mu_b2, LV: lv_b2}
+
+    with ExitStack() as ctx:
+        ctx.enter_context(tc.manual_schedule())
+        keep = ctx.enter_context(tc.tile_pool(name="keep", bufs=1))
+        hidden = ctx.enter_context(tc.tile_pool(name="hidden", bufs=2))
+        score = ctx.enter_context(tc.tile_pool(name="score", bufs=2))
+        psum_l1 = ctx.enter_context(tc.psum_pool(name="psum_l1", bufs=4))
+        psum_tr = ctx.enter_context(tc.psum_pool(name="psum_tr", bufs=2))
+        psum_l2 = ctx.enter_context(tc.psum_pool(name="psum_l2", bufs=2))
+
+        x_sb = keep.tile([P, ROW_TILES, X_DIM], BF16, name="x_sb")
+        y_sb = keep.tile([P, ROW_TILES, Y_DIM], BF16, name="y_sb")
+        w1 = keep.tile([P, 2, HID], U32, name="w1", align_bytes=64)
+        w2 = keep.tile([P, 2, HID_PASSES, Y_DIM], U32, name="w2", align_bytes=64)
+        planes = keep.tile([P, 4, 512], U8, name="planes", align_bytes=64)
+        w1_slot = {MU: 0, LV: 1}
+        w2_slot = {MU: 2, LV: 3}
+        b1_rows = keep.tile([P, 2, HID], BF16, name="b1_rows")
+        b2_rows = keep.tile([P, 2, Y_DIM], BF16, name="b2_rows")
+        b1_all = keep.tile([P, 2, HID], BF16, name="b1_all")
+        b2_all = keep.tile([P, 2, Y_DIM], BF16, name="b2_all")
+        ones_bf = keep.tile([P, P], BF16, name="ones_bf")
+        ones_f32 = keep.tile([P, P], F32, name="ones_f32")
+        ident = keep.tile([P, P], F32, name="ident")
+        one_column = keep.tile([P, 1], F32, name="one_column")
+
+        nc.vector.memset(planes[:].bitcast(I32), 0)
+        nc.vector.memset(b1_rows[:, MU, :].bitcast(I32), 0)
+        nc.vector.memset(ones_bf[:], 1.0)
+        nc.vector.memset(one_column[:], 1.0)
+        nc.vector.memset(b1_rows[:, LV, :].bitcast(I32), 0)
+        nc.vector.memset(b2_rows[:].bitcast(I32), 0)
+        nc.vector.memset(ones_f32[:], 1.0)
+        make_identity(nc, ident[:])
+        nc.scalar.activation(out=one_column[:], in_=one_column[:], func=ACT.Sqrt)
+
+        def load_planes(slot, four_planes):
+            for quad in range(4):
+                nc.sync.dma_start(
+                    out=planes[32 * quad : 32 * quad + 16, slot, :].bitcast(I32),
+                    in_=four_planes[:, 4 * quad : 4 * quad + 4, :].bitcast(I32),
+                )
+
+        def load_w1(head):
+            flat = w1_words_in[head][0].rearrange("p n t -> p (n t)")
+            for c in range(HID_PASSES):
+                nc.sync.dma_start(
+                    out=w1[:, head, c * K_PASS : (c + 1) * K_PASS].bitcast(I32),
+                    in_=flat[:, c * 4 * K_PASS : (c + 1) * 4 * K_PASS].bitcast(I32),
+                )
+
+        def load_w2(head):
+            nc.sync.dma_start(
+                out=w2[:, head, :, :].bitcast(I32),
+                in_=w2_words_in[head].rearrange("g p n t -> p g (n t)").bitcast(I32),
+            )
+
+        x_view = x_samples.rearrange("(p r) k -> p r k", r=ROW_TILES)
+        nc.sync.dma_start(out=x_sb[:, 0:2, :], in_=x_view[:, 0:2, :])
+        for head in (MU, LV):
+            nc.scalar.dma_start(out=b1_rows[0:1, head, :], in_=b1_in[head].rearrange("(o n) -> o n", o=1))
+        for head in (MU, LV):
+            nc.scalar.dma_start(out=b2_rows[0:1, head, :], in_=b2_in[head].rearrange("(o n) -> o n", o=1))
+        for head in (MU, LV):
+            load_planes(w1_slot[head], w1_scales_in[head][0].rearrange("q (c n) -> c q n", c=4))
+        for head in (MU, LV):
+            load_planes(w2_slot[head], w2_scales_in[head])
+        load_w1(MU)
+        load_w1(LV)
+        nc.sync.dma_start(out=y_sb[:], in_=y_samples.rearrange("(p r) d -> p r d", r=ROW_TILES))
+        load_w2(MU)
+        nc.sync.dma_start(out=x_sb[:, 2:ROW_TILES, :], in_=x_view[:, 2:ROW_TILES, :])
+        load_w2(LV)
+
+        def spread_bias(rows, spread):
+            for c in range(rows.shape[-1] // K_PASS):
+                bank = psum_l2.tile([P, K_PASS], F32, name="bias_bank", tag="l2")
+                nc.tensor.matmul(
+                    out=bank[:], lhsT=ones_bf[:], rhs=rows[:, c * K_PASS : (c + 1) * K_PASS], start=True, stop=True
+                )
+                nc.scalar.copy(out=spread[:, c * K_PASS : (c + 1) * K_PASS], in_=bank[:])
+
+        x_grouped = keep.tile([P, ROW_TILES * K_PASS], BF16, name="x_grouped", align_bytes=64)
+        x_codes = keep.tile([P, ROW_TILES * P], U32, name="x_codes", align_bytes=64)
+        x_scales = keep.tile([P, ROW_TILES * P], U8, name="x_scales", align_bytes=64)
+        x_words = x_sb[:].bitcast(F32)
+        x_grouped_words = x_grouped[:].bitcast(F32).rearrange("p (j u) -> p j u", u=2)
+
+        def transpose_x(pair):
+            bank = psum_l2.tile([P, 2, 2 * P], F32, name="x_bank", tag="l2")
+            for half in range(2):
+                for u in range(2):
+                    nc.tensor.transpose(
+                        bank[:, u, half * P : (half + 1) * P],
+                        x_words[:, 2 * pair + half, u : X_DIM // 2 : 2],
+                        ident[:],
+                    )
+            nc.scalar.copy(
+                out=x_grouped_words[:, pair * 2 * P : (pair + 1) * 2 * P, :],
+                in_=bank[:].rearrange("p u j -> p j u"),
+            )
+
+        def quantise_x(pair):
+            nc.vector.quantize_mx(
+                out=x_codes[:, pair * 2 * P : (pair + 1) * 2 * P].bitcast(FP8X4),
+                scales=x_scales[:, pair * 2 * P : (pair + 1) * 2 * P],
+                in_=x_grouped[:, pair * 2 * K_PASS : (pair + 1) * 2 * K_PASS],
+            )
+
+        l1_banks = {}
+        pre_of = {}
+        grouped_of = {}
+        quantised_of = {}
+        acc_of = {}
+
+        def layer1(n):
+            r, head = divmod(n, 2)
+            l1_banks[n] = []
+            for c in range(HID_PASSES):
+                bank = psum_l1.tile([P, K_PASS], F32, name="l1_bank", tag="l1")
+                nc.tensor.matmul_mx(
+                    out=bank[:],
+                    lhsT=x_codes[:, r * P : (r + 1) * P].bitcast(FP8X4),
+                    lhsT_scale=x_scales[:, r * P : (r + 1) * P],
+                    rhs=w1[:, head, c * K_PASS : (c + 1) * K_PASS].bitcast(FP8X4),
+                    rhs_scale=planes[4 * c : P, w1_slot[head], :],
+                    start=True,
+                    stop=True,
+                )
+                l1_banks[n].append(bank)
+
+        def add_bias(n):
+            head = n % 2
+            pre = hidden.tile([P, HID_PASSES, K_PASS], BF16, name="pre")
+            for c in range(HID_PASSES):
+                nc.vector.tensor_tensor(
+                    out=pre[:, c, :].rearrange("p (u q e) -> p u q e", u=2, e=2),
+                    in0=l1_banks[n][c][:].rearrange("p (q u e) -> p u q e", u=2, e=2),
+                    in1=b1_all[:, head, c * K_PASS : (c + 1) * K_PASS].rearrange(
+                        "p (q u e) -> p u q e", u=2, e=2
+                    ),
+                    op=ALU.add,
+                )
+            pre_of[n] = pre
+
+        def transpose_hidden(n):
+            pre_words = pre_of[n][:].bitcast(F32)
+            grouped = hidden.tile([P, HID_PASSES * K_PASS], BF16, name="grouped", align_bytes=64)
+            banks = []
+            for pair in range(HID_PASSES // 2):
+                bank = psum_tr.tile([P, 2, 2 * P], F32, name="tr_bank", tag="tr")
+                for half in range(2):
+                    for u in range(2):
+                        nc.tensor.transpose(
+                            bank[:, u, half * P : (half + 1) * P],
+                            pre_words[:, 2 * pair + half, u * P : (u + 1) * P],
+                            ident[:],
+                        )
+                banks.append(bank)
+            for pair in range(HID_PASSES // 2):
+                nc.scalar.activation(
+                    out=grouped[:, pair * 2 * K_PASS : (pair + 1) * 2 * K_PASS].rearrange(
+                        "p (j u e) -> p j u e", u=2, e=2
+                    ),
+                    in_=banks[pair][:].bitcast(BF16).rearrange("p u (j e) -> p j u e", e=2),
+                    func=ACT.Relu,
+                )
+            grouped_of[n] = grouped
+
+        def quantise_hidden(n):
+            codes = hidden.tile([P, HID_PASSES * P], U32, name="codes", align_bytes=64)
+            scales = hidden.tile([P, HID_PASSES * P], U8, name="scales", align_bytes=64)
+            nc.vector.quantize_mx(out=codes[:].bitcast(FP8X4), scales=scales[:], in_=grouped_of[n][:])
+            quantised_of[n] = (codes, scales)
+
+        def layer2(n):
+            head = n % 2
+            codes, scales = quantised_of[n]
+            acc = psum_l2.tile([P, Y_DIM], F32, name="l2_bank", tag="l2")
+            for g in range(HID_PASSES):
+                nc.tensor.matmul_mx(
+                    out=acc[:],
+                    lhsT=codes[:, g * P : (g + 1) * P].bitcast(FP8X4),
+                    lhsT_scale=scales[:, g * P : (g + 1) * P],
+                    rhs=w2[:, head, g, :].bitcast(FP8X4),
+                    rhs_scale=planes[4 * g : P, w2_slot[head], :],
+                    start=(g == 0),
+                    stop=(g == HID_PASSES - 1),
+                )
+            acc_of[n] = acc
+
+        inv_n = 1.0 / N_ROWS
+        y_mean = keep.tile([P, Y_DIM], F32, name="y_mean")
+        y_std = keep.tile([P, Y_DIM], F32, name="y_std")
+        mean_squared = keep.tile([P, Y_DIM], F32, name="mean_squared")
+        diagonal = keep.tile([P, Y_DIM // P, P], F32, name="diagonal")
+        variance = keep.tile([P, Y_DIM], F32, name="variance")
+        stat_banks = {}
+
+        def column_sums():
+            sum_bank = psum_l2.tile([P, Y_DIM], F32, name="sum_bank", tag="l2")
+            for r in range(ROW_TILES):
+                nc.tensor.matmul(
+                    out=sum_bank[:], lhsT=ones_bf[:], rhs=y_sb[:, r, :], start=(r == 0), stop=(r == ROW_TILES - 1)
+                )
+            nc.scalar.activation(out=y_mean[:], in_=sum_bank[:], func=ACT.Copy, scale=inv_n)
+            nc.scalar.activation(out=mean_squared[:], in_=y_mean[:], func=ACT.Square)
+
+        def column_gram():
+            gram_bank = psum_l2.tile([P, Y_DIM // P, P], F32, name="gram_bank", tag="l2")
+            for b in range(Y_DIM // P):
+                for r in range(ROW_TILES):
+                    nc.tensor.matmul(
+                        out=gram_bank[:, b, :],
+                        lhsT=y_sb[:, r, b * P : (b + 1) * P],
+                        rhs=y_sb[:, r, b * P : (b + 1) * P],
+                        start=(r == 0),
+                        stop=(r == ROW_TILES - 1),
+                    )
+            stat_banks["gram"] = gram_bank
+
+        def keep_diagonal():
+            nc.vector.tensor_tensor(
+                out=diagonal[:],
+                in0=stat_banks["gram"][:],
+                in1=ident[:].unsqueeze(1).to_broadcast([P, Y_DIM // P, P]),
+                op=ALU.mult,
+            )
+
+        def spread_squares():
+            square_bank = psum_l2.tile([P, Y_DIM], F32, name="square_bank", tag="l2")
+            nc.tensor.matmul(
+                out=square_bank[:],
+                lhsT=ones_f32[:],
+                rhs=diagonal[:].rearrange("p b d -> p (b d)"),
+                start=True,
+                stop=True,
+            )
+            stat_banks["square"] = square_bank
+
+        def column_variance():
+            nc.vector.scalar_tensor_tensor(
+                out=variance[:],
+                in0=stat_banks["square"][:],
+                scalar=inv_n,
+                in1=mean_squared[:],
+                op0=ALU.mult,
+                op1=ALU.subtract,
+            )
+            nc.vector.tensor_scalar_max(out=variance[:], in0=variance[:], scalar1=0.0)
+
+        pos_sum = keep.tile([P, ROW_TILES], F32, name="pos_sum")
+        neg_sum = keep.tile([P, ROW_TILES], F32, name="neg_sum")
+        logit_of = {}
+        e_of = {}
+        diff_of = {}
+        weighted_of = {}
+
+        def leave_psum(n):
+            r, head = divmod(n, 2)
+            if head == MU:
+                mean = score.tile([P, Y_DIM], F32, name="mean")
+                nc.vector.tensor_tensor(out=mean[:], in0=acc_of[n][:], in1=b2_all[:, MU, :], op=ALU.add)
+                diff = score.tile([P, 2, Y_DIM], F32, name="diff")
+                nc.gpsimd.tensor_tensor(out=diff[:, 0, :], in0=mean[:], in1=y_sb[:, r, :], op=ALU.subtract)
+                nc.gpsimd.tensor_tensor(out=diff[:, 1, :], in0=mean[:], in1=y_mean[:], op=ALU.subtract)
+                diff_of[r] = diff
+            else:
+                logit = score.tile([P, Y_DIM], F32, name="logit")
+                nc.vector.tensor_tensor(out=logit[:], in0=acc_of[n][:], in1=b2_all[:, LV, :], op=ALU.add)
+                logit_of[r] = logit
+
+        def half_weight(r):
+            logvar = score.tile([P, Y_DIM], F32, name="logvar")
+            nc.scalar.activation(out=logvar[:], in_=logit_of[r][:], func=ACT.Tanh)
+            e = score.tile([P, Y_DIM], F32, name="e")
+            nc.scalar.activation(out=e[:], in_=logvar[:], func=ACT.Exp, scale=-0.5)
+            e_of[r] = e
+
+        def products(r):
+            e = e_of[r]
+            weighted = score.tile([P, 3, Y_DIM], F32, name="weighted")
+            nc.gpsimd.tensor_tensor(
+                out=weighted[:, 0:2, :],
+                in0=diff_of[r][:],
+                in1=e[:].unsqueeze(1).to_broadcast([P, 2, Y_DIM]),
+                op=ALU.mult,
+            )
+            nc.gpsimd.tensor_tensor(out=weighted[:, 2, :], in0=y_std[:], in1=e[:], op=ALU.mult)
+            weighted_of[r] = weighted
+
+        def sums_of_squares(r):
+            weighted = weighted_of[r]
+            squares = score.tile([P, 3, Y_DIM], F32, name="squares")
+            nc.scalar.activation(
+                out=squares[:, 0, :], in_=weighted[:, 0, :], func=ACT.Square, accum_out=pos_sum[:, r : r + 1]
+            )
+            nc.scalar.activation(
+                out=squares[:, 1:3, :], in_=weighted[:, 1:3, :], func=ACT.Square, accum_out=neg_sum[:, r : r + 1]
+            )
+
+        transpose_x(0)
+        quantise_x(0)
+        spread_bias(b1_rows[:, MU, :], b1_all[:, MU, :])
+        for s in range(-1, UNITS + 4):
+            if 0 <= s - 2 < UNITS:
+                quantise_hidden(s - 2)
+            if s == 3:
+                keep_diagonal()
+            if s == 4:
+                nc.scalar.activation(out=y_std[:], in_=variance[:], func=ACT.Sqrt)
+            if s % 2 == 0 and 0 <= (s - 4) // 2 < ROW_TILES:
+                half_weight((s - 4) // 2)
+            if 0 <= s - 1 < UNITS:
+                transpose_hidden(s - 1)
+            if s % 4 == 2 and 0 < (s + 2) // 4 < ROW_TILES // 2:
+                transpose_x((s + 2) // 4)
+            if s == 3:
+                spread_squares()
+            if 0 <= s - 2 < UNITS:
+                layer2(s - 2)
+            if 0 <= s < UNITS:
+                add_bias(s)
+            if 0 <= s + 1 < UNITS:
+                layer1(s + 1)
+            if s == -1:
+                spread_bias(b1_rows[:, LV, :], b1_all[:, LV, :])
+                spread_bias(b2_rows[:, MU, :], b2_all[:, MU, :])
+                spread_bias(b2_rows[:, LV, :], b2_all[:, LV, :])
+            if s == 1:
+                column_sums()
+            if s == 2:
+                column_gram()
+            if s % 4 == 2 and 0 < (s + 2) // 4 < ROW_TILES // 2:
+                quantise_x((s + 2) // 4)
+            if 0 <= s - 2 < UNITS:
+                leave_psum(s - 2)
+            if s == 3:
+                column_variance()
+            if s % 2 == 0 and 0 <= (s - 4) // 2 < ROW_TILES:
+                products((s - 4) // 2)
+            if s % 2 == 1 and 0 <= (s - 5) // 2 < ROW_TILES:
+                sums_of_squares((s - 5) // 2)
+
+        pos_row = keep.tile([P, ROW_TILES], F32, name="pos_row")
+        neg_row = keep.tile([P, ROW_TILES], F32, name="neg_row")
+        nc.vector.tensor_scalar(out=pos_row[:], in0=pos_sum[:], scalar1=-0.5, scalar2=None, op0=ALU.mult)
+        nc.vector.tensor_scalar(
+            out=neg_row[:], in0=neg_sum[:], scalar1=-0.5 / N_ROWS, scalar2=None, op0=ALU.mult
+        )
+        nc.sync.dma_start(out=out_0.rearrange("(p r) -> p r", r=ROW_TILES), in_=pos_row[:])
+        nc.sync.dma_start(out=out_1.rearrange("(p r) -> p r", r=ROW_TILES), in_=neg_row[:])

@@ -59,8 +59,8 @@ def tile_infoncemi_pa_kernel(
         hidden = ctx.enter_context(tc.tile_pool(name="hidden", bufs=2))
         score = ctx.enter_context(tc.tile_pool(name="score", bufs=2))
         psum_l1 = ctx.enter_context(tc.psum_pool(name="psum_l1", bufs=4))
-        psum_tr = ctx.enter_context(tc.psum_pool(name="psum_tr", bufs=2))
-        psum_l2 = ctx.enter_context(tc.psum_pool(name="psum_l2", bufs=2))
+        psum_tr = ctx.enter_context(tc.psum_pool(name="psum_tr", bufs=3))
+        psum_l2 = ctx.enter_context(tc.psum_pool(name="psum_l2", bufs=1))
 
         x_sb = keep.tile([P, ROW_TILES, X_DIM], BF16, name="x_sb")
         y_sb = keep.tile([P, ROW_TILES, Y_DIM], BF16, name="y_sb")
@@ -128,7 +128,7 @@ def tile_infoncemi_pa_kernel(
 
         def spread_bias(rows, spread):
             for c in range(rows.shape[-1] // K_PASS):
-                bank = psum_l2.tile([P, K_PASS], F32, name="bias_bank", tag="l2")
+                bank = psum_tr.tile([P, K_PASS], F32, name="bias_bank", tag="tr")
                 nc.tensor.matmul(
                     out=bank[:], lhsT=ones_bf[:], rhs=rows[:, c * K_PASS : (c + 1) * K_PASS], start=True, stop=True
                 )
@@ -141,7 +141,7 @@ def tile_infoncemi_pa_kernel(
         x_grouped_words = x_grouped[:].bitcast(F32).rearrange("p (j u) -> p j u", u=2)
 
         def transpose_x(pair):
-            bank = psum_l2.tile([P, 2, 2 * P], F32, name="x_bank", tag="l2")
+            bank = psum_tr.tile([P, 2, 2 * P], F32, name="x_bank", tag="tr")
             for half in range(2):
                 for u in range(2):
                     nc.tensor.transpose(
@@ -252,7 +252,7 @@ def tile_infoncemi_pa_kernel(
         stat_banks = {}
 
         def column_sums():
-            sum_bank = psum_l2.tile([P, Y_DIM], F32, name="sum_bank", tag="l2")
+            sum_bank = psum_tr.tile([P, Y_DIM], F32, name="sum_bank", tag="tr")
             for r in range(ROW_TILES):
                 nc.tensor.matmul(
                     out=sum_bank[:], lhsT=ones_bf[:], rhs=y_sb[:, r, :], start=(r == 0), stop=(r == ROW_TILES - 1)
@@ -261,7 +261,7 @@ def tile_infoncemi_pa_kernel(
             nc.scalar.activation(out=mean_squared[:], in_=y_mean[:], func=ACT.Square)
 
         def column_gram():
-            gram_bank = psum_l2.tile([P, Y_DIM // P, P], F32, name="gram_bank", tag="l2")
+            gram_bank = psum_tr.tile([P, Y_DIM // P, P], F32, name="gram_bank", tag="tr")
             for b in range(Y_DIM // P):
                 for r in range(ROW_TILES):
                     nc.tensor.matmul(
@@ -282,7 +282,7 @@ def tile_infoncemi_pa_kernel(
             )
 
         def spread_squares():
-            square_bank = psum_l2.tile([P, Y_DIM], F32, name="square_bank", tag="l2")
+            square_bank = psum_tr.tile([P, Y_DIM], F32, name="square_bank", tag="tr")
             nc.tensor.matmul(
                 out=square_bank[:],
                 lhsT=ones_f32[:],
@@ -305,6 +305,7 @@ def tile_infoncemi_pa_kernel(
 
         pos_sum = keep.tile([P, ROW_TILES], F32, name="pos_sum")
         neg_sum = keep.tile([P, ROW_TILES], F32, name="neg_sum")
+        mean_of = {}
         logit_of = {}
         e_of = {}
         diff_of = {}
@@ -315,14 +316,18 @@ def tile_infoncemi_pa_kernel(
             if head == MU:
                 mean = score.tile([P, Y_DIM], F32, name="mean")
                 nc.vector.tensor_tensor(out=mean[:], in0=acc_of[n][:], in1=b2_all[:, MU, :], op=ALU.add)
-                diff = score.tile([P, 2, Y_DIM], F32, name="diff")
-                nc.gpsimd.tensor_tensor(out=diff[:, 0, :], in0=mean[:], in1=y_sb[:, r, :], op=ALU.subtract)
-                nc.gpsimd.tensor_tensor(out=diff[:, 1, :], in0=mean[:], in1=y_mean[:], op=ALU.subtract)
-                diff_of[r] = diff
+                mean_of[r] = mean
             else:
                 logit = score.tile([P, Y_DIM], F32, name="logit")
                 nc.vector.tensor_tensor(out=logit[:], in0=acc_of[n][:], in1=b2_all[:, LV, :], op=ALU.add)
                 logit_of[r] = logit
+
+        def differences(r):
+            mean = mean_of[r]
+            diff = score.tile([P, 2, Y_DIM], F32, name="diff")
+            nc.gpsimd.tensor_tensor(out=diff[:, 0, :], in0=mean[:], in1=y_sb[:, r, :], op=ALU.subtract)
+            nc.gpsimd.tensor_tensor(out=diff[:, 1, :], in0=mean[:], in1=y_mean[:], op=ALU.subtract)
+            diff_of[r] = diff
 
         def half_weight(r):
             logvar = score.tile([P, Y_DIM], F32, name="logvar")
@@ -332,15 +337,16 @@ def tile_infoncemi_pa_kernel(
             e_of[r] = e
 
         def products(r):
+            engine = nc.vector if r == ROW_TILES - 1 else nc.gpsimd
             e = e_of[r]
             weighted = score.tile([P, 3, Y_DIM], F32, name="weighted")
-            nc.gpsimd.tensor_tensor(
+            engine.tensor_tensor(
                 out=weighted[:, 0:2, :],
                 in0=diff_of[r][:],
                 in1=e[:].unsqueeze(1).to_broadcast([P, 2, Y_DIM]),
                 op=ALU.mult,
             )
-            nc.gpsimd.tensor_tensor(out=weighted[:, 2, :], in0=y_std[:], in1=e[:], op=ALU.mult)
+            engine.tensor_tensor(out=weighted[:, 2, :], in0=y_std[:], in1=e[:], op=ALU.mult)
             weighted_of[r] = weighted
 
         def sums_of_squares(r):
@@ -356,17 +362,17 @@ def tile_infoncemi_pa_kernel(
         transpose_x(0)
         quantise_x(0)
         spread_bias(b1_rows[:, MU, :], b1_all[:, MU, :])
-        for s in range(-1, UNITS + 4):
+        for s in range(-1, UNITS + 6):
             if 0 <= s - 2 < UNITS:
                 quantise_hidden(s - 2)
             if s == 3:
                 keep_diagonal()
+            if 0 <= s - 1 < UNITS:
+                transpose_hidden(s - 1)
             if s == 4:
                 nc.scalar.activation(out=y_std[:], in_=variance[:], func=ACT.Sqrt)
             if s % 2 == 0 and 0 <= (s - 4) // 2 < ROW_TILES:
                 half_weight((s - 4) // 2)
-            if 0 <= s - 1 < UNITS:
-                transpose_hidden(s - 1)
             if s % 4 == 2 and 0 < (s + 2) // 4 < ROW_TILES // 2:
                 transpose_x((s + 2) // 4)
             if s == 3:
@@ -393,8 +399,10 @@ def tile_infoncemi_pa_kernel(
                 column_variance()
             if s % 2 == 0 and 0 <= (s - 4) // 2 < ROW_TILES:
                 products((s - 4) // 2)
-            if s % 2 == 1 and 0 <= (s - 5) // 2 < ROW_TILES:
-                sums_of_squares((s - 5) // 2)
+            if s % 2 == 0 and 0 <= (s - 2) // 2 < ROW_TILES:
+                differences((s - 2) // 2)
+            if s % 2 == 1 and 0 <= (s - 7) // 2 < ROW_TILES:
+                sums_of_squares((s - 7) // 2)
 
         pos_row = keep.tile([P, ROW_TILES], F32, name="pos_row")
         neg_row = keep.tile([P, ROW_TILES], F32, name="neg_row")
@@ -403,4 +411,4 @@ def tile_infoncemi_pa_kernel(
             out=neg_row[:], in0=neg_sum[:], scalar1=-0.5 / N_ROWS, scalar2=None, op0=ALU.mult
         )
         nc.sync.dma_start(out=out_0.rearrange("(p r) -> p r", r=ROW_TILES), in_=pos_row[:])
-        nc.sync.dma_start(out=out_1.rearrange("(p r) -> p r", r=ROW_TILES), in_=neg_row[:])
+        nc.scalar.dma_start(out=out_1.rearrange("(p r) -> p r", r=ROW_TILES), in_=neg_row[:])

@@ -117,13 +117,12 @@ def tile_infoncemi_pa_kernel(
             nc.scalar.dma_start(out=b2_rows[0:1, head, :], in_=b2_in[head].rearrange("(o n) -> o n", o=1))
         for head in (MU, LV):
             load_planes(w1_slot[head], w1_scales_in[head][0].rearrange("q (c n) -> c q n", c=4))
-        for head in (MU, LV):
-            load_planes(w2_slot[head], w2_scales_in[head])
-        load_w1(MU)
-        load_w1(LV)
+            load_w1(head)
         nc.sync.dma_start(out=y_sb[:], in_=y_samples.rearrange("(p r) d -> p r d", r=ROW_TILES))
+        load_planes(w2_slot[MU], w2_scales_in[MU])
         load_w2(MU)
         nc.sync.dma_start(out=x_sb[:, 2:ROW_TILES, :], in_=x_view[:, 2:ROW_TILES, :])
+        load_planes(w2_slot[LV], w2_scales_in[LV])
         load_w2(LV)
 
         def spread_bias(rows, spread):

@@ -13,6 +13,7 @@ U8 = mybir.dt.uint8
 FP8X4 = mybir.dt.float8_e4m3fn_x4
 ALU = mybir.AluOpType
 ACT = mybir.ActivationFunctionType
+AX = mybir.AxisListType
 
 P = 128
 N_ROWS = 1024
@@ -21,9 +22,21 @@ Y_DIM = 512
 HID = 2048
 ROW_TILES = N_ROWS // P
 K_PASS = 512
+PACK = 4
 HID_PASSES = HID // K_PASS
+D_TILES = Y_DIM // P
+CHUNK = 512
+CHUNKS = N_ROWS // CHUNK
+TILES_PER_CHUNK = CHUNK // P
 MU, LV = 0, 1
-UNITS = 2 * ROW_TILES
+UNIT_HEADS = (LV, MU)
+UNITS = CHUNKS * 2
+STEPS = UNITS * HID_PASSES
+
+LAG_L2 = 5
+LAG_EPI = 6
+LAG_Z = 7
+LAG_SUM = 8
 
 
 def tile_infoncemi_pa_kernel(
@@ -56,37 +69,39 @@ def tile_infoncemi_pa_kernel(
     with ExitStack() as ctx:
         ctx.enter_context(tc.manual_schedule())
         keep = ctx.enter_context(tc.tile_pool(name="keep", bufs=1))
-        hidden = ctx.enter_context(tc.tile_pool(name="hidden", bufs=2))
-        score = ctx.enter_context(tc.tile_pool(name="score", bufs=2))
+        hidden = ctx.enter_context(tc.tile_pool(name="hidden", bufs=3))
+        score = ctx.enter_context(tc.tile_pool(name="score", bufs=3))
+        weight_pool = ctx.enter_context(tc.tile_pool(name="weight_pool", bufs=2))
         psum_l1 = ctx.enter_context(tc.psum_pool(name="psum_l1", bufs=4))
-        psum_tr = ctx.enter_context(tc.psum_pool(name="psum_tr", bufs=3))
-        psum_l2 = ctx.enter_context(tc.psum_pool(name="psum_l2", bufs=1))
+        psum_l2 = ctx.enter_context(tc.psum_pool(name="psum_l2", bufs=2))
+        psum_tr = ctx.enter_context(tc.psum_pool(name="psum_tr", bufs=2))
 
         x_sb = keep.tile([P, ROW_TILES, X_DIM], BF16, name="x_sb")
         y_sb = keep.tile([P, ROW_TILES, Y_DIM], BF16, name="y_sb")
         w1 = keep.tile([P, 2, HID], U32, name="w1", align_bytes=64)
+        w1_perm = keep.tile([P, 2, HID], U32, name="w1_perm", align_bytes=64)
         w2 = keep.tile([P, 2, HID_PASSES, Y_DIM], U32, name="w2", align_bytes=64)
         planes = keep.tile([P, 4, 512], U8, name="planes", align_bytes=64)
+        planes_perm = keep.tile([P, 2, 512], U8, name="planes_perm", align_bytes=64)
         w1_slot = {MU: 0, LV: 1}
         w2_slot = {MU: 2, LV: 3}
-        b1_rows = keep.tile([P, 2, HID], BF16, name="b1_rows")
+        b1_bf = keep.tile([P, 2, HID_PASSES * PACK], BF16, name="b1_bf")
+        b1_col = keep.tile([P, 2, HID_PASSES * PACK], F32, name="b1_col")
         b2_rows = keep.tile([P, 2, Y_DIM], BF16, name="b2_rows")
-        b1_all = keep.tile([P, 2, HID], BF16, name="b1_all")
-        b2_all = keep.tile([P, 2, Y_DIM], BF16, name="b2_all")
-        ones_bf = keep.tile([P, P], BF16, name="ones_bf")
-        ones_f32 = keep.tile([P, P], F32, name="ones_f32")
+        b2_col = keep.tile([P, 2, D_TILES], F32, name="b2_col")
+        ones_bf = keep.tile([P, 2], BF16, name="ones_bf")
+        ones_f32 = keep.tile([P, 2], F32, name="ones_f32")
         ident = keep.tile([P, P], F32, name="ident")
-        one_column = keep.tile([P, 1], F32, name="one_column")
+        ident_bf = keep.tile([P, P], BF16, name="ident_bf")
+        warm = keep.tile([P, 1], F32, name="warm")
 
+        nc.vector.memset(warm[:], 0.0)
         nc.vector.memset(planes[:].bitcast(I32), 0)
-        nc.vector.memset(b1_rows[:, MU, :].bitcast(I32), 0)
         nc.vector.memset(ones_bf[:], 1.0)
-        nc.vector.memset(one_column[:], 1.0)
-        nc.vector.memset(b1_rows[:, LV, :].bitcast(I32), 0)
-        nc.vector.memset(b2_rows[:].bitcast(I32), 0)
         nc.vector.memset(ones_f32[:], 1.0)
+        nc.vector.memset(b2_rows[:].bitcast(I32), 0)
         make_identity(nc, ident[:])
-        nc.scalar.activation(out=one_column[:], in_=one_column[:], func=ACT.Sqrt)
+        make_identity(nc, ident_bf[:])
 
         def load_planes(slot, four_planes):
             for quad in range(4):
@@ -111,33 +126,45 @@ def tile_infoncemi_pa_kernel(
 
         x_view = x_samples.rearrange("(p r) k -> p r k", r=ROW_TILES)
         nc.sync.dma_start(out=x_sb[:, 0:2, :], in_=x_view[:, 0:2, :])
-        for head in (MU, LV):
-            nc.scalar.dma_start(out=b1_rows[0:1, head, :], in_=b1_in[head].rearrange("(o n) -> o n", o=1))
-        for head in (MU, LV):
+        nc.sync.dma_start(out=x_sb[:, 2:4, :], in_=x_view[:, 2:4, :])
+        for head in (LV, MU):
+            nc.scalar.dma_start(
+                out=b1_bf[:, head, :].rearrange("p (g t) -> p g t", t=PACK),
+                in_=b1_in[head].rearrange("(g p t) -> p g t", g=HID_PASSES, t=PACK),
+            )
+        for head in (LV, MU):
             nc.scalar.dma_start(out=b2_rows[0:1, head, :], in_=b2_in[head].rearrange("(o n) -> o n", o=1))
-        for head in (MU, LV):
-            load_planes(w1_slot[head], w1_scales_in[head][0].rearrange("q (c n) -> c q n", c=4))
-            load_w1(head)
+        nc.scalar.activation(out=warm[:], in_=warm[:], func=ACT.Exp)
+        load_planes(w1_slot[LV], w1_scales_in[LV][0].rearrange("q (c n) -> c q n", c=4))
+        load_w1(LV)
+        nc.sync.dma_start(out=x_sb[:, 4:ROW_TILES, :], in_=x_view[:, 4:ROW_TILES, :])
+        load_planes(w1_slot[MU], w1_scales_in[MU][0].rearrange("q (c n) -> c q n", c=4))
+        load_w1(MU)
+        load_planes(w2_slot[LV], w2_scales_in[LV])
+        load_w2(LV)
         nc.sync.dma_start(out=y_sb[:], in_=y_samples.rearrange("(p r) d -> p r d", r=ROW_TILES))
         load_planes(w2_slot[MU], w2_scales_in[MU])
         load_w2(MU)
-        nc.sync.dma_start(out=x_sb[:, 2:ROW_TILES, :], in_=x_view[:, 2:ROW_TILES, :])
-        load_planes(w2_slot[LV], w2_scales_in[LV])
-        load_w2(LV)
 
-        def spread_bias(rows, spread):
-            for c in range(rows.shape[-1] // K_PASS):
-                bank = psum_tr.tile([P, K_PASS], F32, name="bias_bank", tag="tr")
-                nc.tensor.matmul(
-                    out=bank[:], lhsT=ones_bf[:], rhs=rows[:, c * K_PASS : (c + 1) * K_PASS], start=True, stop=True
-                )
-                nc.scalar.copy(out=spread[:, c * K_PASS : (c + 1) * K_PASS], in_=bank[:])
+        def permute_planes(head):
+            nc.vector.tensor_copy(
+                out=planes_perm[:, head, :].rearrange("p (t m) -> p t m", t=PACK),
+                in_=planes[:, w1_slot[head], :].rearrange("p (m t) -> p t m", t=PACK),
+            )
+
+        def permute_w1(head, g):
+            cols = slice(g * K_PASS, (g + 1) * K_PASS)
+            nc.vector.tensor_copy(
+                out=w1_perm[:, head, cols].bitcast(I32).rearrange("p (t m) -> p t m", t=PACK),
+                in_=w1[:, head, cols].bitcast(I32).rearrange("p (m t) -> p t m", t=PACK),
+            )
 
         x_grouped = keep.tile([P, ROW_TILES * K_PASS], BF16, name="x_grouped", align_bytes=64)
         x_codes = keep.tile([P, ROW_TILES * P], U32, name="x_codes", align_bytes=64)
         x_scales = keep.tile([P, ROW_TILES * P], U8, name="x_scales", align_bytes=64)
         x_words = x_sb[:].bitcast(F32)
         x_grouped_words = x_grouped[:].bitcast(F32).rearrange("p (j u) -> p j u", u=2)
+        x_banks = {}
 
         def transpose_x(pair):
             bank = psum_tr.tile([P, 2, 2 * P], F32, name="x_bank", tag="tr")
@@ -148,9 +175,12 @@ def tile_infoncemi_pa_kernel(
                         x_words[:, 2 * pair + half, u : X_DIM // 2 : 2],
                         ident[:],
                     )
+            x_banks[pair] = bank
+
+        def regroup_x(pair):
             nc.scalar.copy(
                 out=x_grouped_words[:, pair * 2 * P : (pair + 1) * 2 * P, :],
-                in_=bank[:].rearrange("p u j -> p j u"),
+                in_=x_banks[pair][:].rearrange("p u j -> p j u"),
             )
 
         def quantise_x(pair):
@@ -160,254 +190,280 @@ def tile_infoncemi_pa_kernel(
                 in_=x_grouped[:, pair * 2 * K_PASS : (pair + 1) * 2 * K_PASS],
             )
 
+        inv_n = 1.0 / N_ROWS
+        y_t = keep.tile([P, D_TILES, N_ROWS], BF16, name="y_t")
+        y_sum = keep.tile([P, D_TILES], F32, name="y_sum")
+        y_sumsq = keep.tile([P, D_TILES], F32, name="y_sumsq")
+        y_mean = keep.tile([P, D_TILES], F32, name="y_mean")
+        mean_sq = keep.tile([P, D_TILES], F32, name="mean_sq")
+        y_var = keep.tile([P, D_TILES], F32, name="y_var")
+        centre = keep.tile([P, D_TILES], F32, name="centre")
+        diag_junk = keep.tile([P, P], F32, name="diag_junk")
+        y_banks = {}
+
+        def y_tensor(j):
+            cols = slice(j * P, (j + 1) * P)
+            turned = psum_tr.tile([P, ROW_TILES, P], BF16, name="y_turned", tag="tr")
+            for r in range(ROW_TILES):
+                nc.tensor.transpose(turned[:, r, :], y_sb[:, r, cols], ident_bf[:])
+            stats = psum_tr.tile([P, P + 2], F32, name="y_stats", tag="tr")
+            for r in range(ROW_TILES):
+                nc.tensor.matmul(
+                    out=stats[:, 0:P], lhsT=y_sb[:, r, cols], rhs=y_sb[:, r, cols],
+                    start=(r == 0), stop=(r == ROW_TILES - 1),
+                )
+            for r in range(ROW_TILES):
+                nc.tensor.matmul(
+                    out=stats[:, P : P + 1], lhsT=y_sb[:, r, cols], rhs=ones_bf[:, 0:1],
+                    start=(r == 0), stop=(r == ROW_TILES - 1),
+                )
+            y_banks[j] = (turned, stats)
+
+        def y_scalar(j):
+            nc.scalar.copy(out=y_t[:, j, :], in_=y_banks[j][0][:].rearrange("p r i -> p (r i)"))
+
+        def y_vector(j):
+            stats = y_banks[j][1]
+            nc.vector.scalar_tensor_tensor(
+                out=diag_junk[:], in0=stats[:, 0:P], scalar=1.0, in1=ident[:],
+                op0=ALU.mult, op1=ALU.mult, accum_out=y_sumsq[:, j : j + 1],
+            )
+            nc.vector.tensor_copy(out=y_sum[:, j : j + 1], in_=stats[:, P : P + 1])
+
+        def y_finish():
+            nc.vector.tensor_scalar(out=y_mean[:], in0=y_sum[:], scalar1=inv_n, scalar2=None, op0=ALU.mult)
+            nc.vector.tensor_tensor(out=mean_sq[:], in0=y_mean[:], in1=y_mean[:], op=ALU.mult)
+            nc.vector.scalar_tensor_tensor(
+                out=y_var[:], in0=y_sumsq[:], scalar=inv_n, in1=mean_sq[:], op0=ALU.mult, op1=ALU.subtract
+            )
+            nc.vector.tensor_tensor(out=centre[:], in0=b2_col[:, MU, :], in1=y_mean[:], op=ALU.subtract)
+
         l1_banks = {}
-        pre_of = {}
+        stage_of = {}
         grouped_of = {}
-        quantised_of = {}
+        codes_of = {}
         acc_of = {}
 
-        def layer1(n):
-            r, head = divmod(n, 2)
-            l1_banks[n] = []
-            for c in range(HID_PASSES):
-                bank = psum_l1.tile([P, K_PASS], F32, name="l1_bank", tag="l1")
+        def unit_of(step):
+            u, g = divmod(step, HID_PASSES)
+            chunk, k = divmod(u, 2)
+            return u, chunk, UNIT_HEADS[k], g
+
+        def layer1(step):
+            u, chunk, head, g = unit_of(step)
+            l1_banks[step] = []
+            for t in range(PACK):
+                bank = psum_l1.tile([P, CHUNK], F32, name="l1_bank", tag="l1")
+                cols = slice(g * K_PASS + t * P, g * K_PASS + (t + 1) * P)
                 nc.tensor.matmul_mx(
                     out=bank[:],
-                    lhsT=x_codes[:, r * P : (r + 1) * P].bitcast(FP8X4),
-                    lhsT_scale=x_scales[:, r * P : (r + 1) * P],
-                    rhs=w1[:, head, c * K_PASS : (c + 1) * K_PASS].bitcast(FP8X4),
-                    rhs_scale=planes[4 * c : P, w1_slot[head], :],
+                    lhsT=w1_perm[:, head, cols].bitcast(FP8X4),
+                    lhsT_scale=planes_perm[4 * g : P, head, t * P : (t + 1) * P],
+                    rhs=x_codes[:, chunk * CHUNK : (chunk + 1) * CHUNK].bitcast(FP8X4),
+                    rhs_scale=x_scales[:, chunk * CHUNK : (chunk + 1) * CHUNK],
                     start=True,
                     stop=True,
                 )
-                l1_banks[n].append(bank)
+                l1_banks[step].append(bank)
 
-        def add_bias(n):
-            head = n % 2
-            pre = hidden.tile([P, HID_PASSES, K_PASS], BF16, name="pre")
-            for c in range(HID_PASSES):
-                nc.vector.tensor_tensor(
-                    out=pre[:, c, :].rearrange("p (u q e) -> p u q e", u=2, e=2),
-                    in0=l1_banks[n][c][:].rearrange("p (q u e) -> p u q e", u=2, e=2),
-                    in1=b1_all[:, head, c * K_PASS : (c + 1) * K_PASS].rearrange(
-                        "p (q u e) -> p u q e", u=2, e=2
-                    ),
-                    op=ALU.add,
+        def new_stage(step):
+            stage_of[step] = hidden.tile([P, PACK, CHUNK], BF16, name="stage")
+
+        def leave_l1(step, t, engine):
+            u, chunk, head, g = unit_of(step)
+            bias = b1_col[:, head, g * PACK + t : g * PACK + t + 1]
+            if engine == "scalar":
+                nc.scalar.activation(out=stage_of[step][:, t, :], in_=l1_banks[step][t][:], func=ACT.Relu, bias=bias)
+            else:
+                nc.vector.tensor_scalar(
+                    out=stage_of[step][:, t, :], in0=l1_banks[step][t][:], scalar1=bias, scalar2=0.0,
+                    op0=ALU.add, op1=ALU.max,
                 )
-            pre_of[n] = pre
 
-        def transpose_hidden(n):
-            pre_words = pre_of[n][:].bitcast(F32)
-            grouped = hidden.tile([P, HID_PASSES * K_PASS], BF16, name="grouped", align_bytes=64)
-            banks = []
-            for pair in range(HID_PASSES // 2):
-                bank = psum_tr.tile([P, 2, 2 * P], F32, name="tr_bank", tag="tr")
-                for half in range(2):
-                    for u in range(2):
-                        nc.tensor.transpose(
-                            bank[:, u, half * P : (half + 1) * P],
-                            pre_words[:, 2 * pair + half, u * P : (u + 1) * P],
-                            ident[:],
-                        )
-                banks.append(bank)
-            for pair in range(HID_PASSES // 2):
-                nc.scalar.activation(
-                    out=grouped[:, pair * 2 * K_PASS : (pair + 1) * 2 * K_PASS].rearrange(
-                        "p (j u e) -> p j u e", u=2, e=2
-                    ),
-                    in_=banks[pair][:].bitcast(BF16).rearrange("p u (j e) -> p j u e", e=2),
-                    func=ACT.Relu,
-                )
-            grouped_of[n] = grouped
+        def interleave(step):
+            grouped = hidden.tile([P, CHUNK, PACK], BF16, name="grouped", align_bytes=64)
+            nc.vector.tensor_copy(out=grouped[:], in_=stage_of[step][:].rearrange("p t n -> p n t"))
+            grouped_of[step] = grouped
 
-        def quantise_hidden(n):
-            codes = hidden.tile([P, HID_PASSES * P], U32, name="codes", align_bytes=64)
-            scales = hidden.tile([P, HID_PASSES * P], U8, name="scales", align_bytes=64)
-            nc.vector.quantize_mx(out=codes[:].bitcast(FP8X4), scales=scales[:], in_=grouped_of[n][:])
-            quantised_of[n] = (codes, scales)
+        def quantise_hidden(step):
+            u, chunk, head, g = unit_of(step)
+            if g == 0:
+                codes = hidden.tile([P, HID_PASSES, CHUNK], U32, name="codes", align_bytes=64)
+                scales = hidden.tile([P, HID_PASSES, CHUNK], U8, name="scales", align_bytes=64)
+                codes_of[u] = (codes, scales)
+            codes, scales = codes_of[u]
+            nc.vector.quantize_mx(
+                out=codes[:, g, :].bitcast(FP8X4),
+                scales=scales[:, g, :],
+                in_=grouped_of[step][:].rearrange("p n t -> p (n t)"),
+            )
 
-        def layer2(n):
-            head = n % 2
-            codes, scales = quantised_of[n]
-            acc = psum_l2.tile([P, Y_DIM], F32, name="l2_bank", tag="l2")
+        def layer2(q):
+            u, chunk, head, j = unit_of(q)
+            codes, scales = codes_of[u]
+            acc = psum_l2.tile([P, CHUNK], F32, name="l2_bank", tag="l2")
             for g in range(HID_PASSES):
                 nc.tensor.matmul_mx(
                     out=acc[:],
-                    lhsT=codes[:, g * P : (g + 1) * P].bitcast(FP8X4),
-                    lhsT_scale=scales[:, g * P : (g + 1) * P],
-                    rhs=w2[:, head, g, :].bitcast(FP8X4),
-                    rhs_scale=planes[4 * g : P, w2_slot[head], :],
+                    lhsT=w2[:, head, g, j * P : (j + 1) * P].bitcast(FP8X4),
+                    lhsT_scale=planes[4 * g : P, w2_slot[head], j * P : (j + 1) * P],
+                    rhs=codes[:, g, :].bitcast(FP8X4),
+                    rhs_scale=scales[:, g, :],
                     start=(g == 0),
                     stop=(g == HID_PASSES - 1),
                 )
-            acc_of[n] = acc
+            acc_of[q] = acc
 
-        inv_n = 1.0 / N_ROWS
-        y_mean = keep.tile([P, Y_DIM], F32, name="y_mean")
-        y_std = keep.tile([P, Y_DIM], F32, name="y_std")
-        mean_squared = keep.tile([P, Y_DIM], F32, name="mean_squared")
-        diagonal = keep.tile([P, Y_DIM // P, P], F32, name="diagonal")
-        variance = keep.tile([P, Y_DIM], F32, name="variance")
-        stat_banks = {}
-
-        def column_sums():
-            sum_bank = psum_tr.tile([P, Y_DIM], F32, name="sum_bank", tag="tr")
-            for r in range(ROW_TILES):
-                nc.tensor.matmul(
-                    out=sum_bank[:], lhsT=ones_bf[:], rhs=y_sb[:, r, :], start=(r == 0), stop=(r == ROW_TILES - 1)
-                )
-            nc.scalar.activation(out=y_mean[:], in_=sum_bank[:], func=ACT.Copy, scale=inv_n)
-            nc.scalar.activation(out=mean_squared[:], in_=y_mean[:], func=ACT.Square)
-
-        def column_gram():
-            gram_bank = psum_tr.tile([P, Y_DIM // P, P], F32, name="gram_bank", tag="tr")
-            for b in range(Y_DIM // P):
-                for r in range(ROW_TILES):
-                    nc.tensor.matmul(
-                        out=gram_bank[:, b, :],
-                        lhsT=y_sb[:, r, b * P : (b + 1) * P],
-                        rhs=y_sb[:, r, b * P : (b + 1) * P],
-                        start=(r == 0),
-                        stop=(r == ROW_TILES - 1),
-                    )
-            stat_banks["gram"] = gram_bank
-
-        def keep_diagonal():
-            nc.vector.tensor_tensor(
-                out=diagonal[:],
-                in0=stat_banks["gram"][:],
-                in1=ident[:].unsqueeze(1).to_broadcast([P, Y_DIM // P, P]),
-                op=ALU.mult,
-            )
-
-        def spread_squares():
-            square_bank = psum_tr.tile([P, Y_DIM], F32, name="square_bank", tag="tr")
-            nc.tensor.matmul(
-                out=square_bank[:],
-                lhsT=ones_f32[:],
-                rhs=diagonal[:].rearrange("p b d -> p (b d)"),
-                start=True,
-                stop=True,
-            )
-            stat_banks["square"] = square_bank
-
-        def column_variance():
-            nc.vector.scalar_tensor_tensor(
-                out=variance[:],
-                in0=stat_banks["square"][:],
-                scalar=inv_n,
-                in1=mean_squared[:],
-                op0=ALU.mult,
-                op1=ALU.subtract,
-            )
-            nc.vector.tensor_scalar_max(out=variance[:], in0=variance[:], scalar1=0.0)
-
-        pos_sum = keep.tile([P, ROW_TILES], F32, name="pos_sum")
-        neg_sum = keep.tile([P, ROW_TILES], F32, name="neg_sum")
-        mean_of = {}
-        logit_of = {}
-        e_of = {}
+        logvar_of = {}
+        weight_of = {}
         diff_of = {}
-        weighted_of = {}
+        sq_own_of = {}
+        sq_all_of = {}
+        term_of = {}
+        sums_bank = {}
 
-        def leave_psum(n):
-            r, head = divmod(n, 2)
-            if head == MU:
-                mean = score.tile([P, Y_DIM], F32, name="mean")
-                nc.vector.tensor_tensor(out=mean[:], in0=acc_of[n][:], in1=b2_all[:, MU, :], op=ALU.add)
-                mean_of[r] = mean
+        def first_scalar(q):
+            u, chunk, head, j = unit_of(q)
+            if head == LV:
+                logvar = score.tile([P, CHUNK], F32, name="logvar")
+                nc.scalar.activation(out=logvar[:], in_=acc_of[q][:], func=ACT.Tanh, bias=b2_col[:, LV, j : j + 1])
+                logvar_of[q] = logvar
             else:
-                logit = score.tile([P, Y_DIM], F32, name="logit")
-                nc.vector.tensor_tensor(out=logit[:], in0=acc_of[n][:], in1=b2_all[:, LV, :], op=ALU.add)
-                logit_of[r] = logit
+                sq_all = score.tile([P, CHUNK], F32, name="sq_all")
+                nc.scalar.activation(out=sq_all[:], in_=acc_of[q][:], func=ACT.Square, bias=centre[:, j : j + 1])
+                sq_all_of[q] = sq_all
 
-        def differences(r):
-            mean = mean_of[r]
-            diff = score.tile([P, 2, Y_DIM], F32, name="diff")
-            nc.gpsimd.tensor_tensor(out=diff[:, 0, :], in0=mean[:], in1=y_sb[:, r, :], op=ALU.subtract)
-            nc.gpsimd.tensor_tensor(out=diff[:, 1, :], in0=mean[:], in1=y_mean[:], op=ALU.subtract)
-            diff_of[r] = diff
+        def first_vector(q):
+            u, chunk, head, j = unit_of(q)
+            if head == MU:
+                diff = score.tile([P, CHUNK], F32, name="diff")
+                nc.vector.scalar_tensor_tensor(
+                    out=diff[:], in0=acc_of[q][:], scalar=b2_col[:, MU, j : j + 1],
+                    in1=y_t[:, j, chunk * CHUNK : (chunk + 1) * CHUNK], op0=ALU.add, op1=ALU.subtract,
+                )
+                diff_of[q] = diff
 
-        def half_weight(r):
-            logvar = score.tile([P, Y_DIM], F32, name="logvar")
-            nc.scalar.activation(out=logvar[:], in_=logit_of[r][:], func=ACT.Tanh)
-            e = score.tile([P, Y_DIM], F32, name="e")
-            nc.scalar.activation(out=e[:], in_=logvar[:], func=ACT.Exp, scale=-0.5)
-            e_of[r] = e
+        def second_scalar(q):
+            u, chunk, head, j = unit_of(q)
+            if head == LV:
+                if j == 0:
+                    weight_of[chunk] = weight_pool.tile([P, D_TILES, CHUNK], F32, name="weight")
+                nc.scalar.activation(out=weight_of[chunk][:, j, :], in_=logvar_of[q][:], func=ACT.Exp, scale=-1.0)
+            else:
+                sq_own = score.tile([P, CHUNK], F32, name="sq_own")
+                nc.scalar.activation(out=sq_own[:], in_=diff_of[q][:], func=ACT.Square)
+                sq_own_of[q] = sq_own
 
-        def products(r):
-            engine = nc.vector if r == ROW_TILES - 1 else nc.gpsimd
-            e = e_of[r]
-            weighted = score.tile([P, 3, Y_DIM], F32, name="weighted")
-            engine.tensor_tensor(
-                out=weighted[:, 0:2, :],
-                in0=diff_of[r][:],
-                in1=e[:].unsqueeze(1).to_broadcast([P, 2, Y_DIM]),
-                op=ALU.mult,
-            )
-            engine.tensor_tensor(out=weighted[:, 2, :], in0=y_std[:], in1=e[:], op=ALU.mult)
-            weighted_of[r] = weighted
+        def weighted_terms(q):
+            u, chunk, head, j = unit_of(q)
+            if head == MU:
+                term_all = score.tile([P, CHUNK], F32, name="term_all")
+                nc.vector.scalar_tensor_tensor(
+                    out=term_all[:], in0=sq_all_of[q][:], scalar=y_var[:, j : j + 1],
+                    in1=weight_of[chunk][:, j, :], op0=ALU.add, op1=ALU.mult,
+                )
+                term_own = score.tile([P, CHUNK], F32, name="term_own")
+                nc.vector.tensor_tensor(out=term_own[:], in0=sq_own_of[q][:], in1=weight_of[chunk][:, j, :], op=ALU.mult)
+                term_of[q] = (term_own, term_all)
 
-        def sums_of_squares(r):
-            weighted = weighted_of[r]
-            squares = score.tile([P, 3, Y_DIM], F32, name="squares")
-            nc.scalar.activation(
-                out=squares[:, 0, :], in_=weighted[:, 0, :], func=ACT.Square, accum_out=pos_sum[:, r : r + 1]
-            )
-            nc.scalar.activation(
-                out=squares[:, 1:3, :], in_=weighted[:, 1:3, :], func=ACT.Square, accum_out=neg_sum[:, r : r + 1]
-            )
+        def sum_over_d(q):
+            u, chunk, head, j = unit_of(q)
+            if head == MU:
+                if "bank" not in sums_bank:
+                    sums_bank["bank"] = psum_tr.tile([P, 2 * ROW_TILES * D_TILES], F32, name="sums", tag="tr")
+                bank = sums_bank["bank"]
+                for o in range(2):
+                    for i in range(TILES_PER_CHUNK):
+                        r = chunk * TILES_PER_CHUNK + i
+                        col = (o * ROW_TILES + r) * D_TILES + j
+                        nc.tensor.matmul(
+                            out=bank[:, col : col + 1], lhsT=term_of[q][o][:, i * P : (i + 1) * P],
+                            rhs=ones_f32[:, 0:1], start=True, stop=True,
+                        )
+
+        def vector_share(step):
+            q = step - LAG_EPI
+            if 0 <= q < STEPS and unit_of(q)[2] == LV:
+                return 1
+            return 0
 
         transpose_x(0)
+        transpose_x(1)
+        regroup_x(0)
+        regroup_x(1)
+        nc.vector.tensor_copy(out=b1_col[:], in_=b1_bf[:])
         quantise_x(0)
-        spread_bias(b1_rows[:, MU, :], b1_all[:, MU, :])
-        for s in range(-1, UNITS + 6):
-            if 0 <= s - 2 < UNITS:
-                quantise_hidden(s - 2)
-            if s == 3:
-                keep_diagonal()
-            if 0 <= s - 1 < UNITS:
-                transpose_hidden(s - 1)
-            if s == 4:
-                nc.scalar.activation(out=y_std[:], in_=variance[:], func=ACT.Sqrt)
-            if s % 2 == 0 and 0 <= (s - 4) // 2 < ROW_TILES:
-                half_weight((s - 4) // 2)
-            if s % 4 == 2 and 0 < (s + 2) // 4 < ROW_TILES // 2:
-                transpose_x((s + 2) // 4)
-            if s == 3:
-                spread_squares()
-            if 0 <= s - 2 < UNITS:
-                layer2(s - 2)
-            if 0 <= s < UNITS:
-                add_bias(s)
-            if 0 <= s + 1 < UNITS:
-                layer1(s + 1)
-            if s == -1:
-                spread_bias(b1_rows[:, LV, :], b1_all[:, LV, :])
-                spread_bias(b2_rows[:, MU, :], b2_all[:, MU, :])
-                spread_bias(b2_rows[:, LV, :], b2_all[:, LV, :])
-            if s == 1:
-                column_sums()
-            if s == 2:
-                column_gram()
-            if s % 4 == 2 and 0 < (s + 2) // 4 < ROW_TILES // 2:
-                quantise_x((s + 2) // 4)
-            if 0 <= s - 2 < UNITS:
-                leave_psum(s - 2)
-            if s == 3:
-                column_variance()
-            if s % 2 == 0 and 0 <= (s - 4) // 2 < ROW_TILES:
-                products((s - 4) // 2)
-            if s % 2 == 0 and 0 <= (s - 2) // 2 < ROW_TILES:
-                differences((s - 2) // 2)
-            if s % 2 == 1 and 0 <= (s - 7) // 2 < ROW_TILES:
-                sums_of_squares((s - 7) // 2)
+        quantise_x(1)
+        permute_planes(LV)
+        permute_w1(LV, 0)
+        b2_bank = psum_tr.tile([P, 2, D_TILES], F32, name="b2_bank", tag="tr")
+        for head in (LV, MU):
+            for j in range(D_TILES):
+                nc.tensor.matmul(
+                    out=b2_bank[:, head, j : j + 1], lhsT=b2_rows[:, head, j * P : (j + 1) * P],
+                    rhs=ones_bf[:, 0:1], start=True, stop=True,
+                )
 
-        pos_row = keep.tile([P, ROW_TILES], F32, name="pos_row")
-        neg_row = keep.tile([P, ROW_TILES], F32, name="neg_row")
-        nc.vector.tensor_scalar(out=pos_row[:], in0=pos_sum[:], scalar1=-0.5, scalar2=None, op0=ALU.mult)
-        nc.vector.tensor_scalar(
-            out=neg_row[:], in0=neg_sum[:], scalar1=-0.5 / N_ROWS, scalar2=None, op0=ALU.mult
+        for i in range(STEPS + LAG_SUM + 1):
+            if i < STEPS:
+                layer1(i)
+            if i in (2, 3):
+                transpose_x(i)
+            if 6 <= i < 6 + D_TILES:
+                y_tensor(i - 6)
+            if 0 <= i - LAG_L2 < STEPS:
+                layer2(i - LAG_L2)
+            if 0 <= i - LAG_SUM < STEPS:
+                sum_over_d(i - LAG_SUM)
+
+            if 0 <= i - 1 < STEPS:
+                interleave(i - 1)
+            if 0 <= i - LAG_EPI < STEPS:
+                first_scalar(i - LAG_EPI)
+                first_vector(i - LAG_EPI)
+            if i < STEPS:
+                new_stage(i)
+                share = vector_share(i)
+                for t in range(PACK - share):
+                    leave_l1(i, t, "scalar")
+                for t in range(PACK - share, PACK):
+                    leave_l1(i, t, "vector")
+            if i in (2, 3):
+                regroup_x(i)
+            if 6 <= i < 6 + D_TILES:
+                y_scalar(i - 6)
+            if 0 <= i - 1 < STEPS:
+                quantise_hidden(i - 1)
+            if 0 <= i - LAG_EPI < STEPS:
+                second_scalar(i - LAG_EPI)
+            if 0 <= i - LAG_Z < STEPS:
+                weighted_terms(i - LAG_Z)
+            if i < 3:
+                permute_w1(LV, i + 1)
+            if i == 0:
+                nc.vector.tensor_copy(out=b2_col[:], in_=b2_bank[:])
+            if i == 3:
+                permute_planes(MU)
+            if 3 <= i < 3 + HID_PASSES:
+                permute_w1(MU, i - 3)
+            if i in (3, 4):
+                quantise_x(i - 1)
+            if 6 <= i < 6 + D_TILES:
+                y_vector(i - 6)
+            if i == 6 + D_TILES - 1:
+                y_finish()
+
+        totals = keep.tile([P, 2 * ROW_TILES], F32, name="totals")
+        result = keep.tile([P, 2, ROW_TILES], F32, name="result")
+        nc.vector.tensor_reduce(
+            out=totals[:], in_=sums_bank["bank"][:].rearrange("p (c j) -> p c j", j=D_TILES), axis=AX.X, op=ALU.add
         )
-        nc.sync.dma_start(out=out_0.rearrange("(p r) -> p r", r=ROW_TILES), in_=pos_row[:])
-        nc.scalar.dma_start(out=out_1.rearrange("(p r) -> p r", r=ROW_TILES), in_=neg_row[:])
+        nc.vector.tensor_scalar(
+            out=result[:, 0, :], in0=totals[:, 0:ROW_TILES], scalar1=-0.5, scalar2=None, op0=ALU.mult
+        )
+        nc.vector.tensor_scalar(
+            out=result[:, 1, :], in0=totals[:, ROW_TILES : 2 * ROW_TILES], scalar1=-0.5 / N_ROWS, scalar2=None,
+            op0=ALU.mult,
+        )
+        nc.sync.dma_start(out=out_0.rearrange("(p r) -> p r", r=ROW_TILES), in_=result[:, 0, :])
+        nc.scalar.dma_start(out=out_1.rearrange("(p r) -> p r", r=ROW_TILES), in_=result[:, 1, :])

@@ -29,7 +29,7 @@ CHUNK = 512
 CHUNKS = N_ROWS // CHUNK
 TILES_PER_CHUNK = CHUNK // P
 MU, LV = 0, 1
-UNIT_HEADS = (LV, MU)
+UNIT_HEADS = (MU, LV)
 UNITS = CHUNKS * 2
 STEPS = UNITS * HID_PASSES
 
@@ -71,7 +71,7 @@ def tile_infoncemi_pa_kernel(
         keep = ctx.enter_context(tc.tile_pool(name="keep", bufs=1))
         hidden = ctx.enter_context(tc.tile_pool(name="hidden", bufs=3))
         score = ctx.enter_context(tc.tile_pool(name="score", bufs=3))
-        weight_pool = ctx.enter_context(tc.tile_pool(name="weight_pool", bufs=2))
+        chunk_pool = ctx.enter_context(tc.tile_pool(name="chunk_pool", bufs=2))
         psum_l1 = ctx.enter_context(tc.psum_pool(name="psum_l1", bufs=4))
         psum_l2 = ctx.enter_context(tc.psum_pool(name="psum_l2", bufs=2))
         psum_tr = ctx.enter_context(tc.psum_pool(name="psum_tr", bufs=2))
@@ -127,7 +127,7 @@ def tile_infoncemi_pa_kernel(
         x_view = x_samples.rearrange("(p r) k -> p r k", r=ROW_TILES)
         nc.sync.dma_start(out=x_sb[:, 0:2, :], in_=x_view[:, 0:2, :])
         nc.sync.dma_start(out=x_sb[:, 2:4, :], in_=x_view[:, 2:4, :])
-        for head in (LV, MU):
+        for head in (MU, LV):
             nc.scalar.dma_start(
                 out=b1_bf[:, head, :].rearrange("p (g t) -> p g t", t=PACK),
                 in_=b1_in[head].rearrange("(g p t) -> p g t", g=HID_PASSES, t=PACK),
@@ -135,16 +135,16 @@ def tile_infoncemi_pa_kernel(
         for head in (LV, MU):
             nc.scalar.dma_start(out=b2_rows[0:1, head, :], in_=b2_in[head].rearrange("(o n) -> o n", o=1))
         nc.scalar.activation(out=warm[:], in_=warm[:], func=ACT.Exp)
-        load_planes(w1_slot[LV], w1_scales_in[LV][0].rearrange("q (c n) -> c q n", c=4))
-        load_w1(LV)
-        nc.sync.dma_start(out=x_sb[:, 4:ROW_TILES, :], in_=x_view[:, 4:ROW_TILES, :])
         load_planes(w1_slot[MU], w1_scales_in[MU][0].rearrange("q (c n) -> c q n", c=4))
         load_w1(MU)
-        load_planes(w2_slot[LV], w2_scales_in[LV])
-        load_w2(LV)
         nc.sync.dma_start(out=y_sb[:], in_=y_samples.rearrange("(p r) d -> p r d", r=ROW_TILES))
+        load_planes(w1_slot[LV], w1_scales_in[LV][0].rearrange("q (c n) -> c q n", c=4))
+        load_w1(LV)
         load_planes(w2_slot[MU], w2_scales_in[MU])
         load_w2(MU)
+        nc.sync.dma_start(out=x_sb[:, 4:ROW_TILES, :], in_=x_view[:, 4:ROW_TILES, :])
+        load_planes(w2_slot[LV], w2_scales_in[LV])
+        load_w2(LV)
 
         def permute_planes(head):
             nc.vector.tensor_copy(
@@ -317,10 +317,9 @@ def tile_infoncemi_pa_kernel(
         logvar_of = {}
         weight_of = {}
         diff_of = {}
-        sq_own_of = {}
-        sq_all_of = {}
-        term_of = {}
-        sums_bank = {}
+        squares_of = {}
+        OWN, ALL = 0, 1
+        totals = keep.tile([P, 2, ROW_TILES], F32, name="totals")
 
         def first_scalar(q):
             u, chunk, head, j = unit_of(q)
@@ -329,9 +328,11 @@ def tile_infoncemi_pa_kernel(
                 nc.scalar.activation(out=logvar[:], in_=acc_of[q][:], func=ACT.Tanh, bias=b2_col[:, LV, j : j + 1])
                 logvar_of[q] = logvar
             else:
-                sq_all = score.tile([P, CHUNK], F32, name="sq_all")
-                nc.scalar.activation(out=sq_all[:], in_=acc_of[q][:], func=ACT.Square, bias=centre[:, j : j + 1])
-                sq_all_of[q] = sq_all
+                if j == 0:
+                    squares_of[chunk] = chunk_pool.tile([P, 2, D_TILES, CHUNK], F32, name="squares")
+                nc.scalar.activation(
+                    out=squares_of[chunk][:, ALL, j, :], in_=acc_of[q][:], func=ACT.Square, bias=centre[:, j : j + 1]
+                )
 
         def first_vector(q):
             u, chunk, head, j = unit_of(q)
@@ -346,46 +347,44 @@ def tile_infoncemi_pa_kernel(
         def second_scalar(q):
             u, chunk, head, j = unit_of(q)
             if head == LV:
-                if j == 0:
-                    weight_of[chunk] = weight_pool.tile([P, D_TILES, CHUNK], F32, name="weight")
-                nc.scalar.activation(out=weight_of[chunk][:, j, :], in_=logvar_of[q][:], func=ACT.Exp, scale=-1.0)
+                weight = score.tile([P, CHUNK], F32, name="weight")
+                nc.scalar.activation(out=weight[:], in_=logvar_of[q][:], func=ACT.Exp, scale=-1.0)
+                weight_of[q] = weight
             else:
-                sq_own = score.tile([P, CHUNK], F32, name="sq_own")
-                nc.scalar.activation(out=sq_own[:], in_=diff_of[q][:], func=ACT.Square)
-                sq_own_of[q] = sq_own
+                nc.scalar.activation(out=squares_of[chunk][:, OWN, j, :], in_=diff_of[q][:], func=ACT.Square)
 
         def weighted_terms(q):
             u, chunk, head, j = unit_of(q)
-            if head == MU:
-                term_all = score.tile([P, CHUNK], F32, name="term_all")
+            if head == LV:
+                sq = squares_of[chunk]
                 nc.vector.scalar_tensor_tensor(
-                    out=term_all[:], in0=sq_all_of[q][:], scalar=y_var[:, j : j + 1],
-                    in1=weight_of[chunk][:, j, :], op0=ALU.add, op1=ALU.mult,
+                    out=sq[:, ALL, j, :], in0=sq[:, ALL, j, :], scalar=y_var[:, j : j + 1],
+                    in1=weight_of[q][:], op0=ALU.add, op1=ALU.mult,
                 )
-                term_own = score.tile([P, CHUNK], F32, name="term_own")
-                nc.vector.tensor_tensor(out=term_own[:], in0=sq_own_of[q][:], in1=weight_of[chunk][:, j, :], op=ALU.mult)
-                term_of[q] = (term_own, term_all)
+                nc.vector.tensor_tensor(out=sq[:, OWN, j, :], in0=sq[:, OWN, j, :], in1=weight_of[q][:], op=ALU.mult)
 
-        def sum_over_d(q):
-            u, chunk, head, j = unit_of(q)
-            if head == MU:
-                if "bank" not in sums_bank:
-                    sums_bank["bank"] = psum_tr.tile([P, 2 * ROW_TILES * D_TILES], F32, name="sums", tag="tr")
-                bank = sums_bank["bank"]
-                for o in range(2):
-                    for i in range(TILES_PER_CHUNK):
-                        r = chunk * TILES_PER_CHUNK + i
-                        col = (o * ROW_TILES + r) * D_TILES + j
+        sum_banks = {}
+
+        def sum_over_d_tensor(chunk):
+            for o in (OWN, ALL):
+                bank = psum_tr.tile([P, TILES_PER_CHUNK, P], F32, name="sum_bank", tag="tr")
+                for i in range(TILES_PER_CHUNK):
+                    for j in range(D_TILES):
                         nc.tensor.matmul(
-                            out=bank[:, col : col + 1], lhsT=term_of[q][o][:, i * P : (i + 1) * P],
-                            rhs=ones_f32[:, 0:1], start=True, stop=True,
+                            out=bank[:, i, :], lhsT=squares_of[chunk][:, o, j, i * P : (i + 1) * P], rhs=ident[:],
+                            is_transpose=True, start=(j == 0), stop=(j == D_TILES - 1),
                         )
+                sum_banks[(chunk, o)] = bank
+
+        def sum_over_d_vector(chunk):
+            for o in (OWN, ALL):
+                nc.vector.tensor_reduce(
+                    out=totals[:, o, chunk * TILES_PER_CHUNK : (chunk + 1) * TILES_PER_CHUNK],
+                    in_=sum_banks[(chunk, o)][:], axis=AX.X, op=ALU.add,
+                )
 
         def vector_share(step):
-            q = step - LAG_EPI
-            if 0 <= q < STEPS and unit_of(q)[2] == LV:
-                return 1
-            return 0
+            return 1
 
         transpose_x(0)
         transpose_x(1)
@@ -394,27 +393,30 @@ def tile_infoncemi_pa_kernel(
         nc.vector.tensor_copy(out=b1_col[:], in_=b1_bf[:])
         quantise_x(0)
         quantise_x(1)
-        permute_planes(LV)
-        permute_w1(LV, 0)
+        permute_planes(MU)
+        for g in range(HID_PASSES):
+            permute_w1(MU, g)
         b2_bank = psum_tr.tile([P, 2, D_TILES], F32, name="b2_bank", tag="tr")
-        for head in (LV, MU):
+        for head in (MU, LV):
             for j in range(D_TILES):
                 nc.tensor.matmul(
                     out=b2_bank[:, head, j : j + 1], lhsT=b2_rows[:, head, j * P : (j + 1) * P],
                     rhs=ones_bf[:, 0:1], start=True, stop=True,
                 )
 
+        Y_FROM = 2
+        X_FROM = 4
         for i in range(STEPS + LAG_SUM + 1):
             if i < STEPS:
                 layer1(i)
-            if i in (2, 3):
-                transpose_x(i)
-            if 6 <= i < 6 + D_TILES:
-                y_tensor(i - 6)
+            if X_FROM <= i < X_FROM + 2:
+                transpose_x(i - X_FROM + 2)
+            if Y_FROM <= i < Y_FROM + D_TILES:
+                y_tensor(i - Y_FROM)
             if 0 <= i - LAG_L2 < STEPS:
                 layer2(i - LAG_L2)
-            if 0 <= i - LAG_SUM < STEPS:
-                sum_over_d(i - LAG_SUM)
+            if i - LAG_SUM in (2 * HID_PASSES - 1, 4 * HID_PASSES - 1):
+                sum_over_d_tensor((i - LAG_SUM) // (2 * HID_PASSES))
 
             if 0 <= i - 1 < STEPS:
                 interleave(i - 1)
@@ -428,42 +430,35 @@ def tile_infoncemi_pa_kernel(
                     leave_l1(i, t, "scalar")
                 for t in range(PACK - share, PACK):
                     leave_l1(i, t, "vector")
-            if i in (2, 3):
-                regroup_x(i)
-            if 6 <= i < 6 + D_TILES:
-                y_scalar(i - 6)
+            if X_FROM <= i < X_FROM + 2:
+                regroup_x(i - X_FROM + 2)
+            if Y_FROM <= i < Y_FROM + D_TILES:
+                y_scalar(i - Y_FROM)
             if 0 <= i - 1 < STEPS:
                 quantise_hidden(i - 1)
             if 0 <= i - LAG_EPI < STEPS:
                 second_scalar(i - LAG_EPI)
             if 0 <= i - LAG_Z < STEPS:
                 weighted_terms(i - LAG_Z)
-            if i < 3:
-                permute_w1(LV, i + 1)
+            if i - LAG_SUM in (2 * HID_PASSES - 1, 4 * HID_PASSES - 1):
+                sum_over_d_vector((i - LAG_SUM) // (2 * HID_PASSES))
             if i == 0:
                 nc.vector.tensor_copy(out=b2_col[:], in_=b2_bank[:])
-            if i == 3:
-                permute_planes(MU)
-            if 3 <= i < 3 + HID_PASSES:
-                permute_w1(MU, i - 3)
-            if i in (3, 4):
-                quantise_x(i - 1)
-            if 6 <= i < 6 + D_TILES:
-                y_vector(i - 6)
-            if i == 6 + D_TILES - 1:
+            if i == 2:
+                permute_planes(LV)
+            if 2 <= i < 2 + HID_PASSES:
+                permute_w1(LV, i - 2)
+            if X_FROM + 1 <= i < X_FROM + 3:
+                quantise_x(i - X_FROM + 1)
+            if Y_FROM <= i < Y_FROM + D_TILES:
+                y_vector(i - Y_FROM)
+            if i == Y_FROM + D_TILES - 1:
                 y_finish()
 
-        totals = keep.tile([P, 2 * ROW_TILES], F32, name="totals")
         result = keep.tile([P, 2, ROW_TILES], F32, name="result")
-        nc.vector.tensor_reduce(
-            out=totals[:], in_=sums_bank["bank"][:].rearrange("p (c j) -> p c j", j=D_TILES), axis=AX.X, op=ALU.add
-        )
+        nc.vector.tensor_scalar(out=result[:, OWN, :], in0=totals[:, OWN, :], scalar1=-0.5, scalar2=None, op0=ALU.mult)
         nc.vector.tensor_scalar(
-            out=result[:, 0, :], in0=totals[:, 0:ROW_TILES], scalar1=-0.5, scalar2=None, op0=ALU.mult
+            out=result[:, ALL, :], in0=totals[:, ALL, :], scalar1=-0.5 / N_ROWS, scalar2=None, op0=ALU.mult
         )
-        nc.vector.tensor_scalar(
-            out=result[:, 1, :], in0=totals[:, ROW_TILES : 2 * ROW_TILES], scalar1=-0.5 / N_ROWS, scalar2=None,
-            op0=ALU.mult,
-        )
-        nc.sync.dma_start(out=out_0.rearrange("(p r) -> p r", r=ROW_TILES), in_=result[:, 0, :])
-        nc.scalar.dma_start(out=out_1.rearrange("(p r) -> p r", r=ROW_TILES), in_=result[:, 1, :])
+        nc.sync.dma_start(out=out_0.rearrange("(p r) -> p r", r=ROW_TILES), in_=result[:, OWN, :])
+        nc.scalar.dma_start(out=out_1.rearrange("(p r) -> p r", r=ROW_TILES), in_=result[:, ALL, :])

@@ -29,8 +29,8 @@ CHUNK = 512
 CHUNKS = N_ROWS // CHUNK
 TILES_PER_CHUNK = CHUNK // P
 MU, LV = 0, 1
-UNIT_HEADS = (MU, LV)
-UNITS = CHUNKS * 2
+UNIT_ORDER = ((0, LV), (0, MU), (1, MU), (1, LV))
+UNITS = len(UNIT_ORDER)
 STEPS = UNITS * HID_PASSES
 
 LAG_L2 = 5
@@ -127,7 +127,7 @@ def tile_infoncemi_pa_kernel(
         x_view = x_samples.rearrange("(p r) k -> p r k", r=ROW_TILES)
         nc.sync.dma_start(out=x_sb[:, 0:2, :], in_=x_view[:, 0:2, :])
         nc.sync.dma_start(out=x_sb[:, 2:4, :], in_=x_view[:, 2:4, :])
-        for head in (MU, LV):
+        for head in (LV, MU):
             nc.scalar.dma_start(
                 out=b1_bf[:, head, :].rearrange("p (g t) -> p g t", t=PACK),
                 in_=b1_in[head].rearrange("(g p t) -> p g t", g=HID_PASSES, t=PACK),
@@ -135,16 +135,16 @@ def tile_infoncemi_pa_kernel(
         for head in (LV, MU):
             nc.scalar.dma_start(out=b2_rows[0:1, head, :], in_=b2_in[head].rearrange("(o n) -> o n", o=1))
         nc.scalar.activation(out=warm[:], in_=warm[:], func=ACT.Exp)
-        load_planes(w1_slot[MU], w1_scales_in[MU][0].rearrange("q (c n) -> c q n", c=4))
-        load_w1(MU)
-        nc.sync.dma_start(out=y_sb[:], in_=y_samples.rearrange("(p r) d -> p r d", r=ROW_TILES))
         load_planes(w1_slot[LV], w1_scales_in[LV][0].rearrange("q (c n) -> c q n", c=4))
         load_w1(LV)
-        load_planes(w2_slot[MU], w2_scales_in[MU])
-        load_w2(MU)
-        nc.sync.dma_start(out=x_sb[:, 4:ROW_TILES, :], in_=x_view[:, 4:ROW_TILES, :])
+        load_planes(w1_slot[MU], w1_scales_in[MU][0].rearrange("q (c n) -> c q n", c=4))
+        load_w1(MU)
         load_planes(w2_slot[LV], w2_scales_in[LV])
         load_w2(LV)
+        nc.sync.dma_start(out=x_sb[:, 4:ROW_TILES, :], in_=x_view[:, 4:ROW_TILES, :])
+        nc.sync.dma_start(out=y_sb[:], in_=y_samples.rearrange("(p r) d -> p r d", r=ROW_TILES))
+        load_planes(w2_slot[MU], w2_scales_in[MU])
+        load_w2(MU)
 
         def permute_planes(head):
             nc.vector.tensor_copy(
@@ -166,8 +166,8 @@ def tile_infoncemi_pa_kernel(
         x_grouped_words = x_grouped[:].bitcast(F32).rearrange("p (j u) -> p j u", u=2)
         x_banks = {}
 
-        def transpose_x(pair):
-            bank = psum_tr.tile([P, 2, 2 * P], F32, name="x_bank", tag="tr")
+        def transpose_x(pair, pool, tag):
+            bank = pool.tile([P, 2, 2 * P], F32, name="x_bank", tag=tag)
             for half in range(2):
                 for u in range(2):
                     nc.tensor.transpose(
@@ -246,8 +246,7 @@ def tile_infoncemi_pa_kernel(
 
         def unit_of(step):
             u, g = divmod(step, HID_PASSES)
-            chunk, k = divmod(u, 2)
-            return u, chunk, UNIT_HEADS[k], g
+            return u, UNIT_ORDER[u][0], UNIT_ORDER[u][1], g
 
         def layer1(step):
             u, chunk, head, g = unit_of(step)
@@ -314,6 +313,9 @@ def tile_infoncemi_pa_kernel(
                 )
             acc_of[q] = acc
 
+        last_of = {}
+        for u in range(UNITS):
+            last_of[UNIT_ORDER[u][0]] = u
         logvar_of = {}
         weight_of = {}
         diff_of = {}
@@ -347,55 +349,75 @@ def tile_infoncemi_pa_kernel(
         def second_scalar(q):
             u, chunk, head, j = unit_of(q)
             if head == LV:
-                weight = score.tile([P, CHUNK], F32, name="weight")
-                nc.scalar.activation(out=weight[:], in_=logvar_of[q][:], func=ACT.Exp, scale=-1.0)
-                weight_of[q] = weight
+                if j == 0:
+                    weight_of[chunk] = chunk_pool.tile([P, D_TILES, CHUNK], F32, name="weight")
+                nc.scalar.activation(out=weight_of[chunk][:, j, :], in_=logvar_of[q][:], func=ACT.Exp, scale=-1.0)
             else:
                 nc.scalar.activation(out=squares_of[chunk][:, OWN, j, :], in_=diff_of[q][:], func=ACT.Square)
 
         def weighted_terms(q):
             u, chunk, head, j = unit_of(q)
-            if head == LV:
+            if u == last_of[chunk]:
                 sq = squares_of[chunk]
                 nc.vector.scalar_tensor_tensor(
                     out=sq[:, ALL, j, :], in0=sq[:, ALL, j, :], scalar=y_var[:, j : j + 1],
-                    in1=weight_of[q][:], op0=ALU.add, op1=ALU.mult,
+                    in1=weight_of[chunk][:, j, :], op0=ALU.add, op1=ALU.mult,
                 )
-                nc.vector.tensor_tensor(out=sq[:, OWN, j, :], in0=sq[:, OWN, j, :], in1=weight_of[q][:], op=ALU.mult)
+                nc.vector.tensor_tensor(
+                    out=sq[:, OWN, j, :], in0=sq[:, OWN, j, :], in1=weight_of[chunk][:, j, :], op=ALU.mult
+                )
 
+        late_totals = keep.tile([P, 2, TILES_PER_CHUNK], F32, name="late_totals")
         sum_banks = {}
 
-        def sum_over_d_tensor(chunk):
+        def sum_over_d_tensor(chunk, d_tiles, pool, tag):
             for o in (OWN, ALL):
-                bank = psum_tr.tile([P, TILES_PER_CHUNK, P], F32, name="sum_bank", tag="tr")
+                bank = pool.tile([P, TILES_PER_CHUNK, P], F32, name="sum_bank", tag=tag)
                 for i in range(TILES_PER_CHUNK):
-                    for j in range(D_TILES):
+                    for j in d_tiles:
                         nc.tensor.matmul(
                             out=bank[:, i, :], lhsT=squares_of[chunk][:, o, j, i * P : (i + 1) * P], rhs=ident[:],
-                            is_transpose=True, start=(j == 0), stop=(j == D_TILES - 1),
+                            is_transpose=True, start=(j == d_tiles[0]), stop=(j == d_tiles[-1]),
                         )
                 sum_banks[(chunk, o)] = bank
 
-        def sum_over_d_vector(chunk):
+        def sum_over_d_vector(chunk, out):
             for o in (OWN, ALL):
-                nc.vector.tensor_reduce(
-                    out=totals[:, o, chunk * TILES_PER_CHUNK : (chunk + 1) * TILES_PER_CHUNK],
-                    in_=sum_banks[(chunk, o)][:], axis=AX.X, op=ALU.add,
-                )
+                nc.vector.tensor_reduce(out=out[:, o, :], in_=sum_banks[(chunk, o)][:], axis=AX.X, op=ALU.add)
+
+        Y_STEPS = {6: (0,), 7: (1,), 8: (2,), 9: (3,)}
+        X_STEP = 5
+        W1_STEP = 2
 
         def vector_share(step):
-            return 1
+            scalar_other = 0.0
+            vector_other = 3.0
+            if 0 <= step - LAG_EPI < STEPS:
+                scalar_other += 2.0
+                if unit_of(step - LAG_EPI)[2] == MU:
+                    vector_other += 1.0
+            if 0 <= step - LAG_Z < STEPS and unit_of(step - LAG_Z)[0] == last_of[unit_of(step - LAG_Z)[1]]:
+                vector_other += 2.0
+            if step == X_STEP:
+                scalar_other += 2.0
+                vector_other += 1.0
+            if step in Y_STEPS:
+                scalar_other += 1.0
+            if W1_STEP <= step < W1_STEP + HID_PASSES:
+                vector_other += 0.5
+            return max(0, min(PACK - 1, int((PACK + scalar_other - vector_other) / 2.0 + 0.5)))
 
-        transpose_x(0)
-        transpose_x(1)
+        transpose_x(0, psum_tr, "tr")
+        transpose_x(1, psum_tr, "tr")
         regroup_x(0)
         regroup_x(1)
         nc.vector.tensor_copy(out=b1_col[:], in_=b1_bf[:])
         quantise_x(0)
+        permute_planes(LV)
+        permute_w1(LV, 0)
         quantise_x(1)
-        permute_planes(MU)
-        for g in range(HID_PASSES):
-            permute_w1(MU, g)
+        for g in range(1, HID_PASSES):
+            permute_w1(LV, g)
         b2_bank = psum_tr.tile([P, 2, D_TILES], F32, name="b2_bank", tag="tr")
         for head in (MU, LV):
             for j in range(D_TILES):
@@ -404,19 +426,22 @@ def tile_infoncemi_pa_kernel(
                     rhs=ones_bf[:, 0:1], start=True, stop=True,
                 )
 
-        Y_FROM = 2
-        X_FROM = 4
         for i in range(STEPS + LAG_SUM + 1):
             if i < STEPS:
                 layer1(i)
-            if X_FROM <= i < X_FROM + 2:
-                transpose_x(i - X_FROM + 2)
-            if Y_FROM <= i < Y_FROM + D_TILES:
-                y_tensor(i - Y_FROM)
+            if i == X_STEP:
+                transpose_x(2, psum_tr, "tr")
+                transpose_x(3, psum_tr, "tr")
+            for j in Y_STEPS.get(i, ()):
+                y_tensor(j)
             if 0 <= i - LAG_L2 < STEPS:
                 layer2(i - LAG_L2)
-            if i - LAG_SUM in (2 * HID_PASSES - 1, 4 * HID_PASSES - 1):
-                sum_over_d_tensor((i - LAG_SUM) // (2 * HID_PASSES))
+            if i - LAG_SUM == last_of[0] * HID_PASSES + 3:
+                sum_over_d_tensor(0, (0, 1, 2, 3), psum_tr, "tr")
+            if i - LAG_SUM == last_of[1] * HID_PASSES + 1:
+                sum_over_d_tensor(1, (0, 1), psum_tr, "tr")
+            if i - LAG_SUM == last_of[1] * HID_PASSES + 3:
+                sum_over_d_tensor(1, (2, 3), psum_l1, "l1")
 
             if 0 <= i - 1 < STEPS:
                 interleave(i - 1)
@@ -430,32 +455,42 @@ def tile_infoncemi_pa_kernel(
                     leave_l1(i, t, "scalar")
                 for t in range(PACK - share, PACK):
                     leave_l1(i, t, "vector")
-            if X_FROM <= i < X_FROM + 2:
-                regroup_x(i - X_FROM + 2)
-            if Y_FROM <= i < Y_FROM + D_TILES:
-                y_scalar(i - Y_FROM)
+            if i == X_STEP:
+                regroup_x(2)
+                regroup_x(3)
+            for j in Y_STEPS.get(i, ()):
+                y_scalar(j)
             if 0 <= i - 1 < STEPS:
                 quantise_hidden(i - 1)
             if 0 <= i - LAG_EPI < STEPS:
                 second_scalar(i - LAG_EPI)
             if 0 <= i - LAG_Z < STEPS:
                 weighted_terms(i - LAG_Z)
-            if i - LAG_SUM in (2 * HID_PASSES - 1, 4 * HID_PASSES - 1):
-                sum_over_d_vector((i - LAG_SUM) // (2 * HID_PASSES))
+            if i - LAG_SUM == last_of[0] * HID_PASSES + 3:
+                sum_over_d_vector(0, totals[:, :, 0:TILES_PER_CHUNK])
+            if i - LAG_SUM == last_of[1] * HID_PASSES + 2:
+                sum_over_d_vector(1, totals[:, :, TILES_PER_CHUNK:ROW_TILES])
+            if i - LAG_SUM == last_of[1] * HID_PASSES + 3:
+                sum_over_d_vector(1, late_totals)
             if i == 0:
                 nc.vector.tensor_copy(out=b2_col[:], in_=b2_bank[:])
-            if i == 2:
-                permute_planes(LV)
-            if 2 <= i < 2 + HID_PASSES:
-                permute_w1(LV, i - 2)
-            if X_FROM + 1 <= i < X_FROM + 3:
-                quantise_x(i - X_FROM + 1)
-            if Y_FROM <= i < Y_FROM + D_TILES:
-                y_vector(i - Y_FROM)
-            if i == Y_FROM + D_TILES - 1:
+            if i == X_STEP:
+                quantise_x(2)
+                quantise_x(3)
+            if i == W1_STEP:
+                permute_planes(MU)
+            if W1_STEP <= i < W1_STEP + HID_PASSES:
+                permute_w1(MU, i - W1_STEP)
+            for j in Y_STEPS.get(i, ()):
+                y_vector(j)
+            if i == max(Y_STEPS):
                 y_finish()
 
         result = keep.tile([P, 2, ROW_TILES], F32, name="result")
+        nc.vector.tensor_tensor(
+            out=totals[:, :, TILES_PER_CHUNK:ROW_TILES], in0=totals[:, :, TILES_PER_CHUNK:ROW_TILES],
+            in1=late_totals[:], op=ALU.add,
+        )
         nc.vector.tensor_scalar(out=result[:, OWN, :], in0=totals[:, OWN, :], scalar1=-0.5, scalar2=None, op0=ALU.mult)
         nc.vector.tensor_scalar(
             out=result[:, ALL, :], in0=totals[:, ALL, :], scalar1=-0.5 / N_ROWS, scalar2=None, op0=ALU.mult

@@ -281,7 +281,10 @@ def tile_infoncemi_pa_kernel(
 
         def interleave(step):
             grouped = hidden.tile([P, CHUNK, PACK], BF16, name="grouped", align_bytes=64)
-            nc.vector.tensor_copy(out=grouped[:], in_=stage_of[step][:].rearrange("p t n -> p n t"))
+            nc.vector.tensor_copy(
+                out=grouped[:].rearrange("p (c i) t -> p c t i", i=4),
+                in_=stage_of[step][:].rearrange("p t (c i) -> p c t i", i=4),
+            )
             grouped_of[step] = grouped
 
         def quantise_hidden(step):
@@ -464,10 +467,10 @@ def tile_infoncemi_pa_kernel(
                 quantise_hidden(i - 1)
             if 0 <= i - LAG_EPI < STEPS:
                 second_scalar(i - LAG_EPI)
+            if i == STEPS + 3:
+                sum_over_d_vector(0, totals[:, :, 0:TILES_PER_CHUNK])
             if 0 <= i - LAG_Z < STEPS:
                 weighted_terms(i - LAG_Z)
-            if i - LAG_SUM == last_of[0] * HID_PASSES + 3:
-                sum_over_d_vector(0, totals[:, :, 0:TILES_PER_CHUNK])
             if i - LAG_SUM == last_of[1] * HID_PASSES + 2:
                 sum_over_d_vector(1, totals[:, :, TILES_PER_CHUNK:ROW_TILES])
             if i - LAG_SUM == last_of[1] * HID_PASSES + 3:

@@ -37,6 +37,9 @@ LAG_L2 = 5
 LAG_EPI = 6
 LAG_Z = 7
 LAG_SUM = 8
+LN2 = 0.6931471805599453
+ROOT_INV_N = 1.0 / 32.0
+assert ROOT_INV_N * ROOT_INV_N * N_ROWS == 1.0
 
 
 def tile_infoncemi_pa_kernel(
@@ -232,11 +235,14 @@ def tile_infoncemi_pa_kernel(
 
         def y_finish():
             nc.vector.tensor_scalar(out=y_mean[:], in0=y_sum[:], scalar1=inv_n, scalar2=None, op0=ALU.mult)
-            nc.vector.tensor_tensor(out=mean_sq[:], in0=y_mean[:], in1=y_mean[:], op=ALU.mult)
             nc.vector.scalar_tensor_tensor(
-                out=y_var[:], in0=y_sumsq[:], scalar=inv_n, in1=mean_sq[:], op0=ALU.mult, op1=ALU.subtract
+                out=mean_sq[:], in0=y_mean[:], scalar=inv_n, in1=y_mean[:], op0=ALU.mult, op1=ALU.mult
+            )
+            nc.vector.scalar_tensor_tensor(
+                out=y_var[:], in0=y_sumsq[:], scalar=inv_n * inv_n, in1=mean_sq[:], op0=ALU.mult, op1=ALU.subtract
             )
             nc.vector.tensor_tensor(out=centre[:], in0=b2_col[:, MU, :], in1=y_mean[:], op=ALU.subtract)
+            nc.vector.tensor_scalar(out=centre[:], in0=centre[:], scalar1=ROOT_INV_N, scalar2=None, op0=ALU.mult)
 
         l1_banks = {}
         stage_of = {}
@@ -336,7 +342,8 @@ def tile_infoncemi_pa_kernel(
                 if j == 0:
                     squares_of[chunk] = chunk_pool.tile([P, 2, D_TILES, CHUNK], F32, name="squares")
                 nc.scalar.activation(
-                    out=squares_of[chunk][:, ALL, j, :], in_=acc_of[q][:], func=ACT.Square, bias=centre[:, j : j + 1]
+                    out=squares_of[chunk][:, ALL, j, :], in_=acc_of[q][:], func=ACT.Square, scale=ROOT_INV_N,
+                    bias=centre[:, j : j + 1],
                 )
 
         def first_vector(q):
@@ -354,7 +361,9 @@ def tile_infoncemi_pa_kernel(
             if head == LV:
                 if j == 0:
                     weight_of[chunk] = chunk_pool.tile([P, D_TILES, CHUNK], F32, name="weight")
-                nc.scalar.activation(out=weight_of[chunk][:, j, :], in_=logvar_of[q][:], func=ACT.Exp, scale=-1.0)
+                nc.scalar.activation(
+                    out=weight_of[chunk][:, j, :], in_=logvar_of[q][:], func=ACT.Exp, scale=-1.0, bias=-LN2
+                )
             else:
                 nc.scalar.activation(out=squares_of[chunk][:, OWN, j, :], in_=diff_of[q][:], func=ACT.Square)
 
@@ -371,10 +380,11 @@ def tile_infoncemi_pa_kernel(
                 )
 
         late_totals = keep.tile([P, 2, TILES_PER_CHUNK], F32, name="late_totals")
+        result = keep.tile([P, 2, ROW_TILES], F32, name="result")
         sum_banks = {}
 
         def sum_over_d_tensor(chunk, d_tiles, pool, tag):
-            for o in (OWN, ALL):
+            for o in (ALL, OWN):
                 bank = pool.tile([P, TILES_PER_CHUNK, P], F32, name="sum_bank", tag=tag)
                 for i in range(TILES_PER_CHUNK):
                     for j in d_tiles:
@@ -385,7 +395,7 @@ def tile_infoncemi_pa_kernel(
                 sum_banks[(chunk, o)] = bank
 
         def sum_over_d_vector(chunk, out):
-            for o in (OWN, ALL):
+            for o in (ALL, OWN):
                 nc.vector.tensor_reduce(out=out[:, o, :], in_=sum_banks[(chunk, o)][:], axis=AX.X, op=ALU.add)
 
         Y_STEPS = {6: (0,), 7: (1,), 8: (2,), 9: (3,)}
@@ -463,18 +473,6 @@ def tile_infoncemi_pa_kernel(
                 regroup_x(3)
             for j in Y_STEPS.get(i, ()):
                 y_scalar(j)
-            if 0 <= i - 1 < STEPS:
-                quantise_hidden(i - 1)
-            if 0 <= i - LAG_EPI < STEPS:
-                second_scalar(i - LAG_EPI)
-            if i == STEPS + 3:
-                sum_over_d_vector(0, totals[:, :, 0:TILES_PER_CHUNK])
-            if 0 <= i - LAG_Z < STEPS:
-                weighted_terms(i - LAG_Z)
-            if i - LAG_SUM == last_of[1] * HID_PASSES + 2:
-                sum_over_d_vector(1, totals[:, :, TILES_PER_CHUNK:ROW_TILES])
-            if i - LAG_SUM == last_of[1] * HID_PASSES + 3:
-                sum_over_d_vector(1, late_totals)
             if i == 0:
                 nc.vector.tensor_copy(out=b2_col[:], in_=b2_bank[:])
             if i == X_STEP:
@@ -488,15 +486,26 @@ def tile_infoncemi_pa_kernel(
                 y_vector(j)
             if i == max(Y_STEPS):
                 y_finish()
+            if 0 <= i - 1 < STEPS:
+                quantise_hidden(i - 1)
+            if 0 <= i - LAG_EPI < STEPS:
+                second_scalar(i - LAG_EPI)
+            if i == STEPS + 3:
+                sum_over_d_vector(0, totals[:, :, 0:TILES_PER_CHUNK])
+                nc.vector.tensor_scalar(
+                    out=result[:, :, 0:TILES_PER_CHUNK], in0=totals[:, :, 0:TILES_PER_CHUNK], scalar1=-1.0, scalar2=None,
+                    op0=ALU.mult,
+                )
+            if 0 <= i - LAG_Z < STEPS:
+                weighted_terms(i - LAG_Z)
+            if i - LAG_SUM == last_of[1] * HID_PASSES + 2:
+                sum_over_d_vector(1, totals[:, :, TILES_PER_CHUNK:ROW_TILES])
+            if i - LAG_SUM == last_of[1] * HID_PASSES + 3:
+                sum_over_d_vector(1, late_totals)
 
-        result = keep.tile([P, 2, ROW_TILES], F32, name="result")
-        nc.vector.tensor_tensor(
-            out=totals[:, :, TILES_PER_CHUNK:ROW_TILES], in0=totals[:, :, TILES_PER_CHUNK:ROW_TILES],
-            in1=late_totals[:], op=ALU.add,
-        )
-        nc.vector.tensor_scalar(out=result[:, OWN, :], in0=totals[:, OWN, :], scalar1=-0.5, scalar2=None, op0=ALU.mult)
-        nc.vector.tensor_scalar(
-            out=result[:, ALL, :], in0=totals[:, ALL, :], scalar1=-0.5 / N_ROWS, scalar2=None, op0=ALU.mult
+        nc.vector.scalar_tensor_tensor(
+            out=result[:, :, TILES_PER_CHUNK:ROW_TILES], in0=totals[:, :, TILES_PER_CHUNK:ROW_TILES], scalar=-1.0,
+            in1=late_totals[:], op0=ALU.mult, op1=ALU.subtract,
         )
         nc.sync.dma_start(out=out_0.rearrange("(p r) -> p r", r=ROW_TILES), in_=result[:, OWN, :])
         nc.scalar.dma_start(out=out_1.rearrange("(p r) -> p r", r=ROW_TILES), in_=result[:, ALL, :])

@@ -113,13 +113,12 @@ def tile_infoncemi_pa_kernel(
                     in_=four_planes[:, 4 * quad : 4 * quad + 4, :].bitcast(I32),
                 )
 
-        def load_w1(head):
+        def load_w1(head, c):
             flat = w1_words_in[head][0].rearrange("p n t -> p (n t)")
-            for c in range(HID_PASSES):
-                nc.sync.dma_start(
-                    out=w1[:, head, c * K_PASS : (c + 1) * K_PASS].bitcast(I32),
-                    in_=flat[:, c * 4 * K_PASS : (c + 1) * 4 * K_PASS].bitcast(I32),
-                )
+            nc.sync.dma_start(
+                out=w1[:, head, c * K_PASS : (c + 1) * K_PASS].bitcast(I32),
+                in_=flat[:, c * 4 * K_PASS : (c + 1) * 4 * K_PASS].bitcast(I32),
+            )
 
         def load_w2(head):
             nc.sync.dma_start(
@@ -127,21 +126,30 @@ def tile_infoncemi_pa_kernel(
                 in_=w2_words_in[head].rearrange("g p n t -> p g (n t)").bitcast(I32),
             )
 
-        x_view = x_samples.rearrange("(p r) k -> p r k", r=ROW_TILES)
-        nc.sync.dma_start(out=x_sb[:, 0:2, :], in_=x_view[:, 0:2, :])
-        nc.sync.dma_start(out=x_sb[:, 2:4, :], in_=x_view[:, 2:4, :])
-        for head in (LV, MU):
-            nc.scalar.dma_start(
+        def load_b1(queue, head):
+            queue.dma_start(
                 out=b1_bf[:, head, :].rearrange("p (g t) -> p g t", t=PACK),
                 in_=b1_in[head].rearrange("(g p t) -> p g t", g=HID_PASSES, t=PACK),
             )
-        for head in (LV, MU):
-            nc.scalar.dma_start(out=b2_rows[0:1, head, :], in_=b2_in[head].rearrange("(o n) -> o n", o=1))
-        nc.scalar.activation(out=warm[:], in_=warm[:], func=ACT.Exp)
+
+        def load_b2(queue, head):
+            queue.dma_start(out=b2_rows[0:1, head, :], in_=b2_in[head].rearrange("(o n) -> o n", o=1))
+
+        x_view = x_samples.rearrange("(p r) k -> p r k", r=ROW_TILES)
+        nc.sync.dma_start(out=x_sb[:, 0:2, :], in_=x_view[:, 0:2, :])
+        nc.sync.dma_start(out=x_sb[:, 2:4, :], in_=x_view[:, 2:4, :])
         load_planes(w1_slot[LV], w1_scales_in[LV][0].rearrange("q (c n) -> c q n", c=4))
-        load_w1(LV)
+        load_w1(LV, 0)
+        load_b1(nc.scalar, LV)
+        nc.scalar.activation(out=warm[:], in_=warm[:], func=ACT.Exp)
+        for c in range(1, HID_PASSES):
+            load_w1(LV, c)
+        load_b1(nc.sync, MU)
+        load_b2(nc.sync, LV)
+        load_b2(nc.sync, MU)
         load_planes(w1_slot[MU], w1_scales_in[MU][0].rearrange("q (c n) -> c q n", c=4))
-        load_w1(MU)
+        for c in range(HID_PASSES):
+            load_w1(MU, c)
         load_planes(w2_slot[LV], w2_scales_in[LV])
         load_w2(LV)
         nc.sync.dma_start(out=x_sb[:, 4:ROW_TILES, :], in_=x_view[:, 4:ROW_TILES, :])
@@ -197,7 +205,7 @@ def tile_infoncemi_pa_kernel(
         y_t = keep.tile([P, D_TILES, N_ROWS], BF16, name="y_t")
         y_sum = keep.tile([P, D_TILES], F32, name="y_sum")
         y_sumsq = keep.tile([P, D_TILES], F32, name="y_sumsq")
-        y_mean = keep.tile([P, D_TILES], F32, name="y_mean")
+        b2_scaled = keep.tile([P, D_TILES], F32, name="b2_scaled")
         mean_sq = keep.tile([P, D_TILES], F32, name="mean_sq")
         y_var = keep.tile([P, D_TILES], F32, name="y_var")
         centre = keep.tile([P, D_TILES], F32, name="centre")
@@ -227,22 +235,22 @@ def tile_infoncemi_pa_kernel(
 
         def y_vector(j):
             stats = y_banks[j][1]
+            nc.vector.tensor_copy(out=y_sum[:, j : j + 1], in_=stats[:, P : P + 1])
             nc.vector.scalar_tensor_tensor(
                 out=diag_junk[:], in0=stats[:, 0:P], scalar=1.0, in1=ident[:],
                 op0=ALU.mult, op1=ALU.mult, accum_out=y_sumsq[:, j : j + 1],
             )
-            nc.vector.tensor_copy(out=y_sum[:, j : j + 1], in_=stats[:, P : P + 1])
 
         def y_finish():
-            nc.vector.tensor_scalar(out=y_mean[:], in0=y_sum[:], scalar1=inv_n, scalar2=None, op0=ALU.mult)
             nc.vector.scalar_tensor_tensor(
-                out=mean_sq[:], in0=y_mean[:], scalar=inv_n, in1=y_mean[:], op0=ALU.mult, op1=ALU.mult
+                out=mean_sq[:], in0=y_sum[:], scalar=inv_n * inv_n * inv_n, in1=y_sum[:], op0=ALU.mult, op1=ALU.mult
+            )
+            nc.vector.scalar_tensor_tensor(
+                out=centre[:], in0=y_sum[:], scalar=-inv_n * ROOT_INV_N, in1=b2_scaled[:], op0=ALU.mult, op1=ALU.add
             )
             nc.vector.scalar_tensor_tensor(
                 out=y_var[:], in0=y_sumsq[:], scalar=inv_n * inv_n, in1=mean_sq[:], op0=ALU.mult, op1=ALU.subtract
             )
-            nc.vector.tensor_tensor(out=centre[:], in0=b2_col[:, MU, :], in1=y_mean[:], op=ALU.subtract)
-            nc.vector.tensor_scalar(out=centre[:], in0=centre[:], scalar1=ROOT_INV_N, scalar2=None, op0=ALU.mult)
 
         l1_banks = {}
         stage_of = {}
@@ -401,6 +409,7 @@ def tile_infoncemi_pa_kernel(
         Y_STEPS = {6: (0,), 7: (1,), 8: (2,), 9: (3,)}
         X_STEP = 5
         W1_STEP = 2
+        B_STEP = 1
 
         def vector_share(step):
             scalar_other = 0.0
@@ -424,24 +433,31 @@ def tile_infoncemi_pa_kernel(
         transpose_x(1, psum_tr, "tr")
         regroup_x(0)
         regroup_x(1)
-        nc.vector.tensor_copy(out=b1_col[:], in_=b1_bf[:])
+        nc.vector.tensor_copy(out=b1_col[:, LV, :], in_=b1_bf[:, LV, :])
         quantise_x(0)
         permute_planes(LV)
         permute_w1(LV, 0)
         quantise_x(1)
         for g in range(1, HID_PASSES):
             permute_w1(LV, g)
-        b2_bank = psum_tr.tile([P, 2, D_TILES], F32, name="b2_bank", tag="tr")
-        for head in (MU, LV):
-            for j in range(D_TILES):
-                nc.tensor.matmul(
-                    out=b2_bank[:, head, j : j + 1], lhsT=b2_rows[:, head, j * P : (j + 1) * P],
-                    rhs=ones_bf[:, 0:1], start=True, stop=True,
-                )
+
+        b2_banks = {}
+
+        def b2_tensor():
+            bank = psum_tr.tile([P, 2, D_TILES], F32, name="b2_bank", tag="tr")
+            for head in (MU, LV):
+                for j in range(D_TILES):
+                    nc.tensor.matmul(
+                        out=bank[:, head, j : j + 1], lhsT=b2_rows[:, head, j * P : (j + 1) * P],
+                        rhs=ones_bf[:, 0:1], start=True, stop=True,
+                    )
+            b2_banks[0] = bank
 
         for i in range(STEPS + LAG_SUM + 1):
             if i < STEPS:
                 layer1(i)
+            if i == B_STEP:
+                b2_tensor()
             if i == X_STEP:
                 transpose_x(2, psum_tr, "tr")
                 transpose_x(3, psum_tr, "tr")
@@ -473,8 +489,12 @@ def tile_infoncemi_pa_kernel(
                 regroup_x(3)
             for j in Y_STEPS.get(i, ()):
                 y_scalar(j)
-            if i == 0:
-                nc.vector.tensor_copy(out=b2_col[:], in_=b2_bank[:])
+            if i == B_STEP:
+                nc.vector.tensor_copy(out=b2_col[:], in_=b2_banks[0][:])
+                nc.vector.tensor_scalar(
+                    out=b2_scaled[:], in0=b2_banks[0][:, MU, :], scalar1=ROOT_INV_N, scalar2=None, op0=ALU.mult
+                )
+                nc.vector.tensor_copy(out=b1_col[:, MU, :], in_=b1_bf[:, MU, :])
             if i == X_STEP:
                 quantise_x(2)
                 quantise_x(3)
@@ -503,9 +523,10 @@ def tile_infoncemi_pa_kernel(
             if i - LAG_SUM == last_of[1] * HID_PASSES + 3:
                 sum_over_d_vector(1, late_totals)
 
-        nc.vector.scalar_tensor_tensor(
-            out=result[:, :, TILES_PER_CHUNK:ROW_TILES], in0=totals[:, :, TILES_PER_CHUNK:ROW_TILES], scalar=-1.0,
-            in1=late_totals[:], op0=ALU.mult, op1=ALU.subtract,
-        )
-        nc.sync.dma_start(out=out_0.rearrange("(p r) -> p r", r=ROW_TILES), in_=result[:, OWN, :])
+        for o in (ALL, OWN):
+            nc.vector.scalar_tensor_tensor(
+                out=result[:, o, TILES_PER_CHUNK:ROW_TILES], in0=totals[:, o, TILES_PER_CHUNK:ROW_TILES], scalar=-1.0,
+                in1=late_totals[:, o, :], op0=ALU.mult, op1=ALU.subtract,
+            )
         nc.scalar.dma_start(out=out_1.rearrange("(p r) -> p r", r=ROW_TILES), in_=result[:, ALL, :])
+        nc.sync.dma_start(out=out_0.rearrange("(p r) -> p r", r=ROW_TILES), in_=result[:, OWN, :])

@@ -26,20 +26,28 @@ PACK = 4
 HID_PASSES = HID // K_PASS
 D_TILES = Y_DIM // P
 CHUNK = 512
-CHUNKS = N_ROWS // CHUNK
 TILES_PER_CHUNK = CHUNK // P
 MU, LV = 0, 1
+OWN, ALL = 0, 1
+
 UNIT_ORDER = ((0, LV), (0, MU), (1, MU), (1, LV))
 UNITS = len(UNIT_ORDER)
 STEPS = UNITS * HID_PASSES
 
-LAG_L2 = 5
-LAG_EPI = 6
-LAG_Z = 7
+LAG_LAYER2 = 5
+LAG_SCORE = 6
+LAG_WEIGHTED = 7
 LAG_SUM = 8
+
+Y_STEPS = (6, 7, 8, 9)
+X_STEP = 5
+W1_STEP = 2
+BIAS_STEP = 1
+
 LN2 = 0.6931471805599453
+INV_N = 1.0 / N_ROWS
 ROOT_INV_N = 1.0 / 32.0
-assert ROOT_INV_N * ROOT_INV_N * N_ROWS == 1.0
+assert ROOT_INV_N * ROOT_INV_N == INV_N
 
 
 def tile_infoncemi_pa_kernel(
@@ -74,18 +82,18 @@ def tile_infoncemi_pa_kernel(
         keep = ctx.enter_context(tc.tile_pool(name="keep", bufs=1))
         hidden = ctx.enter_context(tc.tile_pool(name="hidden", bufs=3))
         score = ctx.enter_context(tc.tile_pool(name="score", bufs=3))
-        chunk_pool = ctx.enter_context(tc.tile_pool(name="chunk_pool", bufs=2))
+        by_chunk = ctx.enter_context(tc.tile_pool(name="by_chunk", bufs=2))
         psum_l1 = ctx.enter_context(tc.psum_pool(name="psum_l1", bufs=4))
         psum_l2 = ctx.enter_context(tc.psum_pool(name="psum_l2", bufs=2))
-        psum_tr = ctx.enter_context(tc.psum_pool(name="psum_tr", bufs=2))
+        psum_misc = ctx.enter_context(tc.psum_pool(name="psum_misc", bufs=2))
 
         x_sb = keep.tile([P, ROW_TILES, X_DIM], BF16, name="x_sb")
         y_sb = keep.tile([P, ROW_TILES, Y_DIM], BF16, name="y_sb")
         w1 = keep.tile([P, 2, HID], U32, name="w1", align_bytes=64)
-        w1_perm = keep.tile([P, 2, HID], U32, name="w1_perm", align_bytes=64)
+        w1_regrouped = keep.tile([P, 2, HID], U32, name="w1_regrouped", align_bytes=64)
         w2 = keep.tile([P, 2, HID_PASSES, Y_DIM], U32, name="w2", align_bytes=64)
         planes = keep.tile([P, 4, 512], U8, name="planes", align_bytes=64)
-        planes_perm = keep.tile([P, 2, 512], U8, name="planes_perm", align_bytes=64)
+        planes_regrouped = keep.tile([P, 2, 512], U8, name="planes_regrouped", align_bytes=64)
         w1_slot = {MU: 0, LV: 1}
         w2_slot = {MU: 2, LV: 3}
         b1_bf = keep.tile([P, 2, HID_PASSES * PACK], BF16, name="b1_bf")
@@ -93,15 +101,13 @@ def tile_infoncemi_pa_kernel(
         b2_rows = keep.tile([P, 2, Y_DIM], BF16, name="b2_rows")
         b2_col = keep.tile([P, 2, D_TILES], F32, name="b2_col")
         ones_bf = keep.tile([P, 2], BF16, name="ones_bf")
-        ones_f32 = keep.tile([P, 2], F32, name="ones_f32")
         ident = keep.tile([P, P], F32, name="ident")
         ident_bf = keep.tile([P, P], BF16, name="ident_bf")
-        warm = keep.tile([P, 1], F32, name="warm")
+        table_seed = keep.tile([P, 1], F32, name="table_seed")
 
-        nc.vector.memset(warm[:], 0.0)
+        nc.vector.memset(table_seed[:], 0.0)
         nc.vector.memset(planes[:].bitcast(I32), 0)
         nc.vector.memset(ones_bf[:], 1.0)
-        nc.vector.memset(ones_f32[:], 1.0)
         nc.vector.memset(b2_rows[:].bitcast(I32), 0)
         make_identity(nc, ident[:])
         make_identity(nc, ident_bf[:])
@@ -113,11 +119,14 @@ def tile_infoncemi_pa_kernel(
                     in_=four_planes[:, 4 * quad : 4 * quad + 4, :].bitcast(I32),
                 )
 
-        def load_w1(head, c):
+        def load_w1_planes(head):
+            load_planes(w1_slot[head], w1_scales_in[head][0].rearrange("q (c n) -> c q n", c=4))
+
+        def load_w1(head, g):
             flat = w1_words_in[head][0].rearrange("p n t -> p (n t)")
             nc.sync.dma_start(
-                out=w1[:, head, c * K_PASS : (c + 1) * K_PASS].bitcast(I32),
-                in_=flat[:, c * 4 * K_PASS : (c + 1) * 4 * K_PASS].bitcast(I32),
+                out=w1[:, head, g * K_PASS : (g + 1) * K_PASS].bitcast(I32),
+                in_=flat[:, g * 4 * K_PASS : (g + 1) * 4 * K_PASS].bitcast(I32),
             )
 
         def load_w2(head):
@@ -135,50 +144,52 @@ def tile_infoncemi_pa_kernel(
         def load_b2(queue, head):
             queue.dma_start(out=b2_rows[0:1, head, :], in_=b2_in[head].rearrange("(o n) -> o n", o=1))
 
+        first_head = UNIT_ORDER[0][1]
+        second_head = UNIT_ORDER[1][1]
         x_view = x_samples.rearrange("(p r) k -> p r k", r=ROW_TILES)
         nc.sync.dma_start(out=x_sb[:, 0:2, :], in_=x_view[:, 0:2, :])
         nc.sync.dma_start(out=x_sb[:, 2:4, :], in_=x_view[:, 2:4, :])
-        load_planes(w1_slot[LV], w1_scales_in[LV][0].rearrange("q (c n) -> c q n", c=4))
-        load_w1(LV, 0)
-        load_b1(nc.scalar, LV)
-        nc.scalar.activation(out=warm[:], in_=warm[:], func=ACT.Exp)
-        for c in range(1, HID_PASSES):
-            load_w1(LV, c)
-        load_b1(nc.sync, MU)
-        load_b2(nc.sync, LV)
-        load_b2(nc.sync, MU)
-        load_planes(w1_slot[MU], w1_scales_in[MU][0].rearrange("q (c n) -> c q n", c=4))
-        for c in range(HID_PASSES):
-            load_w1(MU, c)
-        load_planes(w2_slot[LV], w2_scales_in[LV])
-        load_w2(LV)
+        load_w1_planes(first_head)
+        load_w1(first_head, 0)
+        load_b1(nc.scalar, first_head)
+        nc.scalar.activation(out=table_seed[:], in_=table_seed[:], func=ACT.Exp)
+        for g in range(1, HID_PASSES):
+            load_w1(first_head, g)
+        load_b1(nc.sync, second_head)
+        load_b2(nc.sync, first_head)
+        load_b2(nc.sync, second_head)
+        load_w1_planes(second_head)
+        for g in range(HID_PASSES):
+            load_w1(second_head, g)
+        load_planes(w2_slot[first_head], w2_scales_in[first_head])
+        load_w2(first_head)
         nc.sync.dma_start(out=x_sb[:, 4:ROW_TILES, :], in_=x_view[:, 4:ROW_TILES, :])
         nc.sync.dma_start(out=y_sb[:], in_=y_samples.rearrange("(p r) d -> p r d", r=ROW_TILES))
-        load_planes(w2_slot[MU], w2_scales_in[MU])
-        load_w2(MU)
+        load_planes(w2_slot[second_head], w2_scales_in[second_head])
+        load_w2(second_head)
 
-        def permute_planes(head):
+        def regroup_planes(head):
             nc.vector.tensor_copy(
-                out=planes_perm[:, head, :].rearrange("p (t m) -> p t m", t=PACK),
+                out=planes_regrouped[:, head, :].rearrange("p (t m) -> p t m", t=PACK),
                 in_=planes[:, w1_slot[head], :].rearrange("p (m t) -> p t m", t=PACK),
             )
 
-        def permute_w1(head, g):
+        def regroup_w1(head, g):
             cols = slice(g * K_PASS, (g + 1) * K_PASS)
             nc.vector.tensor_copy(
-                out=w1_perm[:, head, cols].bitcast(I32).rearrange("p (t m) -> p t m", t=PACK),
+                out=w1_regrouped[:, head, cols].bitcast(I32).rearrange("p (t m) -> p t m", t=PACK),
                 in_=w1[:, head, cols].bitcast(I32).rearrange("p (m t) -> p t m", t=PACK),
             )
 
         x_grouped = keep.tile([P, ROW_TILES * K_PASS], BF16, name="x_grouped", align_bytes=64)
-        x_codes = keep.tile([P, ROW_TILES * P], U32, name="x_codes", align_bytes=64)
-        x_scales = keep.tile([P, ROW_TILES * P], U8, name="x_scales", align_bytes=64)
+        x_codes = keep.tile([P, N_ROWS], U32, name="x_codes", align_bytes=64)
+        x_scales = keep.tile([P, N_ROWS], U8, name="x_scales", align_bytes=64)
         x_words = x_sb[:].bitcast(F32)
-        x_grouped_words = x_grouped[:].bitcast(F32).rearrange("p (j u) -> p j u", u=2)
+        x_grouped_words = x_grouped[:].bitcast(F32).rearrange("p (n u) -> p n u", u=2)
         x_banks = {}
 
-        def transpose_x(pair, pool, tag):
-            bank = pool.tile([P, 2, 2 * P], F32, name="x_bank", tag=tag)
+        def transpose_x(pair):
+            bank = psum_misc.tile([P, 2, 2 * P], F32, name="x_bank", tag="misc")
             for half in range(2):
                 for u in range(2):
                     nc.tensor.transpose(
@@ -191,7 +202,7 @@ def tile_infoncemi_pa_kernel(
         def regroup_x(pair):
             nc.scalar.copy(
                 out=x_grouped_words[:, pair * 2 * P : (pair + 1) * 2 * P, :],
-                in_=x_banks[pair][:].rearrange("p u j -> p j u"),
+                in_=x_banks[pair][:].rearrange("p u n -> p n u"),
             )
 
         def quantise_x(pair):
@@ -201,23 +212,41 @@ def tile_infoncemi_pa_kernel(
                 in_=x_grouped[:, pair * 2 * K_PASS : (pair + 1) * 2 * K_PASS],
             )
 
-        inv_n = 1.0 / N_ROWS
+        b2_scaled = keep.tile([P, D_TILES], F32, name="b2_scaled")
+        b2_banks = {}
+
+        def b2_tensor():
+            bank = psum_misc.tile([P, 2, D_TILES], F32, name="b2_bank", tag="misc")
+            for head in (MU, LV):
+                for j in range(D_TILES):
+                    nc.tensor.matmul(
+                        out=bank[:, head, j : j + 1], lhsT=b2_rows[:, head, j * P : (j + 1) * P],
+                        rhs=ones_bf[:, 0:1], start=True, stop=True,
+                    )
+            b2_banks[0] = bank
+
+        def later_biases_vector():
+            nc.vector.tensor_copy(out=b2_col[:], in_=b2_banks[0][:])
+            nc.vector.tensor_scalar(
+                out=b2_scaled[:], in0=b2_banks[0][:, MU, :], scalar1=ROOT_INV_N, scalar2=None, op0=ALU.mult
+            )
+            nc.vector.tensor_copy(out=b1_col[:, second_head, :], in_=b1_bf[:, second_head, :])
+
         y_t = keep.tile([P, D_TILES, N_ROWS], BF16, name="y_t")
         y_sum = keep.tile([P, D_TILES], F32, name="y_sum")
         y_sumsq = keep.tile([P, D_TILES], F32, name="y_sumsq")
-        b2_scaled = keep.tile([P, D_TILES], F32, name="b2_scaled")
         mean_sq = keep.tile([P, D_TILES], F32, name="mean_sq")
         y_var = keep.tile([P, D_TILES], F32, name="y_var")
         centre = keep.tile([P, D_TILES], F32, name="centre")
-        diag_junk = keep.tile([P, P], F32, name="diag_junk")
+        diagonal = keep.tile([P, P], F32, name="diagonal")
         y_banks = {}
 
         def y_tensor(j):
             cols = slice(j * P, (j + 1) * P)
-            turned = psum_tr.tile([P, ROW_TILES, P], BF16, name="y_turned", tag="tr")
+            turned = psum_misc.tile([P, ROW_TILES, P], BF16, name="y_turned", tag="misc")
             for r in range(ROW_TILES):
                 nc.tensor.transpose(turned[:, r, :], y_sb[:, r, cols], ident_bf[:])
-            stats = psum_tr.tile([P, P + 2], F32, name="y_stats", tag="tr")
+            stats = psum_misc.tile([P, P + 2], F32, name="y_stats", tag="misc")
             for r in range(ROW_TILES):
                 nc.tensor.matmul(
                     out=stats[:, 0:P], lhsT=y_sb[:, r, cols], rhs=y_sb[:, r, cols],
@@ -237,30 +266,29 @@ def tile_infoncemi_pa_kernel(
             stats = y_banks[j][1]
             nc.vector.tensor_copy(out=y_sum[:, j : j + 1], in_=stats[:, P : P + 1])
             nc.vector.scalar_tensor_tensor(
-                out=diag_junk[:], in0=stats[:, 0:P], scalar=1.0, in1=ident[:],
+                out=diagonal[:], in0=stats[:, 0:P], scalar=1.0, in1=ident[:],
                 op0=ALU.mult, op1=ALU.mult, accum_out=y_sumsq[:, j : j + 1],
             )
 
-        def y_finish():
+        def y_constants():
             nc.vector.scalar_tensor_tensor(
-                out=mean_sq[:], in0=y_sum[:], scalar=inv_n * inv_n * inv_n, in1=y_sum[:], op0=ALU.mult, op1=ALU.mult
+                out=mean_sq[:], in0=y_sum[:], scalar=INV_N * INV_N * INV_N, in1=y_sum[:], op0=ALU.mult, op1=ALU.mult
             )
             nc.vector.scalar_tensor_tensor(
-                out=centre[:], in0=y_sum[:], scalar=-inv_n * ROOT_INV_N, in1=b2_scaled[:], op0=ALU.mult, op1=ALU.add
+                out=centre[:], in0=y_sum[:], scalar=-INV_N * ROOT_INV_N, in1=b2_scaled[:], op0=ALU.mult, op1=ALU.add
             )
             nc.vector.scalar_tensor_tensor(
-                out=y_var[:], in0=y_sumsq[:], scalar=inv_n * inv_n, in1=mean_sq[:], op0=ALU.mult, op1=ALU.subtract
+                out=y_var[:], in0=y_sumsq[:], scalar=INV_N * INV_N, in1=mean_sq[:], op0=ALU.mult, op1=ALU.subtract
             )
 
         l1_banks = {}
-        stage_of = {}
+        parts_of = {}
         grouped_of = {}
         codes_of = {}
-        acc_of = {}
 
-        def unit_of(step):
-            u, g = divmod(step, HID_PASSES)
-            return u, UNIT_ORDER[u][0], UNIT_ORDER[u][1], g
+        def unit_of(number):
+            u, rest = divmod(number, HID_PASSES)
+            return u, UNIT_ORDER[u][0], UNIT_ORDER[u][1], rest
 
         def layer1(step):
             u, chunk, head, g = unit_of(step)
@@ -270,8 +298,8 @@ def tile_infoncemi_pa_kernel(
                 cols = slice(g * K_PASS + t * P, g * K_PASS + (t + 1) * P)
                 nc.tensor.matmul_mx(
                     out=bank[:],
-                    lhsT=w1_perm[:, head, cols].bitcast(FP8X4),
-                    lhsT_scale=planes_perm[4 * g : P, head, t * P : (t + 1) * P],
+                    lhsT=w1_regrouped[:, head, cols].bitcast(FP8X4),
+                    lhsT_scale=planes_regrouped[4 * g : P, head, t * P : (t + 1) * P],
                     rhs=x_codes[:, chunk * CHUNK : (chunk + 1) * CHUNK].bitcast(FP8X4),
                     rhs_scale=x_scales[:, chunk * CHUNK : (chunk + 1) * CHUNK],
                     start=True,
@@ -279,25 +307,25 @@ def tile_infoncemi_pa_kernel(
                 )
                 l1_banks[step].append(bank)
 
-        def new_stage(step):
-            stage_of[step] = hidden.tile([P, PACK, CHUNK], BF16, name="stage")
-
-        def leave_l1(step, t, engine):
+        def leave_layer1(step, vector_banks):
             u, chunk, head, g = unit_of(step)
-            bias = b1_col[:, head, g * PACK + t : g * PACK + t + 1]
-            if engine == "scalar":
-                nc.scalar.activation(out=stage_of[step][:, t, :], in_=l1_banks[step][t][:], func=ACT.Relu, bias=bias)
-            else:
-                nc.vector.tensor_scalar(
-                    out=stage_of[step][:, t, :], in0=l1_banks[step][t][:], scalar1=bias, scalar2=0.0,
-                    op0=ALU.add, op1=ALU.max,
-                )
+            parts = hidden.tile([P, PACK, CHUNK], BF16, name="parts")
+            for t in range(PACK):
+                bias = b1_col[:, head, g * PACK + t : g * PACK + t + 1]
+                if t < PACK - vector_banks:
+                    nc.scalar.activation(out=parts[:, t, :], in_=l1_banks[step][t][:], func=ACT.Relu, bias=bias)
+                else:
+                    nc.vector.tensor_scalar(
+                        out=parts[:, t, :], in0=l1_banks[step][t][:], scalar1=bias, scalar2=0.0,
+                        op0=ALU.add, op1=ALU.max,
+                    )
+            parts_of[step] = parts
 
         def interleave(step):
             grouped = hidden.tile([P, CHUNK, PACK], BF16, name="grouped", align_bytes=64)
             nc.vector.tensor_copy(
                 out=grouped[:].rearrange("p (c i) t -> p c t i", i=4),
-                in_=stage_of[step][:].rearrange("p t (c i) -> p c t i", i=4),
+                in_=parts_of[step][:].rearrange("p t (c i) -> p c t i", i=4),
             )
             grouped_of[step] = grouped
 
@@ -314,13 +342,22 @@ def tile_infoncemi_pa_kernel(
                 in_=grouped_of[step][:].rearrange("p n t -> p (n t)"),
             )
 
-        def layer2(q):
-            u, chunk, head, j = unit_of(q)
+        l2_banks = {}
+        logvar_of = {}
+        diff_of = {}
+        weight_of = {}
+        terms_of = {}
+        second_unit_of = {}
+        for u in range(UNITS):
+            second_unit_of[UNIT_ORDER[u][0]] = u
+
+        def layer2(bank_no):
+            u, chunk, head, j = unit_of(bank_no)
             codes, scales = codes_of[u]
-            acc = psum_l2.tile([P, CHUNK], F32, name="l2_bank", tag="l2")
+            bank = psum_l2.tile([P, CHUNK], F32, name="l2_bank", tag="l2")
             for g in range(HID_PASSES):
                 nc.tensor.matmul_mx(
-                    out=acc[:],
+                    out=bank[:],
                     lhsT=w2[:, head, g, j * P : (j + 1) * P].bitcast(FP8X4),
                     lhsT_scale=planes[4 * g : P, w2_slot[head], j * P : (j + 1) * P],
                     rhs=codes[:, g, :].bitcast(FP8X4),
@@ -328,65 +365,56 @@ def tile_infoncemi_pa_kernel(
                     start=(g == 0),
                     stop=(g == HID_PASSES - 1),
                 )
-            acc_of[q] = acc
+            l2_banks[bank_no] = bank
 
-        last_of = {}
-        for u in range(UNITS):
-            last_of[UNIT_ORDER[u][0]] = u
-        logvar_of = {}
-        weight_of = {}
-        diff_of = {}
-        squares_of = {}
-        OWN, ALL = 0, 1
-        totals = keep.tile([P, 2, ROW_TILES], F32, name="totals")
-
-        def first_scalar(q):
-            u, chunk, head, j = unit_of(q)
+        def leave_layer2(bank_no):
+            u, chunk, head, j = unit_of(bank_no)
             if head == LV:
                 logvar = score.tile([P, CHUNK], F32, name="logvar")
-                nc.scalar.activation(out=logvar[:], in_=acc_of[q][:], func=ACT.Tanh, bias=b2_col[:, LV, j : j + 1])
-                logvar_of[q] = logvar
+                nc.scalar.activation(
+                    out=logvar[:], in_=l2_banks[bank_no][:], func=ACT.Tanh, bias=b2_col[:, LV, j : j + 1]
+                )
+                logvar_of[bank_no] = logvar
             else:
                 if j == 0:
-                    squares_of[chunk] = chunk_pool.tile([P, 2, D_TILES, CHUNK], F32, name="squares")
+                    terms_of[chunk] = by_chunk.tile([P, 2, D_TILES, CHUNK], F32, name="terms")
                 nc.scalar.activation(
-                    out=squares_of[chunk][:, ALL, j, :], in_=acc_of[q][:], func=ACT.Square, scale=ROOT_INV_N,
+                    out=terms_of[chunk][:, ALL, j, :], in_=l2_banks[bank_no][:], func=ACT.Square, scale=ROOT_INV_N,
                     bias=centre[:, j : j + 1],
                 )
-
-        def first_vector(q):
-            u, chunk, head, j = unit_of(q)
-            if head == MU:
                 diff = score.tile([P, CHUNK], F32, name="diff")
                 nc.vector.scalar_tensor_tensor(
-                    out=diff[:], in0=acc_of[q][:], scalar=b2_col[:, MU, j : j + 1],
+                    out=diff[:], in0=l2_banks[bank_no][:], scalar=b2_col[:, MU, j : j + 1],
                     in1=y_t[:, j, chunk * CHUNK : (chunk + 1) * CHUNK], op0=ALU.add, op1=ALU.subtract,
                 )
-                diff_of[q] = diff
+                diff_of[bank_no] = diff
 
-        def second_scalar(q):
-            u, chunk, head, j = unit_of(q)
+        def second_scalar(bank_no):
+            u, chunk, head, j = unit_of(bank_no)
             if head == LV:
                 if j == 0:
-                    weight_of[chunk] = chunk_pool.tile([P, D_TILES, CHUNK], F32, name="weight")
+                    weight_of[chunk] = by_chunk.tile([P, D_TILES, CHUNK], F32, name="weight")
                 nc.scalar.activation(
-                    out=weight_of[chunk][:, j, :], in_=logvar_of[q][:], func=ACT.Exp, scale=-1.0, bias=-LN2
+                    out=weight_of[chunk][:, j, :], in_=logvar_of[bank_no][:], func=ACT.Exp, scale=-1.0, bias=-LN2
                 )
             else:
-                nc.scalar.activation(out=squares_of[chunk][:, OWN, j, :], in_=diff_of[q][:], func=ACT.Square)
+                nc.scalar.activation(out=terms_of[chunk][:, OWN, j, :], in_=diff_of[bank_no][:], func=ACT.Square)
 
-        def weighted_terms(q):
-            u, chunk, head, j = unit_of(q)
-            if u == last_of[chunk]:
-                sq = squares_of[chunk]
-                nc.vector.scalar_tensor_tensor(
-                    out=sq[:, ALL, j, :], in0=sq[:, ALL, j, :], scalar=y_var[:, j : j + 1],
-                    in1=weight_of[chunk][:, j, :], op0=ALU.add, op1=ALU.mult,
-                )
-                nc.vector.tensor_tensor(
-                    out=sq[:, OWN, j, :], in0=sq[:, OWN, j, :], in1=weight_of[chunk][:, j, :], op=ALU.mult
-                )
+        def finishes_scores(bank_no):
+            return 0 <= bank_no < STEPS and unit_of(bank_no)[0] == second_unit_of[unit_of(bank_no)[1]]
 
+        def weighted_terms(bank_no):
+            u, chunk, head, j = unit_of(bank_no)
+            terms = terms_of[chunk]
+            nc.vector.scalar_tensor_tensor(
+                out=terms[:, ALL, j, :], in0=terms[:, ALL, j, :], scalar=y_var[:, j : j + 1],
+                in1=weight_of[chunk][:, j, :], op0=ALU.add, op1=ALU.mult,
+            )
+            nc.vector.tensor_tensor(
+                out=terms[:, OWN, j, :], in0=terms[:, OWN, j, :], in1=weight_of[chunk][:, j, :], op=ALU.mult
+            )
+
+        totals = keep.tile([P, 2, ROW_TILES], F32, name="totals")
         late_totals = keep.tile([P, 2, TILES_PER_CHUNK], F32, name="late_totals")
         result = keep.tile([P, 2, ROW_TILES], F32, name="result")
         sum_banks = {}
@@ -397,7 +425,7 @@ def tile_infoncemi_pa_kernel(
                 for i in range(TILES_PER_CHUNK):
                     for j in d_tiles:
                         nc.tensor.matmul(
-                            out=bank[:, i, :], lhsT=squares_of[chunk][:, o, j, i * P : (i + 1) * P], rhs=ident[:],
+                            out=bank[:, i, :], lhsT=terms_of[chunk][:, o, j, i * P : (i + 1) * P], rhs=ident[:],
                             is_transpose=True, start=(j == d_tiles[0]), stop=(j == d_tiles[-1]),
                         )
                 sum_banks[(chunk, o)] = bank
@@ -406,19 +434,20 @@ def tile_infoncemi_pa_kernel(
             for o in (ALL, OWN):
                 nc.vector.tensor_reduce(out=out[:, o, :], in_=sum_banks[(chunk, o)][:], axis=AX.X, op=ALU.add)
 
-        Y_STEPS = {6: (0,), 7: (1,), 8: (2,), 9: (3,)}
-        X_STEP = 5
-        W1_STEP = 2
-        B_STEP = 1
+        first_chunk = slice(0, TILES_PER_CHUNK)
+        last_chunk = slice(TILES_PER_CHUNK, ROW_TILES)
+        last_bank_of = {}
+        for chunk in (0, 1):
+            last_bank_of[chunk] = second_unit_of[chunk] * HID_PASSES + D_TILES - 1
 
-        def vector_share(step):
+        def vector_banks_of(step):
             scalar_other = 0.0
             vector_other = 3.0
-            if 0 <= step - LAG_EPI < STEPS:
+            if 0 <= step - LAG_SCORE < STEPS:
                 scalar_other += 2.0
-                if unit_of(step - LAG_EPI)[2] == MU:
+                if unit_of(step - LAG_SCORE)[2] == MU:
                     vector_other += 1.0
-            if 0 <= step - LAG_Z < STEPS and unit_of(step - LAG_Z)[0] == last_of[unit_of(step - LAG_Z)[1]]:
+            if finishes_scores(step - LAG_WEIGHTED):
                 vector_other += 2.0
             if step == X_STEP:
                 scalar_other += 2.0
@@ -429,103 +458,82 @@ def tile_infoncemi_pa_kernel(
                 vector_other += 0.5
             return max(0, min(PACK - 1, int((PACK + scalar_other - vector_other) / 2.0 + 0.5)))
 
-        transpose_x(0, psum_tr, "tr")
-        transpose_x(1, psum_tr, "tr")
+        transpose_x(0)
+        transpose_x(1)
         regroup_x(0)
         regroup_x(1)
-        nc.vector.tensor_copy(out=b1_col[:, LV, :], in_=b1_bf[:, LV, :])
+        nc.vector.tensor_copy(out=b1_col[:, first_head, :], in_=b1_bf[:, first_head, :])
         quantise_x(0)
-        permute_planes(LV)
-        permute_w1(LV, 0)
+        regroup_planes(first_head)
+        regroup_w1(first_head, 0)
         quantise_x(1)
         for g in range(1, HID_PASSES):
-            permute_w1(LV, g)
-
-        b2_banks = {}
-
-        def b2_tensor():
-            bank = psum_tr.tile([P, 2, D_TILES], F32, name="b2_bank", tag="tr")
-            for head in (MU, LV):
-                for j in range(D_TILES):
-                    nc.tensor.matmul(
-                        out=bank[:, head, j : j + 1], lhsT=b2_rows[:, head, j * P : (j + 1) * P],
-                        rhs=ones_bf[:, 0:1], start=True, stop=True,
-                    )
-            b2_banks[0] = bank
+            regroup_w1(first_head, g)
 
         for i in range(STEPS + LAG_SUM + 1):
             if i < STEPS:
                 layer1(i)
-            if i == B_STEP:
+            if i == BIAS_STEP:
                 b2_tensor()
             if i == X_STEP:
-                transpose_x(2, psum_tr, "tr")
-                transpose_x(3, psum_tr, "tr")
-            for j in Y_STEPS.get(i, ()):
-                y_tensor(j)
-            if 0 <= i - LAG_L2 < STEPS:
-                layer2(i - LAG_L2)
-            if i - LAG_SUM == last_of[0] * HID_PASSES + 3:
-                sum_over_d_tensor(0, (0, 1, 2, 3), psum_tr, "tr")
-            if i - LAG_SUM == last_of[1] * HID_PASSES + 1:
-                sum_over_d_tensor(1, (0, 1), psum_tr, "tr")
-            if i - LAG_SUM == last_of[1] * HID_PASSES + 3:
+                transpose_x(2)
+                transpose_x(3)
+            if i in Y_STEPS:
+                y_tensor(Y_STEPS.index(i))
+            if 0 <= i - LAG_LAYER2 < STEPS:
+                layer2(i - LAG_LAYER2)
+            if i - LAG_SUM == last_bank_of[0]:
+                sum_over_d_tensor(0, (0, 1, 2, 3), psum_misc, "misc")
+            if i - LAG_SUM == last_bank_of[1] - 2:
+                sum_over_d_tensor(1, (0, 1), psum_misc, "misc")
+            if i - LAG_SUM == last_bank_of[1]:
                 sum_over_d_tensor(1, (2, 3), psum_l1, "l1")
 
             if 0 <= i - 1 < STEPS:
                 interleave(i - 1)
-            if 0 <= i - LAG_EPI < STEPS:
-                first_scalar(i - LAG_EPI)
-                first_vector(i - LAG_EPI)
+            if 0 <= i - LAG_SCORE < STEPS:
+                leave_layer2(i - LAG_SCORE)
             if i < STEPS:
-                new_stage(i)
-                share = vector_share(i)
-                for t in range(PACK - share):
-                    leave_l1(i, t, "scalar")
-                for t in range(PACK - share, PACK):
-                    leave_l1(i, t, "vector")
+                leave_layer1(i, vector_banks_of(i))
             if i == X_STEP:
                 regroup_x(2)
                 regroup_x(3)
-            for j in Y_STEPS.get(i, ()):
-                y_scalar(j)
-            if i == B_STEP:
-                nc.vector.tensor_copy(out=b2_col[:], in_=b2_banks[0][:])
-                nc.vector.tensor_scalar(
-                    out=b2_scaled[:], in0=b2_banks[0][:, MU, :], scalar1=ROOT_INV_N, scalar2=None, op0=ALU.mult
-                )
-                nc.vector.tensor_copy(out=b1_col[:, MU, :], in_=b1_bf[:, MU, :])
+            if i in Y_STEPS:
+                y_scalar(Y_STEPS.index(i))
+            if i == BIAS_STEP:
+                later_biases_vector()
             if i == X_STEP:
                 quantise_x(2)
                 quantise_x(3)
             if i == W1_STEP:
-                permute_planes(MU)
+                regroup_planes(second_head)
             if W1_STEP <= i < W1_STEP + HID_PASSES:
-                permute_w1(MU, i - W1_STEP)
-            for j in Y_STEPS.get(i, ()):
-                y_vector(j)
-            if i == max(Y_STEPS):
-                y_finish()
+                regroup_w1(second_head, i - W1_STEP)
+            if i in Y_STEPS:
+                y_vector(Y_STEPS.index(i))
+            if i == Y_STEPS[-1]:
+                y_constants()
             if 0 <= i - 1 < STEPS:
                 quantise_hidden(i - 1)
-            if 0 <= i - LAG_EPI < STEPS:
-                second_scalar(i - LAG_EPI)
-            if i == STEPS + 3:
-                sum_over_d_vector(0, totals[:, :, 0:TILES_PER_CHUNK])
+            if 0 <= i - LAG_SCORE < STEPS:
+                second_scalar(i - LAG_SCORE)
+            if i == last_bank_of[1] - D_TILES + 1 + LAG_WEIGHTED:
+                sum_over_d_vector(0, totals[:, :, first_chunk])
+            if finishes_scores(i - LAG_WEIGHTED):
+                weighted_terms(i - LAG_WEIGHTED)
+            if i == last_bank_of[1] - D_TILES + 1 + LAG_WEIGHTED:
                 nc.vector.tensor_scalar(
-                    out=result[:, :, 0:TILES_PER_CHUNK], in0=totals[:, :, 0:TILES_PER_CHUNK], scalar1=-1.0, scalar2=None,
+                    out=result[:, :, first_chunk], in0=totals[:, :, first_chunk], scalar1=-1.0, scalar2=None,
                     op0=ALU.mult,
                 )
-            if 0 <= i - LAG_Z < STEPS:
-                weighted_terms(i - LAG_Z)
-            if i - LAG_SUM == last_of[1] * HID_PASSES + 2:
-                sum_over_d_vector(1, totals[:, :, TILES_PER_CHUNK:ROW_TILES])
-            if i - LAG_SUM == last_of[1] * HID_PASSES + 3:
+            if i - LAG_SUM == last_bank_of[1] - 1:
+                sum_over_d_vector(1, totals[:, :, last_chunk])
+            if i - LAG_SUM == last_bank_of[1]:
                 sum_over_d_vector(1, late_totals)
 
         for o in (ALL, OWN):
             nc.vector.scalar_tensor_tensor(
-                out=result[:, o, TILES_PER_CHUNK:ROW_TILES], in0=totals[:, o, TILES_PER_CHUNK:ROW_TILES], scalar=-1.0,
+                out=result[:, o, last_chunk], in0=totals[:, o, last_chunk], scalar=-1.0,
                 in1=late_totals[:, o, :], op0=ALU.mult, op1=ALU.subtract,
             )
         nc.scalar.dma_start(out=out_1.rearrange("(p r) -> p r", r=ROW_TILES), in_=result[:, ALL, :])

@@ -463,8 +463,8 @@ def tile_infoncemi_pa_kernel(
         regroup_x(0)
         regroup_x(1)
         nc.vector.tensor_copy(out=b1_col[:, first_head, :], in_=b1_bf[:, first_head, :])
-        quantise_x(0)
         regroup_planes(first_head)
+        quantise_x(0)
         regroup_w1(first_head, 0)
         quantise_x(1)
         for g in range(1, HID_PASSES):

@@ -415,7 +415,6 @@ def tile_infoncemi_pa_kernel(
             )
 
         totals = keep.tile([P, 2, ROW_TILES], F32, name="totals")
-        late_totals = keep.tile([P, 2, TILES_PER_CHUNK], F32, name="late_totals")
         result = keep.tile([P, 2, ROW_TILES], F32, name="result")
         sum_banks = {}
 
@@ -433,6 +432,39 @@ def tile_infoncemi_pa_kernel(
         def sum_over_d_vector(chunk, out):
             for o in (ALL, OWN):
                 nc.vector.tensor_reduce(out=out[:, o, :], in_=sum_banks[(chunk, o)][:], axis=AX.X, op=ALU.add)
+
+        last_sum_banks = {}
+
+        def last_sums_tensor(o, row_tiles, d_tiles, pool, tag):
+            for i in row_tiles:
+                if (o, i) not in last_sum_banks:
+                    last_sum_banks[(o, i)] = pool.tile([P, P], F32, name="last_sum_bank", tag=tag)
+                for j in d_tiles:
+                    nc.tensor.matmul(
+                        out=last_sum_banks[(o, i)][:], lhsT=terms_of[1][:, o, j, i * P : (i + 1) * P], rhs=ident[:],
+                        is_transpose=True, start=(j == 0), stop=(j == D_TILES - 1),
+                    )
+
+        def last_sums_vector(o, row_tiles):
+            for i in row_tiles:
+                nc.vector.tensor_reduce(
+                    out=totals[:, o, TILES_PER_CHUNK + i : TILES_PER_CHUNK + i + 1], in_=last_sum_banks[(o, i)][:],
+                    axis=AX.X, op=ALU.add,
+                )
+
+        sum_scrap = keep.tile([P, P], F32, name="sum_scrap")
+
+        def last_sums_scalar(o, row_tiles):
+            for i in row_tiles:
+                nc.scalar.activation(
+                    out=sum_scrap[:], in_=last_sum_banks[(o, i)][:], func=ACT.Copy, scale=-1.0,
+                    accum_out=result[:, o, TILES_PER_CHUNK + i : TILES_PER_CHUNK + i + 1],
+                )
+
+        def change_sign(o):
+            nc.vector.tensor_scalar(
+                out=result[:, o, last_chunk], in0=totals[:, o, last_chunk], scalar1=-1.0, scalar2=None, op0=ALU.mult
+            )
 
         first_chunk = slice(0, TILES_PER_CHUNK)
         last_chunk = slice(TILES_PER_CHUNK, ROW_TILES)
@@ -484,10 +516,15 @@ def tile_infoncemi_pa_kernel(
                 layer2(i - LAG_LAYER2)
             if i - LAG_SUM == last_bank_of[0]:
                 sum_over_d_tensor(0, (0, 1, 2, 3), psum_misc, "misc")
-            if i - LAG_SUM == last_bank_of[1] - 2:
-                sum_over_d_tensor(1, (0, 1), psum_misc, "misc")
-            if i - LAG_SUM == last_bank_of[1]:
-                sum_over_d_tensor(1, (2, 3), psum_l1, "l1")
+            j_last = i - LAG_SUM - (last_bank_of[1] - D_TILES + 1)
+            if 0 <= j_last < D_TILES:
+                last_sums_tensor(ALL, (0, 1, 2, 3), (j_last,), psum_l1, "l1")
+                last_sums_tensor(OWN, (0, 1), (j_last,), psum_misc, "misc")
+                for late in (1, 2):
+                    if j_last == late:
+                        last_sums_tensor(OWN, (1 + late,), tuple(range(late + 1)), psum_l2, "l2")
+                    if j_last > late:
+                        last_sums_tensor(OWN, (1 + late,), (j_last,), psum_l2, "l2")
 
             if 0 <= i - 1 < STEPS:
                 interleave(i - 1)
@@ -526,15 +563,9 @@ def tile_infoncemi_pa_kernel(
                     out=result[:, :, first_chunk], in0=totals[:, :, first_chunk], scalar1=-1.0, scalar2=None,
                     op0=ALU.mult,
                 )
-            if i - LAG_SUM == last_bank_of[1] - 1:
-                sum_over_d_vector(1, totals[:, :, last_chunk])
-            if i - LAG_SUM == last_bank_of[1]:
-                sum_over_d_vector(1, late_totals)
 
-        for o in (ALL, OWN):
-            nc.vector.scalar_tensor_tensor(
-                out=result[:, o, last_chunk], in0=totals[:, o, last_chunk], scalar=-1.0,
-                in1=late_totals[:, o, :], op0=ALU.mult, op1=ALU.subtract,
-            )
+        last_sums_scalar(ALL, (0, 1, 2, 3))
         nc.scalar.dma_start(out=out_1.rearrange("(p r) -> p r", r=ROW_TILES), in_=result[:, ALL, :])
+        last_sums_vector(OWN, (0, 1, 2, 3))
+        change_sign(OWN)
         nc.sync.dma_start(out=out_0.rearrange("(p r) -> p r", r=ROW_TILES), in_=result[:, OWN, :])

@@ -44,6 +44,8 @@ X_STEP = 5
 W1_STEP = 2
 BIAS_STEP = 1
 
+WARM_UP = 5
+
 LN2 = 0.6931471805599453
 INV_N = 1.0 / N_ROWS
 ROOT_INV_N = 1.0 / 32.0
@@ -104,8 +106,10 @@ def tile_infoncemi_pa_kernel(
         ident = keep.tile([P, P], F32, name="ident")
         ident_bf = keep.tile([P, P], BF16, name="ident_bf")
         table_seed = keep.tile([P, 1], F32, name="table_seed")
+        warm = keep.tile([P, CHUNK], BF16, name="warm")
 
         nc.vector.memset(table_seed[:], 0.0)
+        nc.vector.memset(warm[:], 0.0)
         nc.vector.memset(planes[:].bitcast(I32), 0)
         nc.vector.memset(ones_bf[:], 1.0)
         nc.vector.memset(b2_rows[:].bitcast(I32), 0)
@@ -490,6 +494,9 @@ def tile_infoncemi_pa_kernel(
                 vector_other += 0.5
             return max(0, min(PACK - 1, int((PACK + scalar_other - vector_other) / 2.0 + 0.5)))
 
+        warm_bank = psum_l1.tile([P, CHUNK], F32, name="warm_bank", tag="l1")
+        for k in range(WARM_UP):
+            nc.tensor.matmul(out=warm_bank[:], lhsT=warm[:, 0:P], rhs=warm[:], start=True, stop=True)
         transpose_x(0)
         transpose_x(1)
         regroup_x(0)

@@ -355,11 +355,16 @@ def tile_infoncemi_pa_kernel(
         for u in range(UNITS):
             second_unit_of[UNIT_ORDER[u][0]] = u
 
-        def layer2(bank_no):
+        def layer2(bank_no, passes=(0, 1, 2, 3), in_l1=False):
             u, chunk, head, j = unit_of(bank_no)
             codes, scales = codes_of[u]
-            bank = psum_l2.tile([P, CHUNK], F32, name="l2_bank", tag="l2")
-            for g in range(HID_PASSES):
+            if passes[0] == 0:
+                if in_l1:
+                    l2_banks[bank_no] = psum_l1.tile([P, CHUNK], F32, name="l2_bank_late", tag="l1")
+                else:
+                    l2_banks[bank_no] = psum_l2.tile([P, CHUNK], F32, name="l2_bank", tag="l2")
+            bank = l2_banks[bank_no]
+            for g in passes:
                 nc.tensor.matmul_mx(
                     out=bank[:],
                     lhsT=w2[:, head, g, j * P : (j + 1) * P].bitcast(FP8X4),
@@ -369,7 +374,6 @@ def tile_infoncemi_pa_kernel(
                     start=(g == 0),
                     stop=(g == HID_PASSES - 1),
                 )
-            l2_banks[bank_no] = bank
 
         def leave_layer2(bank_no):
             u, chunk, head, j = unit_of(bank_no)
@@ -422,8 +426,8 @@ def tile_infoncemi_pa_kernel(
         result = keep.tile([P, 2, ROW_TILES], F32, name="result")
         sum_banks = {}
 
-        def sum_over_d_tensor(chunk, d_tiles, pool, tag):
-            for o in (ALL, OWN):
+        def sum_over_d_tensor(chunk, d_tiles, pool, tag, outputs=(ALL, OWN)):
+            for o in outputs:
                 bank = pool.tile([P, TILES_PER_CHUNK, P], F32, name="sum_bank", tag=tag)
                 for i in range(TILES_PER_CHUNK):
                     for j in d_tiles:
@@ -433,8 +437,8 @@ def tile_infoncemi_pa_kernel(
                         )
                 sum_banks[(chunk, o)] = bank
 
-        def sum_over_d_vector(chunk, out):
-            for o in (ALL, OWN):
+        def sum_over_d_vector(chunk, out, outputs=(ALL, OWN)):
+            for o in outputs:
                 nc.vector.tensor_reduce(out=out[:, o, :], in_=sum_banks[(chunk, o)][:], axis=AX.X, op=ALU.add)
 
         last_sum_banks = {}
@@ -492,6 +496,8 @@ def tile_infoncemi_pa_kernel(
                 scalar_other += 1.0
             if W1_STEP <= step < W1_STEP + HID_PASSES:
                 vector_other += 0.5
+            if step == STEPS - 1:
+                return 0
             return max(0, min(PACK - 1, int((PACK + scalar_other - vector_other) / 2.0 + 0.5)))
 
         warm_bank = psum_l1.tile([P, CHUNK], F32, name="warm_bank", tag="l1")
@@ -509,6 +515,8 @@ def tile_infoncemi_pa_kernel(
         for g in range(1, HID_PASSES):
             regroup_w1(first_head, g)
 
+        first_last = last_bank_of[1] - D_TILES + 1
+        put_off = (first_last - 2, first_last - 1)
         for i in range(STEPS + LAG_SUM + 1):
             if i < STEPS:
                 layer1(i)
@@ -519,22 +527,35 @@ def tile_infoncemi_pa_kernel(
                 transpose_x(3)
             if i in Y_STEPS:
                 y_tensor(Y_STEPS.index(i))
-            if 0 <= i - LAG_LAYER2 < STEPS:
+            if 0 <= i - LAG_LAYER2 < first_last:
                 layer2(i - LAG_LAYER2)
             if i - LAG_SUM == last_bank_of[0]:
-                sum_over_d_tensor(0, (0, 1, 2, 3), psum_misc, "misc")
-            j_last = i - LAG_SUM - (last_bank_of[1] - D_TILES + 1)
+                sum_over_d_tensor(0, (0, 1, 2, 3), psum_misc, "misc", (ALL,))
+            if i == STEPS:
+                layer2(first_last, (0, 1, 2), True)
+                layer2(first_last + 1, (0, 1, 2), True)
+            if i == STEPS + 1:
+                layer2(first_last, (3,), True)
+                layer2(first_last + 1, (3,), True)
+                layer2(first_last + 2, (0, 1, 2, 3), True)
+                sum_over_d_tensor(0, (0, 1, 2, 3), psum_misc, "misc", (OWN,))
+            if i == STEPS + 2:
+                layer2(first_last + 3, (0, 1, 2, 3), True)
+            j_last = i - LAG_SUM - first_last
             if 0 <= j_last < D_TILES:
-                last_sums_tensor(ALL, (0, 1, 2, 3), (j_last,), psum_l1, "l1")
-                last_sums_tensor(OWN, (0, 1), (j_last,), psum_misc, "misc")
-                for late in (1, 2):
+                last_sums_tensor(ALL, (0, 1), (j_last,), psum_l2, "l2")
+                last_sums_tensor(ALL, (2, 3), (j_last,), psum_l1, "l1")
+                last_sums_tensor(OWN, (0,), (j_last,), psum_misc, "misc")
+                for row_tile, late, pool, tag in ((1, 1, psum_l1, "l1"), (2, 2, psum_misc, "misc"), (3, 2, psum_l1, "l1")):
                     if j_last == late:
-                        last_sums_tensor(OWN, (1 + late,), tuple(range(late + 1)), psum_l2, "l2")
+                        last_sums_tensor(OWN, (row_tile,), tuple(range(late + 1)), pool, tag)
                     if j_last > late:
-                        last_sums_tensor(OWN, (1 + late,), (j_last,), psum_l2, "l2")
+                        last_sums_tensor(OWN, (row_tile,), (j_last,), pool, tag)
 
             if 0 <= i - 1 < STEPS:
                 interleave(i - 1)
+            if i == STEPS:
+                quantise_hidden(i - 1)
             if 0 <= i - LAG_SCORE < STEPS:
                 leave_layer2(i - LAG_SCORE)
             if i < STEPS:
@@ -557,15 +578,19 @@ def tile_infoncemi_pa_kernel(
                 y_vector(Y_STEPS.index(i))
             if i == Y_STEPS[-1]:
                 y_constants()
-            if 0 <= i - 1 < STEPS:
+            if 0 <= i - 1 < STEPS - 1:
                 quantise_hidden(i - 1)
-            if 0 <= i - LAG_SCORE < STEPS:
+            if 0 <= i - LAG_SCORE < STEPS and i - LAG_SCORE not in put_off:
                 second_scalar(i - LAG_SCORE)
-            if i == last_bank_of[1] - D_TILES + 1 + LAG_WEIGHTED:
-                sum_over_d_vector(0, totals[:, :, first_chunk])
+            if i - LAG_SCORE - 2 in put_off:
+                second_scalar(i - LAG_SCORE - 2)
+            if i == first_last + LAG_WEIGHTED:
+                sum_over_d_vector(0, totals[:, :, first_chunk], (ALL,))
             if finishes_scores(i - LAG_WEIGHTED):
                 weighted_terms(i - LAG_WEIGHTED)
-            if i == last_bank_of[1] - D_TILES + 1 + LAG_WEIGHTED:
+            if i == first_last + LAG_WEIGHTED + 1:
+                sum_over_d_vector(0, totals[:, :, first_chunk], (OWN,))
+            if i == first_last + LAG_WEIGHTED + 2:
                 nc.vector.tensor_scalar(
                     out=result[:, :, first_chunk], in0=totals[:, :, first_chunk], scalar1=-1.0, scalar2=None,
                     op0=ALU.mult,

@@ -556,8 +556,10 @@ def tile_infoncemi_pa_kernel(
                 interleave(i - 1)
             if i == STEPS:
                 quantise_hidden(i - 1)
-            if 0 <= i - LAG_SCORE < STEPS:
+            if 0 <= i - LAG_SCORE < STEPS and i - LAG_SCORE != first_last + 1:
                 leave_layer2(i - LAG_SCORE)
+            if i - LAG_SCORE == first_last:
+                leave_layer2(first_last + 1)
             if i < STEPS:
                 leave_layer1(i, vector_banks_of(i))
             if i == X_STEP:
@@ -580,10 +582,10 @@ def tile_infoncemi_pa_kernel(
                 y_constants()
             if 0 <= i - 1 < STEPS - 1:
                 quantise_hidden(i - 1)
+            if i - LAG_SCORE - 4 in put_off:
+                second_scalar(i - LAG_SCORE - 4)
             if 0 <= i - LAG_SCORE < STEPS and i - LAG_SCORE not in put_off:
                 second_scalar(i - LAG_SCORE)
-            if i - LAG_SCORE - 2 in put_off:
-                second_scalar(i - LAG_SCORE - 2)
             if i == first_last + LAG_WEIGHTED:
                 sum_over_d_vector(0, totals[:, :, first_chunk], (ALL,))
             if finishes_scores(i - LAG_WEIGHTED):

@@ -418,8 +418,9 @@ def tile_infoncemi_pa_kernel(
                 out=terms[:, ALL, j, :], in0=terms[:, ALL, j, :], scalar=y_var[:, j : j + 1],
                 in1=weight_of[chunk][:, j, :], op0=ALU.add, op1=ALU.mult,
             )
-            nc.vector.tensor_tensor(
-                out=terms[:, OWN, j, :], in0=terms[:, OWN, j, :], in1=weight_of[chunk][:, j, :], op=ALU.mult
+            nc.vector.scalar_tensor_tensor(
+                out=terms[:, OWN, j, :], in0=terms[:, OWN, j, :], scalar=(-1.0 if chunk == 1 else 1.0),
+                in1=weight_of[chunk][:, j, :], op0=ALU.mult, op1=ALU.mult,
             )
 
         totals = keep.tile([P, 2, ROW_TILES], F32, name="totals")
@@ -456,7 +457,7 @@ def tile_infoncemi_pa_kernel(
         def last_sums_vector(o, row_tiles):
             for i in row_tiles:
                 nc.vector.tensor_reduce(
-                    out=totals[:, o, TILES_PER_CHUNK + i : TILES_PER_CHUNK + i + 1], in_=last_sum_banks[(o, i)][:],
+                    out=result[:, o, TILES_PER_CHUNK + i : TILES_PER_CHUNK + i + 1], in_=last_sum_banks[(o, i)][:],
                     axis=AX.X, op=ALU.add,
                 )
 
@@ -469,13 +470,7 @@ def tile_infoncemi_pa_kernel(
                     accum_out=result[:, o, TILES_PER_CHUNK + i : TILES_PER_CHUNK + i + 1],
                 )
 
-        def change_sign(o):
-            nc.vector.tensor_scalar(
-                out=result[:, o, last_chunk], in0=totals[:, o, last_chunk], scalar1=-1.0, scalar2=None, op0=ALU.mult
-            )
-
         first_chunk = slice(0, TILES_PER_CHUNK)
-        last_chunk = slice(TILES_PER_CHUNK, ROW_TILES)
         last_bank_of = {}
         for chunk in (0, 1):
             last_bank_of[chunk] = second_unit_of[chunk] * HID_PASSES + D_TILES - 1
@@ -601,5 +596,4 @@ def tile_infoncemi_pa_kernel(
         last_sums_scalar(ALL, (0, 1, 2, 3))
         nc.scalar.dma_start(out=out_1.rearrange("(p r) -> p r", r=ROW_TILES), in_=result[:, ALL, :])
         last_sums_vector(OWN, (0, 1, 2, 3))
-        change_sign(OWN)
         nc.sync.dma_start(out=out_0.rearrange("(p r) -> p r", r=ROW_TILES), in_=result[:, OWN, :])

@@ -328,8 +328,8 @@ def tile_infoncemi_pa_kernel(
         def interleave(step):
             grouped = hidden.tile([P, CHUNK, PACK], BF16, name="grouped", align_bytes=64)
             nc.vector.tensor_copy(
-                out=grouped[:].rearrange("p (c i) t -> p c t i", i=4),
-                in_=parts_of[step][:].rearrange("p t (c i) -> p c t i", i=4),
+                out=grouped[:].rearrange("p (c i) t -> p c t i", i=8),
+                in_=parts_of[step][:].rearrange("p t (c i) -> p c t i", i=8),
             )
             grouped_of[step] = grouped
 

@@ -45,6 +45,7 @@ W1_STEP = 2
 BIAS_STEP = 1
 
 WARM_UP = 5
+HOLD_UP = 3
 
 LN2 = 0.6931471805599453
 INV_N = 1.0 / N_ROWS
@@ -108,8 +109,8 @@ def tile_infoncemi_pa_kernel(
         table_seed = keep.tile([P, 1], F32, name="table_seed")
         warm = keep.tile([P, CHUNK], BF16, name="warm")
 
+        nc.gpsimd.memset(warm[:], 0.0)
         nc.vector.memset(table_seed[:], 0.0)
-        nc.vector.memset(warm[:], 0.0)
         nc.vector.memset(planes[:].bitcast(I32), 0)
         nc.vector.memset(ones_bf[:], 1.0)
         nc.vector.memset(b2_rows[:].bitcast(I32), 0)
@@ -214,6 +215,19 @@ def tile_infoncemi_pa_kernel(
                 out=x_codes[:, pair * 2 * P : (pair + 1) * 2 * P].bitcast(FP8X4),
                 scales=x_scales[:, pair * 2 * P : (pair + 1) * 2 * P],
                 in_=x_grouped[:, pair * 2 * K_PASS : (pair + 1) * 2 * K_PASS],
+            )
+
+        def regroup_x_tile(r):
+            nc.scalar.copy(
+                out=x_grouped_words[:, r * P : (r + 1) * P, :],
+                in_=x_banks[r // 2][:, :, (r % 2) * P : (r % 2 + 1) * P].rearrange("p u n -> p n u"),
+            )
+
+        def quantise_x_tile(r):
+            nc.vector.quantize_mx(
+                out=x_codes[:, r * P : (r + 1) * P].bitcast(FP8X4),
+                scales=x_scales[:, r * P : (r + 1) * P],
+                in_=x_grouped[:, r * K_PASS : (r + 1) * K_PASS],
             )
 
         b2_scaled = keep.tile([P, D_TILES], F32, name="b2_scaled")
@@ -500,13 +514,17 @@ def tile_infoncemi_pa_kernel(
             nc.tensor.matmul(out=warm_bank[:], lhsT=warm[:, 0:P], rhs=warm[:], start=True, stop=True)
         transpose_x(0)
         transpose_x(1)
+        for k in range(HOLD_UP):
+            nc.tensor.matmul(out=warm_bank[:], lhsT=warm[:, 0:P], rhs=warm[:], start=True, stop=True)
         regroup_x(0)
-        regroup_x(1)
+        regroup_x_tile(2)
+        regroup_x_tile(3)
         nc.vector.tensor_copy(out=b1_col[:, first_head, :], in_=b1_bf[:, first_head, :])
         regroup_planes(first_head)
         quantise_x(0)
         regroup_w1(first_head, 0)
-        quantise_x(1)
+        quantise_x_tile(2)
+        quantise_x_tile(3)
         for g in range(1, HID_PASSES):
             regroup_w1(first_head, g)
 

from contextlib import ExitStack

import concourse.mybir as mybir
from concourse.masks import make_identity

FLOPS = 4 * 2 * 1024 * 512 * 2048

F32 = mybir.dt.float32
BF16 = mybir.dt.bfloat16
I32 = mybir.dt.int32
U32 = mybir.dt.uint32
U8 = mybir.dt.uint8
FP8X4 = mybir.dt.float8_e4m3fn_x4
ALU = mybir.AluOpType
ACT = mybir.ActivationFunctionType
AX = mybir.AxisListType

P = 128
N_ROWS = 1024
X_DIM = 512
Y_DIM = 512
HID = 2048
ROW_TILES = N_ROWS // P
K_PASS = 512
PACK = 4
HID_PASSES = HID // K_PASS
D_TILES = Y_DIM // P
CHUNK = 512
TILES_PER_CHUNK = CHUNK // P
MU, LV = 0, 1
OWN, ALL = 0, 1

UNIT_ORDER = ((0, LV), (0, MU), (1, MU), (1, LV))
UNITS = len(UNIT_ORDER)
STEPS = UNITS * HID_PASSES

LAG_LAYER2 = 5
LAG_SCORE = 6
LAG_WEIGHTED = 7
LAG_SUM = 8

Y_STEPS = (6, 7, 8, 9)
X_STEP = 5
W1_STEP = 2
BIAS_STEP = 1

WARM_UP = 5
HOLD_UP = 3

LN2 = 0.6931471805599453
INV_N = 1.0 / N_ROWS
ROOT_INV_N = 1.0 / 32.0
assert ROOT_INV_N * ROOT_INV_N == INV_N


def tile_infoncemi_pa_kernel(
    tc,
    x_samples,
    y_samples,
    mu_W1_words,
    mu_W1_scales,
    mu_b1,
    mu_W2_words,
    mu_W2_scales,
    mu_b2,
    lv_W1_words,
    lv_W1_scales,
    lv_b1,
    lv_W2_words,
    lv_W2_scales,
    lv_b2,
    out_0,
    out_1,
):
    nc = tc.nc
    w1_words_in = {MU: mu_W1_words, LV: lv_W1_words}
    w1_scales_in = {MU: mu_W1_scales, LV: lv_W1_scales}
    w2_words_in = {MU: mu_W2_words, LV: lv_W2_words}
    w2_scales_in = {MU: mu_W2_scales, LV: lv_W2_scales}
    b1_in = {MU: mu_b1, LV: lv_b1}
    b2_in = {MU: mu_b2, LV: lv_b2}

    with ExitStack() as ctx:
        ctx.enter_context(tc.manual_schedule())
        keep = ctx.enter_context(tc.tile_pool(name="keep", bufs=1))
        hidden = ctx.enter_context(tc.tile_pool(name="hidden", bufs=3))
        score = ctx.enter_context(tc.tile_pool(name="score", bufs=3))
        by_chunk = ctx.enter_context(tc.tile_pool(name="by_chunk", bufs=2))
        psum_l1 = ctx.enter_context(tc.psum_pool(name="psum_l1", bufs=4))
        psum_l2 = ctx.enter_context(tc.psum_pool(name="psum_l2", bufs=2))
        psum_misc = ctx.enter_context(tc.psum_pool(name="psum_misc", bufs=2))

        x_sb = keep.tile([P, ROW_TILES, X_DIM], BF16, name="x_sb")
        y_sb = keep.tile([P, ROW_TILES, Y_DIM], BF16, name="y_sb")
        w1 = keep.tile([P, 2, HID], U32, name="w1", align_bytes=64)
        w1_regrouped = keep.tile([P, 2, HID], U32, name="w1_regrouped", align_bytes=64)
        w2 = keep.tile([P, 2, HID_PASSES, Y_DIM], U32, name="w2", align_bytes=64)
        planes = keep.tile([P, 4, 512], U8, name="planes", align_bytes=64)
        planes_regrouped = keep.tile([P, 2, 512], U8, name="planes_regrouped", align_bytes=64)
        w1_slot = {MU: 0, LV: 1}
        w2_slot = {MU: 2, LV: 3}
        b1_bf = keep.tile([P, 2, HID_PASSES * PACK], BF16, name="b1_bf")
        b1_col = keep.tile([P, 2, HID_PASSES * PACK], F32, name="b1_col")
        b2_rows = keep.tile([P, 2, Y_DIM], BF16, name="b2_rows")
        b2_col = keep.tile([P, 2, D_TILES], F32, name="b2_col")
        ones_bf = keep.tile([P, 2], BF16, name="ones_bf")
        ident = keep.tile([P, P], F32, name="ident")
        ident_bf = keep.tile([P, P], BF16, name="ident_bf")
        table_seed = keep.tile([P, 1], F32, name="table_seed")
        warm = keep.tile([P, CHUNK], BF16, name="warm")

        nc.gpsimd.memset(warm[:], 0.0)
        nc.vector.memset(table_seed[:], 0.0)
        nc.vector.memset(planes[:].bitcast(I32), 0)
        nc.vector.memset(ones_bf[:], 1.0)
        nc.vector.memset(b2_rows[:].bitcast(I32), 0)
        make_identity(nc, ident[:])
        make_identity(nc, ident_bf[:])

        def load_planes(slot, four_planes):
            for quad in range(4):
                nc.sync.dma_start(
                    out=planes[32 * quad : 32 * quad + 16, slot, :].bitcast(I32),
                    in_=four_planes[:, 4 * quad : 4 * quad + 4, :].bitcast(I32),
                )

        def load_w1_planes(head):
            load_planes(w1_slot[head], w1_scales_in[head][0].rearrange("q (c n) -> c q n", c=4))

        def load_w1(head, g):
            flat = w1_words_in[head][0].rearrange("p n t -> p (n t)")
            nc.sync.dma_start(
                out=w1[:, head, g * K_PASS : (g + 1) * K_PASS].bitcast(I32),
                in_=flat[:, g * 4 * K_PASS : (g + 1) * 4 * K_PASS].bitcast(I32),
            )

        def load_w2(head):
            nc.sync.dma_start(
                out=w2[:, head, :, :].bitcast(I32),
                in_=w2_words_in[head].rearrange("g p n t -> p g (n t)").bitcast(I32),
            )

        def load_b1(queue, head):
            queue.dma_start(
                out=b1_bf[:, head, :].rearrange("p (g t) -> p g t", t=PACK),
                in_=b1_in[head].rearrange("(g p t) -> p g t", g=HID_PASSES, t=PACK),
            )

        def load_b2(queue, head):
            queue.dma_start(out=b2_rows[0:1, head, :], in_=b2_in[head].rearrange("(o n) -> o n", o=1))

        first_head = UNIT_ORDER[0][1]
        second_head = UNIT_ORDER[1][1]
        x_view = x_samples.rearrange("(p r) k -> p r k", r=ROW_TILES)
        nc.sync.dma_start(out=x_sb[:, 0:2, :], in_=x_view[:, 0:2, :])
        nc.sync.dma_start(out=x_sb[:, 2:4, :], in_=x_view[:, 2:4, :])
        load_w1_planes(first_head)
        load_w1(first_head, 0)
        load_b1(nc.scalar, first_head)
        nc.scalar.activation(out=table_seed[:], in_=table_seed[:], func=ACT.Exp)
        for g in range(1, HID_PASSES):
            load_w1(first_head, g)
        load_b1(nc.sync, second_head)
        load_b2(nc.sync, first_head)
        load_b2(nc.sync, second_head)
        load_w1_planes(second_head)
        for g in range(HID_PASSES):
            load_w1(second_head, g)
        load_planes(w2_slot[first_head], w2_scales_in[first_head])
        load_w2(first_head)
        nc.sync.dma_start(out=x_sb[:, 4:ROW_TILES, :], in_=x_view[:, 4:ROW_TILES, :])
        nc.sync.dma_start(out=y_sb[:], in_=y_samples.rearrange("(p r) d -> p r d", r=ROW_TILES))
        load_planes(w2_slot[second_head], w2_scales_in[second_head])
        load_w2(second_head)

        def regroup_planes(head):
            nc.vector.tensor_copy(
                out=planes_regrouped[:, head, :].rearrange("p (t m) -> p t m", t=PACK),
                in_=planes[:, w1_slot[head], :].rearrange("p (m t) -> p t m", t=PACK),
            )

        def regroup_w1(head, g):
            cols = slice(g * K_PASS, (g + 1) * K_PASS)
            nc.vector.tensor_copy(
                out=w1_regrouped[:, head, cols].bitcast(I32).rearrange("p (t m) -> p t m", t=PACK),
                in_=w1[:, head, cols].bitcast(I32).rearrange("p (m t) -> p t m", t=PACK),
            )

        x_grouped = keep.tile([P, ROW_TILES * K_PASS], BF16, name="x_grouped", align_bytes=64)
        x_codes = keep.tile([P, N_ROWS], U32, name="x_codes", align_bytes=64)
        x_scales = keep.tile([P, N_ROWS], U8, name="x_scales", align_bytes=64)
        x_words = x_sb[:].bitcast(F32)
        x_grouped_words = x_grouped[:].bitcast(F32).rearrange("p (n u) -> p n u", u=2)
        x_banks = {}

        def transpose_x(pair):
            bank = psum_misc.tile([P, 2, 2 * P], F32, name="x_bank", tag="misc")
            for half in range(2):
                for u in range(2):
                    nc.tensor.transpose(
                        bank[:, u, half * P : (half + 1) * P],
                        x_words[:, 2 * pair + half, u : X_DIM // 2 : 2],
                        ident[:],
                    )
            x_banks[pair] = bank

        def regroup_x(pair):
            nc.scalar.copy(
                out=x_grouped_words[:, pair * 2 * P : (pair + 1) * 2 * P, :],
                in_=x_banks[pair][:].rearrange("p u n -> p n u"),
            )

        def quantise_x(pair):
            nc.vector.quantize_mx(
                out=x_codes[:, pair * 2 * P : (pair + 1) * 2 * P].bitcast(FP8X4),
                scales=x_scales[:, pair * 2 * P : (pair + 1) * 2 * P],
                in_=x_grouped[:, pair * 2 * K_PASS : (pair + 1) * 2 * K_PASS],
            )

        def regroup_x_tile(r):
            nc.scalar.copy(
                out=x_grouped_words[:, r * P : (r + 1) * P, :],
                in_=x_banks[r // 2][:, :, (r % 2) * P : (r % 2 + 1) * P].rearrange("p u n -> p n u"),
            )

        def quantise_x_tile(r):
            nc.vector.quantize_mx(
                out=x_codes[:, r * P : (r + 1) * P].bitcast(FP8X4),
                scales=x_scales[:, r * P : (r + 1) * P],
                in_=x_grouped[:, r * K_PASS : (r + 1) * K_PASS],
            )

        b2_scaled = keep.tile([P, D_TILES], F32, name="b2_scaled")
        b2_banks = {}

        def b2_tensor():
            bank = psum_misc.tile([P, 2, D_TILES], F32, name="b2_bank", tag="misc")
            for head in (MU, LV):
                for j in range(D_TILES):
                    nc.tensor.matmul(
                        out=bank[:, head, j : j + 1], lhsT=b2_rows[:, head, j * P : (j + 1) * P],
                        rhs=ones_bf[:, 0:1], start=True, stop=True,
                    )
            b2_banks[0] = bank

        def later_biases_vector():
            nc.vector.tensor_copy(out=b2_col[:], in_=b2_banks[0][:])
            nc.vector.tensor_scalar(
                out=b2_scaled[:], in0=b2_banks[0][:, MU, :], scalar1=ROOT_INV_N, scalar2=None, op0=ALU.mult
            )
            nc.vector.tensor_copy(out=b1_col[:, second_head, :], in_=b1_bf[:, second_head, :])

        y_t = keep.tile([P, D_TILES, N_ROWS], BF16, name="y_t")
        y_sum = keep.tile([P, D_TILES], F32, name="y_sum")
        y_sumsq = keep.tile([P, D_TILES], F32, name="y_sumsq")
        mean_sq = keep.tile([P, D_TILES], F32, name="mean_sq")
        y_var = keep.tile([P, D_TILES], F32, name="y_var")
        centre = keep.tile([P, D_TILES], F32, name="centre")
        diagonal = keep.tile([P, P], F32, name="diagonal")
        y_banks = {}

        def y_tensor(j):
            cols = slice(j * P, (j + 1) * P)
            turned = psum_misc.tile([P, ROW_TILES, P], BF16, name="y_turned", tag="misc")
            for r in range(ROW_TILES):
                nc.tensor.transpose(turned[:, r, :], y_sb[:, r, cols], ident_bf[:])
            stats = psum_misc.tile([P, P + 2], F32, name="y_stats", tag="misc")
            for r in range(ROW_TILES):
                nc.tensor.matmul(
                    out=stats[:, 0:P], lhsT=y_sb[:, r, cols], rhs=y_sb[:, r, cols],
                    start=(r == 0), stop=(r == ROW_TILES - 1),
                )
            for r in range(ROW_TILES):
                nc.tensor.matmul(
                    out=stats[:, P : P + 1], lhsT=y_sb[:, r, cols], rhs=ones_bf[:, 0:1],
                    start=(r == 0), stop=(r == ROW_TILES - 1),
                )
            y_banks[j] = (turned, stats)

        def y_scalar(j):
            nc.scalar.copy(out=y_t[:, j, :], in_=y_banks[j][0][:].rearrange("p r i -> p (r i)"))

        def y_vector(j):
            stats = y_banks[j][1]
            nc.vector.tensor_copy(out=y_sum[:, j : j + 1], in_=stats[:, P : P + 1])
            nc.vector.scalar_tensor_tensor(
                out=diagonal[:], in0=stats[:, 0:P], scalar=1.0, in1=ident[:],
                op0=ALU.mult, op1=ALU.mult, accum_out=y_sumsq[:, j : j + 1],
            )

        def y_constants():
            nc.vector.scalar_tensor_tensor(
                out=mean_sq[:], in0=y_sum[:], scalar=INV_N * INV_N * INV_N, in1=y_sum[:], op0=ALU.mult, op1=ALU.mult
            )
            nc.vector.scalar_tensor_tensor(
                out=centre[:], in0=y_sum[:], scalar=-INV_N * ROOT_INV_N, in1=b2_scaled[:], op0=ALU.mult, op1=ALU.add
            )
            nc.vector.scalar_tensor_tensor(
                out=y_var[:], in0=y_sumsq[:], scalar=INV_N * INV_N, in1=mean_sq[:], op0=ALU.mult, op1=ALU.subtract
            )

        l1_banks = {}
        parts_of = {}
        grouped_of = {}
        codes_of = {}

        def unit_of(number):
            u, rest = divmod(number, HID_PASSES)
            return u, UNIT_ORDER[u][0], UNIT_ORDER[u][1], rest

        def layer1(step):
            u, chunk, head, g = unit_of(step)
            l1_banks[step] = []
            for t in range(PACK):
                bank = psum_l1.tile([P, CHUNK], F32, name="l1_bank", tag="l1")
                cols = slice(g * K_PASS + t * P, g * K_PASS + (t + 1) * P)
                nc.tensor.matmul_mx(
                    out=bank[:],
                    lhsT=w1_regrouped[:, head, cols].bitcast(FP8X4),
                    lhsT_scale=planes_regrouped[4 * g : P, head, t * P : (t + 1) * P],
                    rhs=x_codes[:, chunk * CHUNK : (chunk + 1) * CHUNK].bitcast(FP8X4),
                    rhs_scale=x_scales[:, chunk * CHUNK : (chunk + 1) * CHUNK],
                    start=True,
                    stop=True,
                )
                l1_banks[step].append(bank)

        def leave_layer1(step, vector_banks):
            u, chunk, head, g = unit_of(step)
            parts = hidden.tile([P, PACK, CHUNK], BF16, name="parts")
            for t in range(PACK):
                bias = b1_col[:, head, g * PACK + t : g * PACK + t + 1]
                if t < PACK - vector_banks:
                    nc.scalar.activation(out=parts[:, t, :], in_=l1_banks[step][t][:], func=ACT.Relu, bias=bias)
                else:
                    nc.vector.tensor_scalar(
                        out=parts[:, t, :], in0=l1_banks[step][t][:], scalar1=bias, scalar2=0.0,
                        op0=ALU.add, op1=ALU.max,
                    )
            parts_of[step] = parts

        def interleave(step):
            grouped = hidden.tile([P, CHUNK, PACK], BF16, name="grouped", align_bytes=64)
            nc.vector.tensor_copy(
                out=grouped[:].rearrange("p (c i) t -> p c t i", i=8),
                in_=parts_of[step][:].rearrange("p t (c i) -> p c t i", i=8),
            )
            grouped_of[step] = grouped

        def quantise_hidden(step):
            u, chunk, head, g = unit_of(step)
            if g == 0:
                codes = hidden.tile([P, HID_PASSES, CHUNK], U32, name="codes", align_bytes=64)
                scales = hidden.tile([P, HID_PASSES, CHUNK], U8, name="scales", align_bytes=64)
                codes_of[u] = (codes, scales)
            codes, scales = codes_of[u]
            nc.vector.quantize_mx(
                out=codes[:, g, :].bitcast(FP8X4),
                scales=scales[:, g, :],
                in_=grouped_of[step][:].rearrange("p n t -> p (n t)"),
            )

        l2_banks = {}
        logvar_of = {}
        diff_of = {}
        weight_of = {}
        terms_of = {}
        second_unit_of = {}
        for u in range(UNITS):
            second_unit_of[UNIT_ORDER[u][0]] = u

        def layer2(bank_no, passes=(0, 1, 2, 3), in_l1=False):
            u, chunk, head, j = unit_of(bank_no)
            codes, scales = codes_of[u]
            if passes[0] == 0:
                if in_l1:
                    l2_banks[bank_no] = psum_l1.tile([P, CHUNK], F32, name="l2_bank_late", tag="l1")
                else:
                    l2_banks[bank_no] = psum_l2.tile([P, CHUNK], F32, name="l2_bank", tag="l2")
            bank = l2_banks[bank_no]
            for g in passes:
                nc.tensor.matmul_mx(
                    out=bank[:],
                    lhsT=w2[:, head, g, j * P : (j + 1) * P].bitcast(FP8X4),
                    lhsT_scale=planes[4 * g : P, w2_slot[head], j * P : (j + 1) * P],
                    rhs=codes[:, g, :].bitcast(FP8X4),
                    rhs_scale=scales[:, g, :],
                    start=(g == 0),
                    stop=(g == HID_PASSES - 1),
                )

        def leave_layer2(bank_no):
            u, chunk, head, j = unit_of(bank_no)
            if head == LV:
                logvar = score.tile([P, CHUNK], F32, name="logvar")
                nc.scalar.activation(
                    out=logvar[:], in_=l2_banks[bank_no][:], func=ACT.Tanh, bias=b2_col[:, LV, j : j + 1]
                )
                logvar_of[bank_no] = logvar
            else:
                if j == 0:
                    terms_of[chunk] = by_chunk.tile([P, 2, D_TILES, CHUNK], F32, name="terms")
                nc.scalar.activation(
                    out=terms_of[chunk][:, ALL, j, :], in_=l2_banks[bank_no][:], func=ACT.Square, scale=ROOT_INV_N,
                    bias=centre[:, j : j + 1],
                )
                diff = score.tile([P, CHUNK], F32, name="diff")
                nc.vector.scalar_tensor_tensor(
                    out=diff[:], in0=l2_banks[bank_no][:], scalar=b2_col[:, MU, j : j + 1],
                    in1=y_t[:, j, chunk * CHUNK : (chunk + 1) * CHUNK], op0=ALU.add, op1=ALU.subtract,
                )
                diff_of[bank_no] = diff

        def second_scalar(bank_no):
            u, chunk, head, j = unit_of(bank_no)
            if head == LV:
                if j == 0:
                    weight_of[chunk] = by_chunk.tile([P, D_TILES, CHUNK], F32, name="weight")
                nc.scalar.activation(
                    out=weight_of[chunk][:, j, :], in_=logvar_of[bank_no][:], func=ACT.Exp, scale=-1.0, bias=-LN2
                )
            else:
                nc.scalar.activation(out=terms_of[chunk][:, OWN, j, :], in_=diff_of[bank_no][:], func=ACT.Square)

        def finishes_scores(bank_no):
            return 0 <= bank_no < STEPS and unit_of(bank_no)[0] == second_unit_of[unit_of(bank_no)[1]]

        def weighted_terms(bank_no):
            u, chunk, head, j = unit_of(bank_no)
            terms = terms_of[chunk]
            nc.vector.scalar_tensor_tensor(
                out=terms[:, ALL, j, :], in0=terms[:, ALL, j, :], scalar=y_var[:, j : j + 1],
                in1=weight_of[chunk][:, j, :], op0=ALU.add, op1=ALU.mult,
            )
            nc.vector.scalar_tensor_tensor(
                out=terms[:, OWN, j, :], in0=terms[:, OWN, j, :], scalar=(-1.0 if chunk == 1 else 1.0),
                in1=weight_of[chunk][:, j, :], op0=ALU.mult, op1=ALU.mult,
            )

        totals = keep.tile([P, 2, ROW_TILES], F32, name="totals")
        result = keep.tile([P, 2, ROW_TILES], F32, name="result")
        sum_banks = {}

        def sum_over_d_tensor(chunk, d_tiles, pool, tag, outputs=(ALL, OWN)):
            for o in outputs:
                bank = pool.tile([P, TILES_PER_CHUNK, P], F32, name="sum_bank", tag=tag)
                for i in range(TILES_PER_CHUNK):
                    for j in d_tiles:
                        nc.tensor.matmul(
                            out=bank[:, i, :], lhsT=terms_of[chunk][:, o, j, i * P : (i + 1) * P], rhs=ident[:],
                            is_transpose=True, start=(j == d_tiles[0]), stop=(j == d_tiles[-1]),
                        )
                sum_banks[(chunk, o)] = bank

        def sum_over_d_vector(chunk, out, outputs=(ALL, OWN)):
            for o in outputs:
                nc.vector.tensor_reduce(out=out[:, o, :], in_=sum_banks[(chunk, o)][:], axis=AX.X, op=ALU.add)

        last_sum_banks = {}

        def last_sums_tensor(o, row_tiles, d_tiles, pool, tag):
            for i in row_tiles:
                if (o, i) not in last_sum_banks:
                    last_sum_banks[(o, i)] = pool.tile([P, P], F32, name="last_sum_bank", tag=tag)
                for j in d_tiles:
                    nc.tensor.matmul(
                        out=last_sum_banks[(o, i)][:], lhsT=terms_of[1][:, o, j, i * P : (i + 1) * P], rhs=ident[:],
                        is_transpose=True, start=(j == 0), stop=(j == D_TILES - 1),
                    )

        def last_sums_vector(o, row_tiles):
            for i in row_tiles:
                nc.vector.tensor_reduce(
                    out=result[:, o, TILES_PER_CHUNK + i : TILES_PER_CHUNK + i + 1], in_=last_sum_banks[(o, i)][:],
                    axis=AX.X, op=ALU.add,
                )

        sum_scrap = keep.tile([P, P], F32, name="sum_scrap")

        def last_sums_scalar(o, row_tiles):
            for i in row_tiles:
                nc.scalar.activation(
                    out=sum_scrap[:], in_=last_sum_banks[(o, i)][:], func=ACT.Copy, scale=-1.0,
                    accum_out=result[:, o, TILES_PER_CHUNK + i : TILES_PER_CHUNK + i + 1],
                )

        first_chunk = slice(0, TILES_PER_CHUNK)
        last_bank_of = {}
        for chunk in (0, 1):
            last_bank_of[chunk] = second_unit_of[chunk] * HID_PASSES + D_TILES - 1

        def vector_banks_of(step):
            scalar_other = 0.0
            vector_other = 3.0
            if 0 <= step - LAG_SCORE < STEPS:
                scalar_other += 2.0
                if unit_of(step - LAG_SCORE)[2] == MU:
                    vector_other += 1.0
            if finishes_scores(step - LAG_WEIGHTED):
                vector_other += 2.0
            if step == X_STEP:
                scalar_other += 2.0
                vector_other += 1.0
            if step in Y_STEPS:
                scalar_other += 1.0
            if W1_STEP <= step < W1_STEP + HID_PASSES:
                vector_other += 0.5
            if step == STEPS - 1:
                return 0
            return max(0, min(PACK - 1, int((PACK + scalar_other - vector_other) / 2.0 + 0.5)))

        warm_bank = psum_l1.tile([P, CHUNK], F32, name="warm_bank", tag="l1")
        for k in range(WARM_UP):
            nc.tensor.matmul(out=warm_bank[:], lhsT=warm[:, 0:P], rhs=warm[:], start=True, stop=True)
        transpose_x(0)
        transpose_x(1)
        for k in range(HOLD_UP):
            nc.tensor.matmul(out=warm_bank[:], lhsT=warm[:, 0:P], rhs=warm[:], start=True, stop=True)
        regroup_x(0)
        regroup_x_tile(2)
        regroup_x_tile(3)
        nc.vector.tensor_copy(out=b1_col[:, first_head, :], in_=b1_bf[:, first_head, :])
        regroup_planes(first_head)
        quantise_x(0)
        regroup_w1(first_head, 0)
        quantise_x_tile(2)
        quantise_x_tile(3)
        for g in range(1, HID_PASSES):
            regroup_w1(first_head, g)

        first_last = last_bank_of[1] - D_TILES + 1
        put_off = (first_last - 2, first_last - 1)
        for i in range(STEPS + LAG_SUM + 1):
            if i < STEPS:
                layer1(i)
            if i == BIAS_STEP:
                b2_tensor()
            if i == X_STEP:
                transpose_x(2)
                transpose_x(3)
            if i in Y_STEPS:
                y_tensor(Y_STEPS.index(i))
            if 0 <= i - LAG_LAYER2 < first_last:
                layer2(i - LAG_LAYER2)
            if i - LAG_SUM == last_bank_of[0]:
                sum_over_d_tensor(0, (0, 1, 2, 3), psum_misc, "misc", (ALL,))
            if i == STEPS:
                layer2(first_last, (0, 1, 2), True)
                layer2(first_last + 1, (0, 1, 2), True)
            if i == STEPS + 1:
                layer2(first_last, (3,), True)
                layer2(first_last + 1, (3,), True)
                layer2(first_last + 2, (0, 1, 2, 3), True)
                sum_over_d_tensor(0, (0, 1, 2, 3), psum_misc, "misc", (OWN,))
            if i == STEPS + 2:
                layer2(first_last + 3, (0, 1, 2, 3), True)
            j_last = i - LAG_SUM - first_last
            if 0 <= j_last < D_TILES:
                last_sums_tensor(ALL, (0, 1), (j_last,), psum_l2, "l2")
                last_sums_tensor(ALL, (2, 3), (j_last,), psum_l1, "l1")
                last_sums_tensor(OWN, (0,), (j_last,), psum_misc, "misc")
                for row_tile, late, pool, tag in ((1, 1, psum_l1, "l1"), (2, 2, psum_misc, "misc"), (3, 2, psum_l1, "l1")):
                    if j_last == late:
                        last_sums_tensor(OWN, (row_tile,), tuple(range(late + 1)), pool, tag)
                    if j_last > late:
                        last_sums_tensor(OWN, (row_tile,), (j_last,), pool, tag)

            if 0 <= i - 1 < STEPS:
                interleave(i - 1)
            if i == STEPS:
                quantise_hidden(i - 1)
            if 0 <= i - LAG_SCORE < STEPS and i - LAG_SCORE != first_last + 1:
                leave_layer2(i - LAG_SCORE)
            if i - LAG_SCORE == first_last:
                leave_layer2(first_last + 1)
            if i < STEPS:
                leave_layer1(i, vector_banks_of(i))
            if i == X_STEP:
                regroup_x(2)
                regroup_x(3)
            if i in Y_STEPS:
                y_scalar(Y_STEPS.index(i))
            if i == BIAS_STEP:
                later_biases_vector()
            if i == X_STEP:
                quantise_x(2)
                quantise_x(3)
            if i == W1_STEP:
                regroup_planes(second_head)
            if W1_STEP <= i < W1_STEP + HID_PASSES:
                regroup_w1(second_head, i - W1_STEP)
            if i in Y_STEPS:
                y_vector(Y_STEPS.index(i))
            if i == Y_STEPS[-1]:
                y_constants()
            if 0 <= i - 1 < STEPS - 1:
                quantise_hidden(i - 1)
            if i - LAG_SCORE - 4 in put_off:
                second_scalar(i - LAG_SCORE - 4)
            if 0 <= i - LAG_SCORE < STEPS and i - LAG_SCORE not in put_off:
                second_scalar(i - LAG_SCORE)
            if i == first_last + LAG_WEIGHTED:
                sum_over_d_vector(0, totals[:, :, first_chunk], (ALL,))
            if finishes_scores(i - LAG_WEIGHTED):
                weighted_terms(i - LAG_WEIGHTED)
            if i == first_last + LAG_WEIGHTED + 1:
                sum_over_d_vector(0, totals[:, :, first_chunk], (OWN,))
            if i == first_last + LAG_WEIGHTED + 2:
                nc.vector.tensor_scalar(
                    out=result[:, :, first_chunk], in0=totals[:, :, first_chunk], scalar1=-1.0, scalar2=None,
                    op0=ALU.mult,
                )

        last_sums_scalar(ALL, (0, 1, 2, 3))
        nc.scalar.dma_start(out=out_1.rearrange("(p r) -> p r", r=ROW_TILES), in_=result[:, ALL, :])
        last_sums_vector(OWN, (0, 1, 2, 3))
        nc.sync.dma_start(out=out_0.rearrange("(p r) -> p r", r=ROW_TILES), in_=result[:, OWN, :])
